import numpy as np
import ml_dtypes


def mxq(x, axis, fmt="e4m3"):
    dtype, down = {"e4m3": (ml_dtypes.float8_e4m3fn, 7), "e5m2": (ml_dtypes.float8_e5m2, 14)}[fmt]
    v = np.moveaxis(np.asarray(x, np.float32).astype(ml_dtypes.bfloat16).astype(np.float64), axis, -1)
    blocks = v.reshape(v.shape[:-1] + (-1, 32))
    amax = np.abs(blocks).max(-1, keepdims=True)
    byte = np.maximum(np.where(amax > 0, np.frexp(amax)[1] - 1 + 127, 0) - down, 1)
    scale = np.exp2(byte - 127.0)
    codes = (blocks / scale).astype(np.float32).astype(dtype).astype(np.float64)
    return np.moveaxis((codes * scale).reshape(v.shape), -1, axis)


WIDE = False


def mx_kscale(k):
    if not WIDE:
        return np.ones(k)
    levels = np.array([10, -10, 5, -5, 0])
    a = np.random.permutation(np.resize(levels, k // 512 * 4)).reshape(k // 512, 4)
    idx = np.arange(k)
    return np.exp2(a[idx // 512, idx % 128 // 32])


BF16 = ml_dtypes.bfloat16


def bf(x):
    return np.asarray(x, np.float32).astype(BF16)


def f64(x):
    return np.asarray(x).astype(np.float64)


B, T, C, H = 8, 1024, 256, 2
D = C // H


def softmax(a):
    e = np.exp(a - a.max(-1, keepdims=True))
    return e / e.sum(-1, keepdims=True)


def heads(a):
    return a.reshape(B, T, H, D).transpose(0, 2, 1, 3)


def setup_inputs():
    u = np.array(mx_kscale(T), dtype=np.float64)
    u[:D] = u.min()
    u = u / u.min()
    q = np.random.standard_normal((B, T, C)) * 1.5
    k = np.random.standard_normal((B, T, C)) * 1.5
    v = np.random.standard_normal((B, T, C)) * u[None, :, None]
    q[:, :, ::D] = np.sqrt(D)
    k[:, :, ::D] -= np.log(u)[None, :, None]
    return {"q": bf(q), "k": bf(k), "v": bf(v),
            "alpha": bf((1.0 + 0.1 * np.random.standard_normal(1)) / u.max()),
            "beta": bf(1.0 + 0.1 * np.random.standard_normal(1)),
            "gamma": bf((1.0 + 0.1 * np.random.standard_normal(1)) / u.max())}


def reference(q, k, v, alpha, beta, gamma):
    qh, kh, vh = heads(f64(q)), heads(f64(k)), heads(f64(v))
    att = (qh @ kh.transpose(0, 1, 3, 2)) * (1.0 / np.sqrt(D))
    causal = np.tril(np.ones((T, T), dtype=bool))
    att = np.where(causal, att, -1e20)
    att = f64(beta) * softmax(att)
    eye = np.eye(T)
    M = np.triu(np.ones((T, T)), k=1)
    MC = softmax(1e20 * M)
    att = att + f64(alpha) * eye - f64(gamma) * MC
    y = mxq(att, 3, "e4m3") @ mxq(vh, 2, "e4m3")
    return y.transpose(0, 2, 1, 3).reshape(B, T, C)

@@ -1,0 +1,301 @@
+from contextlib import ExitStack
+import math
+
+import concourse.mybir as mybir
+from concourse.masks import make_identity
+
+F32 = mybir.dt.float32
+BF16 = mybir.dt.bfloat16
+I32 = mybir.dt.int32
+U32 = mybir.dt.uint32
+U8 = mybir.dt.uint8
+FP8X4 = mybir.dt.float8_e4m3fn_x4
+ALU = mybir.AluOpType
+EXP = mybir.ActivationFunctionType.Exp
+
+B, T, C, H = 8, 1024, 256, 2
+D = C // H
+P = 128
+NT = T // P
+K_PASS = 4 * P
+HALF = T // 2
+BLOCK = P // 2
+BANK = 512
+MASKED = -1e20
+FLOPS = 2 * 2 * B * H * T * T * D
+
+
+def passes_of(i):
+    return (P * (i + 1) + K_PASS - 1) // K_PASS
+
+
+UNITS = [(i, c) for i in range(NT) for c in range(passes_of(i))]
+QUANT_UNITS = 4
+
+
+def tile_causalshapedattention_pa_t_kernel(tc, q, k, v, alpha, beta, gamma, out):
+    nc = tc.nc
+    scale = 1.0 / math.sqrt(D)
+    with ExitStack() as ctx:
+        const = ctx.enter_context(tc.tile_pool(name="const", bufs=1))
+        loads = ctx.enter_context(tc.tile_pool(name="loads", bufs=2))
+        heads = ctx.enter_context(tc.tile_pool(name="heads", bufs=2))
+        psum_s = ctx.enter_context(tc.psum_pool(name="psum_s", bufs=2))
+        psum_t = ctx.enter_context(tc.psum_pool(name="psum_t", bufs=2))
+        psum_o = ctx.enter_context(tc.psum_pool(name="psum_o", bufs=1))
+        psum_qk = ctx.enter_context(tc.psum_pool(name="psum_qk", bufs=1))
+
+        ident_bf = const.tile([P, P], BF16)
+        make_identity(nc, ident_bf[:])
+        ident_f32 = const.tile([P, P], F32)
+        make_identity(nc, ident_f32[:])
+        key_perm = const.tile([P, P], BF16)
+        nc.vector.tensor_copy(
+            out=key_perm[:].rearrange("k (u p e) -> k u p e", u=2, e=2),
+            in_=ident_bf[:].rearrange("k (p u e) -> k u p e", u=2, e=2),
+        )
+        lower_nat = const.tile([P, P], F32)
+        nc.gpsimd.memset(lower_nat[:], 1.0)
+        nc.gpsimd.affine_select(
+            out=lower_nat[:], in_=lower_nat[:], compare_op=ALU.is_ge, fill=0.0,
+            base=0, pattern=[[-1, P]], channel_multiplier=1,
+        )
+        lower = const.tile([P, P], F32)
+        nc.vector.tensor_copy(
+            out=lower[:].rearrange("k (u p e) -> k u p e", u=2, e=2),
+            in_=lower_nat[:].rearrange("k (p u e) -> k u p e", u=2, e=2),
+        )
+        diag = const.tile([P, P], F32)
+        nc.vector.tensor_copy(
+            out=diag[:].rearrange("k (u p e) -> k u p e", u=2, e=2),
+            in_=ident_f32[:].rearrange("k (p u e) -> k u p e", u=2, e=2),
+        )
+        upper = const.tile([P, P], F32)
+        nc.vector.tensor_scalar(out=upper[:], in0=lower[:], scalar1=-1.0, scalar2=1.0,
+                                op0=ALU.mult, op1=ALU.add)
+        mask_add = const.tile([P, P], BF16)
+        nc.vector.tensor_scalar(out=mask_add[:], in0=upper[:], scalar1=MASKED, scalar2=None,
+                                op0=ALU.mult)
+        ones = const.tile([P, 2, 2 * P], F32)
+        nc.vector.memset(ones[:], 1.0)
+
+        alpha_bf = const.tile([P, 1], BF16)
+        beta_bf = const.tile([P, 1], BF16)
+        gamma_bf = const.tile([P, 1], BF16)
+        nc.sync.dma_start(out=alpha_bf[:], in_=alpha.partition_broadcast(P))
+        nc.sync.dma_start(out=beta_bf[:], in_=beta.partition_broadcast(P))
+        nc.sync.dma_start(out=gamma_bf[:], in_=gamma.partition_broadcast(P))
+        alpha_f = const.tile([P, 1], F32)
+        beta_f = const.tile([P, 1], F32)
+        gamma_f = const.tile([P, 1], F32)
+        nc.vector.tensor_copy(out=alpha_f[:], in_=alpha_bf[:])
+        nc.vector.tensor_copy(out=beta_f[:], in_=beta_bf[:])
+        nc.vector.tensor_copy(out=gamma_f[:], in_=gamma_bf[:])
+
+        row_i32 = const.tile([P, NT], I32)
+        nc.gpsimd.iota(row_i32[:], pattern=[[P, NT]], base=0, channel_multiplier=1)
+        row_f = const.tile([P, NT], F32)
+        nc.vector.tensor_copy(out=row_f[:], in_=row_i32[:])
+        later = const.tile([P, NT], F32)
+        nc.vector.tensor_scalar(out=later[:], in0=row_f[:], scalar1=-1.0, scalar2=float(T - 1),
+                                op0=ALU.mult, op1=ALU.add)
+        nc.vector.tensor_scalar_max(out=later[:], in0=later[:], scalar1=1.0)
+        inv_later = const.tile([P, NT], F32)
+        nc.vector.reciprocal(out=inv_later[:], in_=later[:])
+        above = const.tile([P, NT], F32)
+        nc.vector.tensor_scalar(out=above[:], in0=inv_later[:], scalar1=gamma_f[:, 0:1], scalar2=-1.0,
+                                op0=ALU.mult, op1=ALU.mult)
+        last_row = const.tile([P, NT], F32)
+        nc.vector.tensor_scalar(out=last_row[:], in0=row_f[:], scalar1=float(T - 1), scalar2=-1.0 / T,
+                                op0=ALU.is_equal, op1=ALU.mult)
+        below = const.tile([P, NT], F32)
+        nc.vector.tensor_scalar(out=below[:], in0=last_row[:], scalar1=gamma_f[:, 0:1], scalar2=None,
+                                op0=ALU.mult)
+
+        shape_add = const.tile([P, NT, P], F32)
+        for i in range(NT):
+            nc.vector.tensor_scalar(out=shape_add[:, i, :], in0=upper[:], scalar1=above[:, i:i + 1],
+                                    scalar2=None, op0=ALU.mult)
+            nc.vector.scalar_tensor_tensor(out=shape_add[:, i, :], in0=lower[:], scalar=below[:, i:i + 1],
+                                           in1=shape_add[:, i, :], op0=ALU.mult, op1=ALU.add)
+            nc.vector.scalar_tensor_tensor(out=shape_add[:, i, :], in0=diag[:], scalar=alpha_f[:, 0:1],
+                                           in1=shape_add[:, i, :], op0=ALU.mult, op1=ALU.add)
+
+        a_tiles = []
+        for s in range(2):
+            row_set = []
+            for i in range(NT):
+                width = 2 * P * passes_of(i)
+                a_t = const.tile([P, 2, width], BF16, name="a%d_%d" % (s, i))
+                used = BLOCK * (i + 1)
+                if used < width:
+                    nc.vector.tensor_scalar(out=a_t[:, :, used:], in0=ones[:, :, :width - used],
+                                            scalar1=above[:, i:i + 1], scalar2=None, op0=ALU.mult)
+                row_set.append(a_t)
+            a_tiles.append(row_set)
+
+        def transpose_pair(word_views, grouped_words):
+            bank = psum_t.tile([P, 2, 2, P], F32, name="bank")
+            for n in range(2):
+                for u in range(2):
+                    nc.tensor.transpose(bank[:, n, u, :], word_views[n][:, u, :], ident_f32[:])
+            nc.scalar.copy(out=grouped_words, in_=bank[:].rearrange("p n u i -> p n i u"))
+
+        n_far = NT - len([i for i in range(NT) if passes_of(i) == 2])
+        far_a = const.tile([P, n_far, 2, 2 * P], BF16)
+        far_grouped = const.tile([P, n_far, P, 4], BF16, align_bytes=64)
+        far_codes = const.tile([P, n_far, P], U32, align_bytes=64)
+        far_scales = const.tile([P, n_far, P], U8, align_bytes=64)
+        for i in range(n_far):
+            nc.vector.tensor_scalar(out=far_a[:, i], in0=ones[:], scalar1=above[:, i:i + 1],
+                                    scalar2=None, op0=ALU.mult)
+        for g in range(0, n_far, 2):
+            transpose_pair([far_a[:, g + n].bitcast(F32) for n in range(2)],
+                           far_grouped[:, g:g + 2].bitcast(F32))
+        nc.vector.quantize_mx(
+            out=far_codes[:].rearrange("p n i -> p (n i)").bitcast(FP8X4),
+            scales=far_scales[:].rearrange("p n i -> p (n i)"),
+            in_=far_grouped[:].rearrange("p n i t -> p (n i t)"),
+        )
+
+        raw = {}
+        values = {}
+        state = {}
+        results = {}
+
+        def load(b):
+            q_sb = loads.tile([P, NT, C], BF16, name="q_sb")
+            k_sb = loads.tile([P, NT, C], BF16, name="k_sb")
+            v_sb = loads.tile([P, 2, 4, C], BF16, name="v_sb")
+            nc.sync.dma_start(out=q_sb[:], in_=q[b, :, :].rearrange("(n p) c -> p n c", p=P))
+            nc.sync.dma_start(out=k_sb[:], in_=k[b, :, :].rearrange("(n p) c -> p n c", p=P))
+            nc.sync.dma_start(out=v_sb[:], in_=v[b, :, :].rearrange("(c p t) w -> p c t w", p=P, t=4))
+            raw[b] = (q_sb, k_sb, v_sb)
+
+        def quantise_v(b):
+            v_sb = raw[b][2]
+            v_grouped = loads.tile([P, 2, C, 4], BF16, name="v_grouped", align_bytes=64)
+            v_codes = loads.tile([P, 2, C], U32, name="v_codes", align_bytes=64)
+            v_scales = loads.tile([P, 2, C], U8, name="v_scales", align_bytes=64)
+            nc.vector.tensor_copy(out=v_grouped[:], in_=v_sb[:].rearrange("p c t w -> p c w t"))
+            nc.vector.quantize_mx(
+                out=v_codes[:].rearrange("p c w -> p (c w)").bitcast(FP8X4),
+                scales=v_scales[:].rearrange("p c w -> p (c w)"),
+                in_=v_grouped[:].rearrange("p c w t -> p (c w t)"),
+            )
+            values[b] = (v_codes, v_scales)
+            results[b] = loads.tile([P, NT, C], F32, name="out_sb")
+
+        def scores(b, h):
+            q_sb, k_sb = raw[b][0], raw[b][1]
+            cols = slice(h * D, (h + 1) * D)
+            qT_ps = psum_qk.tile([P, NT, P], BF16, name="qk_ps")
+            for n in range(NT):
+                nc.tensor.transpose(qT_ps[:, n, :], q_sb[:, n, cols], ident_bf[:])
+            qT = heads.tile([P, NT, P], BF16, name="qT")
+            nc.vector.tensor_copy(out=qT[:], in_=qT_ps[:])
+            kT_ps = psum_qk.tile([P, NT, P], BF16, name="qk_ps")
+            for n in range(NT):
+                nc.tensor.transpose(kT_ps[:, n, :], k_sb[:, n, cols], key_perm[:])
+            kT = heads.tile([P, 2, HALF], BF16, name="kT")
+            nc.vector.tensor_copy(
+                out=kT[:].rearrange("d u (j x) -> d u j x", x=BLOCK),
+                in_=kT_ps[:].rearrange("d j (u x) -> d u j x", u=2),
+            )
+            neg_max = heads.tile([P, NT], F32, name="neg_max")
+            neg_max_half = heads.tile([P, NT], F32, name="neg_max_half")
+            row_sum = heads.tile([P, NT], F32, name="row_sum")
+            exps = []
+            for i in range(NT):
+                used = BLOCK * (i + 1)
+                s_ps = psum_s.tile([P, 2, BANK], F32, name="s_ps")
+                one_bank = 2 * used <= BANK
+                if one_bank:
+                    s_view = s_ps[:, 0, :2 * used].rearrange("q (u x) -> q u x", u=2)
+                else:
+                    s_view = s_ps[:, :, :used]
+                for u in range(2):
+                    nc.tensor.matmul(s_view[:, u, :], lhsT=qT[:, i, :], rhs=kT[:, u, :used],
+                                     start=True, stop=False)
+                    nc.tensor.matmul(s_view[:, u, used - BLOCK:], lhsT=ident_bf[:],
+                                     rhs=mask_add[:, u * BLOCK:(u + 1) * BLOCK], start=False, stop=True)
+                e_t = heads.tile([P, 2, used], F32, name="e%d" % i)
+                if one_bank:
+                    nc.vector.tensor_scalar(out=e_t[:], in0=s_view, scalar1=-scale, scalar2=None,
+                                            op0=ALU.mult, op1=ALU.min, accum_out=neg_max[:, i:i + 1])
+                else:
+                    nc.vector.tensor_scalar(out=e_t[:, 0, :], in0=s_view[:, 0, :], scalar1=-scale, scalar2=None,
+                                            op0=ALU.mult, op1=ALU.min, accum_out=neg_max_half[:, i:i + 1])
+                    nc.vector.tensor_scalar(out=e_t[:, 1, :], in0=s_view[:, 1, :], scalar1=-scale,
+                                            scalar2=neg_max_half[:, i:i + 1],
+                                            op0=ALU.mult, op1=ALU.min, accum_out=neg_max[:, i:i + 1])
+                nc.scalar.activation(out=e_t[:], in_=e_t[:], func=EXP, bias=neg_max[:, i:i + 1], scale=-1.0,
+                                     accum_out=row_sum[:, i:i + 1])
+                exps.append(e_t)
+            state[(b, h)] = (exps, row_sum)
+
+        def finish(b, h):
+            exps, row_sum = state[(b, h)]
+            row_set = a_tiles[h]
+            v_codes, v_scales = values[b]
+            out_sb = results[b]
+            cols = slice(h * D, (h + 1) * D)
+            gain = heads.tile([P, NT], F32, name="gain")
+            nc.vector.reciprocal(out=gain[:], in_=row_sum[:])
+            nc.vector.tensor_scalar(out=gain[:], in0=gain[:], scalar1=beta_f[:, 0:1], scalar2=None, op0=ALU.mult)
+            for i in range(NT):
+                used = BLOCK * (i + 1)
+                if i > 0:
+                    nc.gpsimd.tensor_scalar(out=row_set[i][:, :, :used - BLOCK], in0=exps[i][:, :, :used - BLOCK],
+                                            scalar1=gain[:, i:i + 1], scalar2=below[:, i:i + 1],
+                                            op0=ALU.mult, op1=ALU.add)
+                nc.vector.scalar_tensor_tensor(
+                    out=row_set[i][:, :, used - BLOCK:used], in0=exps[i][:, :, used - BLOCK:],
+                    scalar=gain[:, i:i + 1], in1=shape_add[:, i, :].rearrange("q (u x) -> q u x", u=2),
+                    op0=ALU.mult, op1=ALU.add)
+            grouped = heads.tile([P, len(UNITS), P, 4], BF16, name="grouped", align_bytes=64)
+            codes = heads.tile([P, len(UNITS), P], U32, name="codes", align_bytes=64)
+            scales = heads.tile([P, len(UNITS), P], U8, name="scales", align_bytes=64)
+            for g in range(0, len(UNITS), 2):
+                views = []
+                for n in range(2):
+                    i, c = UNITS[g + n]
+                    views.append(row_set[i][:].bitcast(F32)[:, :, c * P:(c + 1) * P])
+                transpose_pair(views, grouped[:, g:g + 2].bitcast(F32))
+            for g in range(0, len(UNITS), QUANT_UNITS):
+                nc.vector.quantize_mx(
+                    out=codes[:, g:g + QUANT_UNITS].rearrange("p n i -> p (n i)").bitcast(FP8X4),
+                    scales=scales[:, g:g + QUANT_UNITS].rearrange("p n i -> p (n i)"),
+                    in_=grouped[:, g:g + QUANT_UNITS].rearrange("p n i t -> p (n i t)"),
+                )
+            for g in range(0, NT, 4):
+                o_ps = psum_o.tile([P, 4, P], F32, name="o_ps")
+                for n in range(4):
+                    i = g + n
+                    for c in range(2):
+                        if c < passes_of(i):
+                            unit = UNITS.index((i, c))
+                            a_codes, a_scales = codes[:, unit, :], scales[:, unit, :]
+                        else:
+                            a_codes, a_scales = far_codes[:, i, :], far_scales[:, i, :]
+                        nc.tensor.matmul_mx(
+                            out=o_ps[:, n, :],
+                            lhsT=a_codes.bitcast(FP8X4), lhsT_scale=a_scales,
+                            rhs=v_codes[:, c, cols].bitcast(FP8X4), rhs_scale=v_scales[:, c, cols],
+                            start=(c == 0), stop=(c == 1),
+                        )
+                nc.scalar.copy(out=out_sb[:, g:g + 4, cols], in_=o_ps[:])
+            if h == H - 1:
+                nc.sync.dma_start(out=out[b, :, :].rearrange("(n p) c -> p n c", p=P), in_=out_sb[:])
+
+        jobs = [(b, h) for b in range(B) for h in range(H)]
+        load(0)
+        for n, (b, h) in enumerate(jobs):
+            if h == 0:
+                if b + 1 < B:
+                    load(b + 1)
+                quantise_v(b)
+            scores(b, h)
+            if n > 0:
+                finish(*jobs[n - 1])
+        finish(*jobs[-1])

@@ -18,6 +18,7 @@ D = C // H
 P = 128
 NT = T // P
 K_PASS = 4 * P
+PASSES = T // K_PASS
 HALF = T // 2
 BLOCK = P // 2
 BANK = 512
@@ -31,6 +32,8 @@ def passes_of(i):
 
 UNITS = [(i, c) for i in range(NT) for c in range(passes_of(i))]
 QUANT_UNITS = 4
+N_FAR = len([i for i in range(NT) if passes_of(i) < PASSES])
+FAR_STEP = 8
 
 
 def tile_causalshapedattention_pa_t_kernel(tc, q, k, v, alpha, beta, gamma, out):
@@ -40,60 +43,73 @@ def tile_causalshapedattention_pa_t_kernel(tc, q, k, v, alpha, beta, gamma, out)
         const = ctx.enter_context(tc.tile_pool(name="const", bufs=1))
         loads = ctx.enter_context(tc.tile_pool(name="loads", bufs=2))
         heads = ctx.enter_context(tc.tile_pool(name="heads", bufs=2))
-        psum_s = ctx.enter_context(tc.psum_pool(name="psum_s", bufs=2))
+        psum_s = ctx.enter_context(tc.psum_pool(name="psum_s", bufs=4))
         psum_t = ctx.enter_context(tc.psum_pool(name="psum_t", bufs=2))
         psum_o = ctx.enter_context(tc.psum_pool(name="psum_o", bufs=1))
         psum_qk = ctx.enter_context(tc.psum_pool(name="psum_qk", bufs=1))
+        long_lived = ctx.enter_context(tc.tile_pool(name="long_lived", bufs=4))
+
+        raw = {}
+        job = {}
+
+        def load(b):
+            q_sb = loads.tile([P, NT, C], BF16, name="q_sb")
+            k_sb = loads.tile([P, NT, C], BF16, name="k_sb")
+            v_sb = loads.tile([P, PASSES, 4, C], BF16, name="v_sb")
+            nc.sync.dma_start(out=q_sb[:], in_=q[b, :, :].rearrange("(n p) c -> p n c", p=P))
+            nc.sync.dma_start(out=k_sb[:], in_=k[b, :, :].rearrange("(n p) c -> p n c", p=P))
+            nc.sync.dma_start(out=v_sb[:], in_=v[b, :, :].rearrange("(c p t) w -> p c t w", p=P, t=4))
+            raw[b] = (q_sb, k_sb, v_sb)
+
+        alpha_bf = const.tile([P, 1], BF16)
+        beta_bf = const.tile([P, 1], BF16)
+        gamma_bf = const.tile([P, 1], BF16)
+        nc.scalar.dma_start(out=gamma_bf[:], in_=gamma.partition_broadcast(P))
+        nc.scalar.dma_start(out=alpha_bf[:], in_=alpha.partition_broadcast(P))
+        nc.scalar.dma_start(out=beta_bf[:], in_=beta.partition_broadcast(P))
+        load(0)
 
         ident_bf = const.tile([P, P], BF16)
         make_identity(nc, ident_bf[:])
         ident_f32 = const.tile([P, P], F32)
         make_identity(nc, ident_f32[:])
-        key_perm = const.tile([P, P], BF16)
-        nc.vector.tensor_copy(
-            out=key_perm[:].rearrange("k (u p e) -> k u p e", u=2, e=2),
-            in_=ident_bf[:].rearrange("k (p u e) -> k u p e", u=2, e=2),
-        )
         lower_nat = const.tile([P, P], F32)
         nc.gpsimd.memset(lower_nat[:], 1.0)
         nc.gpsimd.affine_select(
             out=lower_nat[:], in_=lower_nat[:], compare_op=ALU.is_ge, fill=0.0,
             base=0, pattern=[[-1, P]], channel_multiplier=1,
         )
+        row_i32 = const.tile([P, NT], I32)
+        nc.gpsimd.iota(row_i32[:], pattern=[[P, NT]], base=0, channel_multiplier=1)
+        ones = const.tile([P, 2, 2 * P], F32)
+        nc.gpsimd.memset(ones[:], 1.0)
+
+        def to_key_order(dst, src):
+            nc.vector.tensor_copy(
+                out=dst[:].rearrange("k (u p e) -> k u p e", u=2, e=2),
+                in_=src[:].rearrange("k (p u e) -> k u p e", u=2, e=2),
+            )
+
+        key_perm = const.tile([P, P], BF16)
+        to_key_order(key_perm, ident_bf)
         lower = const.tile([P, P], F32)
-        nc.vector.tensor_copy(
-            out=lower[:].rearrange("k (u p e) -> k u p e", u=2, e=2),
-            in_=lower_nat[:].rearrange("k (p u e) -> k u p e", u=2, e=2),
-        )
+        to_key_order(lower, lower_nat)
         diag = const.tile([P, P], F32)
-        nc.vector.tensor_copy(
-            out=diag[:].rearrange("k (u p e) -> k u p e", u=2, e=2),
-            in_=ident_f32[:].rearrange("k (p u e) -> k u p e", u=2, e=2),
-        )
+        to_key_order(diag, ident_f32)
         upper = const.tile([P, P], F32)
         nc.vector.tensor_scalar(out=upper[:], in0=lower[:], scalar1=-1.0, scalar2=1.0,
                                 op0=ALU.mult, op1=ALU.add)
         mask_add = const.tile([P, P], BF16)
         nc.vector.tensor_scalar(out=mask_add[:], in0=upper[:], scalar1=MASKED, scalar2=None,
                                 op0=ALU.mult)
-        ones = const.tile([P, 2, 2 * P], F32)
-        nc.vector.memset(ones[:], 1.0)
 
-        alpha_bf = const.tile([P, 1], BF16)
-        beta_bf = const.tile([P, 1], BF16)
-        gamma_bf = const.tile([P, 1], BF16)
-        nc.sync.dma_start(out=alpha_bf[:], in_=alpha.partition_broadcast(P))
-        nc.sync.dma_start(out=beta_bf[:], in_=beta.partition_broadcast(P))
-        nc.sync.dma_start(out=gamma_bf[:], in_=gamma.partition_broadcast(P))
         alpha_f = const.tile([P, 1], F32)
         beta_f = const.tile([P, 1], F32)
         gamma_f = const.tile([P, 1], F32)
+        nc.vector.tensor_copy(out=gamma_f[:], in_=gamma_bf[:])
         nc.vector.tensor_copy(out=alpha_f[:], in_=alpha_bf[:])
         nc.vector.tensor_copy(out=beta_f[:], in_=beta_bf[:])
-        nc.vector.tensor_copy(out=gamma_f[:], in_=gamma_bf[:])
 
-        row_i32 = const.tile([P, NT], I32)
-        nc.gpsimd.iota(row_i32[:], pattern=[[P, NT]], base=0, channel_multiplier=1)
         row_f = const.tile([P, NT], F32)
         nc.vector.tensor_copy(out=row_f[:], in_=row_i32[:])
         later = const.tile([P, NT], F32)
@@ -112,6 +128,35 @@ def tile_causalshapedattention_pa_t_kernel(tc, q, k, v, alpha, beta, gamma, out)
         nc.vector.tensor_scalar(out=below[:], in0=last_row[:], scalar1=gamma_f[:, 0:1], scalar2=None,
                                 op0=ALU.mult)
 
+        a_tiles = []
+        for s in range(2):
+            row_set = []
+            for i in range(NT):
+                width = 2 * P * passes_of(i)
+                a_t = const.tile([P, 2, width], BF16, name="a%d_%d" % (s, i))
+                used = BLOCK * (i + 1)
+                if used < width:
+                    nc.gpsimd.tensor_scalar(out=a_t[:, :, used:], in0=ones[:, :, :width - used],
+                                            scalar1=above[:, i:i + 1], scalar2=0.0, op0=ALU.mult, op1=ALU.add)
+                row_set.append(a_t)
+            a_tiles.append(row_set)
+
+        def transpose_units(word_views, grouped_words):
+            n_units = len(word_views)
+            bank = psum_t.tile([P, n_units, 2, P], F32, name="bank")
+            for n in range(n_units):
+                for u in range(2):
+                    nc.tensor.transpose(bank[:, n, u, :], word_views[n][:, u, :], ident_f32[:])
+            nc.scalar.copy(out=grouped_words, in_=bank[:].rearrange("p n u i -> p n i u"))
+
+        far_a = const.tile([P, N_FAR, 2, 2 * P], BF16)
+        far_grouped = const.tile([P, N_FAR, P, 4], BF16, align_bytes=64)
+        far_codes = const.tile([P, N_FAR, P], U32, align_bytes=64)
+        far_scales = const.tile([P, N_FAR, P], U8, align_bytes=64)
+        for i in range(N_FAR):
+            nc.gpsimd.tensor_scalar(out=far_a[:, i], in0=ones[:], scalar1=above[:, i:i + 1],
+                                    scalar2=0.0, op0=ALU.mult, op1=ALU.add)
+
         shape_add = const.tile([P, NT, P], F32)
         for i in range(NT):
             nc.vector.tensor_scalar(out=shape_add[:, i, :], in0=upper[:], scalar1=above[:, i:i + 1],
@@ -121,181 +166,209 @@ def tile_causalshapedattention_pa_t_kernel(tc, q, k, v, alpha, beta, gamma, out)
             nc.vector.scalar_tensor_tensor(out=shape_add[:, i, :], in0=diag[:], scalar=alpha_f[:, 0:1],
                                            in1=shape_add[:, i, :], op0=ALU.mult, op1=ALU.add)
 
-        a_tiles = []
-        for s in range(2):
-            row_set = []
-            for i in range(NT):
-                width = 2 * P * passes_of(i)
-                a_t = const.tile([P, 2, width], BF16, name="a%d_%d" % (s, i))
-                used = BLOCK * (i + 1)
-                if used < width:
-                    nc.vector.tensor_scalar(out=a_t[:, :, used:], in0=ones[:, :, :width - used],
-                                            scalar1=above[:, i:i + 1], scalar2=None, op0=ALU.mult)
-                row_set.append(a_t)
-            a_tiles.append(row_set)
+        n_rows = B * H * NT
 
-        def transpose_pair(word_views, grouped_words):
-            bank = psum_t.tile([P, 2, 2, P], F32, name="bank")
-            for n in range(2):
-                for u in range(2):
-                    nc.tensor.transpose(bank[:, n, u, :], word_views[n][:, u, :], ident_f32[:])
-            nc.scalar.copy(out=grouped_words, in_=bank[:].rearrange("p n u i -> p n i u"))
+        def place(r):
+            n, i = divmod(r, NT)
+            b, h = divmod(n, H)
+            return n, i, b, slice(h * D, (h + 1) * D)
 
-        n_far = NT - len([i for i in range(NT) if passes_of(i) == 2])
-        far_a = const.tile([P, n_far, 2, 2 * P], BF16)
-        far_grouped = const.tile([P, n_far, P, 4], BF16, align_bytes=64)
-        far_codes = const.tile([P, n_far, P], U32, align_bytes=64)
-        far_scales = const.tile([P, n_far, P], U8, align_bytes=64)
-        for i in range(n_far):
-            nc.vector.tensor_scalar(out=far_a[:, i], in0=ones[:], scalar1=above[:, i:i + 1],
-                                    scalar2=None, op0=ALU.mult)
-        for g in range(0, n_far, 2):
-            transpose_pair([far_a[:, g + n].bitcast(F32) for n in range(2)],
-                           far_grouped[:, g:g + 2].bitcast(F32))
-        nc.vector.quantize_mx(
-            out=far_codes[:].rearrange("p n i -> p (n i)").bitcast(FP8X4),
-            scales=far_scales[:].rearrange("p n i -> p (n i)"),
-            in_=far_grouped[:].rearrange("p n i t -> p (n i t)"),
-        )
+        def first_of_sequence(r):
+            return r % (H * NT) == 0
 
-        raw = {}
-        values = {}
-        state = {}
-        results = {}
-
-        def load(b):
-            q_sb = loads.tile([P, NT, C], BF16, name="q_sb")
-            k_sb = loads.tile([P, NT, C], BF16, name="k_sb")
-            v_sb = loads.tile([P, 2, 4, C], BF16, name="v_sb")
-            nc.sync.dma_start(out=q_sb[:], in_=q[b, :, :].rearrange("(n p) c -> p n c", p=P))
-            nc.sync.dma_start(out=k_sb[:], in_=k[b, :, :].rearrange("(n p) c -> p n c", p=P))
-            nc.sync.dma_start(out=v_sb[:], in_=v[b, :, :].rearrange("(c p t) w -> p c t w", p=P, t=4))
-            raw[b] = (q_sb, k_sb, v_sb)
-
-        def quantise_v(b):
-            v_sb = raw[b][2]
-            v_grouped = loads.tile([P, 2, C, 4], BF16, name="v_grouped", align_bytes=64)
-            v_codes = loads.tile([P, 2, C], U32, name="v_codes", align_bytes=64)
-            v_scales = loads.tile([P, 2, C], U8, name="v_scales", align_bytes=64)
-            nc.vector.tensor_copy(out=v_grouped[:], in_=v_sb[:].rearrange("p c t w -> p c w t"))
+        def open_job(n, b, cols):
+            v_grouped = heads.tile([P, PASSES, D, 4], BF16, name="v_grouped", align_bytes=64)
+            v_codes = long_lived.tile([P, PASSES, D], U32, name="v_codes", align_bytes=64)
+            v_scales = long_lived.tile([P, PASSES, D], U8, name="v_scales", align_bytes=64)
+            nc.vector.tensor_copy(out=v_grouped[:], in_=raw[b][2][:, :, :, cols].rearrange("p c t w -> p c w t"))
             nc.vector.quantize_mx(
                 out=v_codes[:].rearrange("p c w -> p (c w)").bitcast(FP8X4),
                 scales=v_scales[:].rearrange("p c w -> p (c w)"),
                 in_=v_grouped[:].rearrange("p c w t -> p (c w t)"),
             )
-            values[b] = (v_codes, v_scales)
-            results[b] = loads.tile([P, NT, C], F32, name="out_sb")
+            job[n] = {
+                "v_codes": v_codes, "v_scales": v_scales, "qk_ps": {}, "s": {}, "e": {}, "bank": {},
+                "qkT": heads.tile([P, NT, 2, P], BF16, name="qkT"),
+                "neg_max": heads.tile([P, NT], F32, name="neg_max"),
+                "neg_max_half": heads.tile([P, NT], F32, name="neg_max_half"),
+                "row_sum": heads.tile([P, NT], F32, name="row_sum"),
+            }
 
-        def scores(b, h):
-            q_sb, k_sb = raw[b][0], raw[b][1]
-            cols = slice(h * D, (h + 1) * D)
-            qT_ps = psum_qk.tile([P, NT, P], BF16, name="qk_ps")
-            for n in range(NT):
-                nc.tensor.transpose(qT_ps[:, n, :], q_sb[:, n, cols], ident_bf[:])
-            qT = heads.tile([P, NT, P], BF16, name="qT")
-            nc.vector.tensor_copy(out=qT[:], in_=qT_ps[:])
-            kT_ps = psum_qk.tile([P, NT, P], BF16, name="qk_ps")
-            for n in range(NT):
-                nc.tensor.transpose(kT_ps[:, n, :], k_sb[:, n, cols], key_perm[:])
-            kT = heads.tile([P, 2, HALF], BF16, name="kT")
-            nc.vector.tensor_copy(
-                out=kT[:].rearrange("d u (j x) -> d u j x", x=BLOCK),
-                in_=kT_ps[:].rearrange("d j (u x) -> d u j x", u=2),
-            )
-            neg_max = heads.tile([P, NT], F32, name="neg_max")
-            neg_max_half = heads.tile([P, NT], F32, name="neg_max_half")
-            row_sum = heads.tile([P, NT], F32, name="row_sum")
-            exps = []
-            for i in range(NT):
-                used = BLOCK * (i + 1)
-                s_ps = psum_s.tile([P, 2, BANK], F32, name="s_ps")
-                one_bank = 2 * used <= BANK
-                if one_bank:
-                    s_view = s_ps[:, 0, :2 * used].rearrange("q (u x) -> q u x", u=2)
-                else:
-                    s_view = s_ps[:, :, :used]
-                for u in range(2):
-                    nc.tensor.matmul(s_view[:, u, :], lhsT=qT[:, i, :], rhs=kT[:, u, :used],
-                                     start=True, stop=False)
-                    nc.tensor.matmul(s_view[:, u, used - BLOCK:], lhsT=ident_bf[:],
-                                     rhs=mask_add[:, u * BLOCK:(u + 1) * BLOCK], start=False, stop=True)
-                e_t = heads.tile([P, 2, used], F32, name="e%d" % i)
-                if one_bank:
-                    nc.vector.tensor_scalar(out=e_t[:], in0=s_view, scalar1=-scale, scalar2=None,
-                                            op0=ALU.mult, op1=ALU.min, accum_out=neg_max[:, i:i + 1])
-                else:
-                    nc.vector.tensor_scalar(out=e_t[:, 0, :], in0=s_view[:, 0, :], scalar1=-scale, scalar2=None,
-                                            op0=ALU.mult, op1=ALU.min, accum_out=neg_max_half[:, i:i + 1])
-                    nc.vector.tensor_scalar(out=e_t[:, 1, :], in0=s_view[:, 1, :], scalar1=-scale,
-                                            scalar2=neg_max_half[:, i:i + 1],
-                                            op0=ALU.mult, op1=ALU.min, accum_out=neg_max[:, i:i + 1])
-                nc.scalar.activation(out=e_t[:], in_=e_t[:], func=EXP, bias=neg_max[:, i:i + 1], scale=-1.0,
-                                     accum_out=row_sum[:, i:i + 1])
-                exps.append(e_t)
-            state[(b, h)] = (exps, row_sum)
-
-        def finish(b, h):
-            exps, row_sum = state[(b, h)]
-            row_set = a_tiles[h]
-            v_codes, v_scales = values[b]
-            out_sb = results[b]
-            cols = slice(h * D, (h + 1) * D)
-            gain = heads.tile([P, NT], F32, name="gain")
-            nc.vector.reciprocal(out=gain[:], in_=row_sum[:])
-            nc.vector.tensor_scalar(out=gain[:], in0=gain[:], scalar1=beta_f[:, 0:1], scalar2=None, op0=ALU.mult)
-            for i in range(NT):
-                used = BLOCK * (i + 1)
-                if i > 0:
-                    nc.gpsimd.tensor_scalar(out=row_set[i][:, :, :used - BLOCK], in0=exps[i][:, :, :used - BLOCK],
-                                            scalar1=gain[:, i:i + 1], scalar2=below[:, i:i + 1],
-                                            op0=ALU.mult, op1=ALU.add)
-                nc.vector.scalar_tensor_tensor(
-                    out=row_set[i][:, :, used - BLOCK:used], in0=exps[i][:, :, used - BLOCK:],
-                    scalar=gain[:, i:i + 1], in1=shape_add[:, i, :].rearrange("q (u x) -> q u x", u=2),
-                    op0=ALU.mult, op1=ALU.add)
-            grouped = heads.tile([P, len(UNITS), P, 4], BF16, name="grouped", align_bytes=64)
-            codes = heads.tile([P, len(UNITS), P], U32, name="codes", align_bytes=64)
-            scales = heads.tile([P, len(UNITS), P], U8, name="scales", align_bytes=64)
-            for g in range(0, len(UNITS), 2):
-                views = []
-                for n in range(2):
-                    i, c = UNITS[g + n]
-                    views.append(row_set[i][:].bitcast(F32)[:, :, c * P:(c + 1) * P])
-                transpose_pair(views, grouped[:, g:g + 2].bitcast(F32))
-            for g in range(0, len(UNITS), QUANT_UNITS):
-                nc.vector.quantize_mx(
-                    out=codes[:, g:g + QUANT_UNITS].rearrange("p n i -> p (n i)").bitcast(FP8X4),
-                    scales=scales[:, g:g + QUANT_UNITS].rearrange("p n i -> p (n i)"),
-                    in_=grouped[:, g:g + QUANT_UNITS].rearrange("p n i t -> p (n i t)"),
-                )
-            for g in range(0, NT, 4):
-                o_ps = psum_o.tile([P, 4, P], F32, name="o_ps")
-                for n in range(4):
-                    i = g + n
-                    for c in range(2):
-                        if c < passes_of(i):
-                            unit = UNITS.index((i, c))
-                            a_codes, a_scales = codes[:, unit, :], scales[:, unit, :]
-                        else:
-                            a_codes, a_scales = far_codes[:, i, :], far_scales[:, i, :]
-                        nc.tensor.matmul_mx(
-                            out=o_ps[:, n, :],
-                            lhsT=a_codes.bitcast(FP8X4), lhsT_scale=a_scales,
-                            rhs=v_codes[:, c, cols].bitcast(FP8X4), rhs_scale=v_scales[:, c, cols],
-                            start=(c == 0), stop=(c == 1),
-                        )
-                nc.scalar.copy(out=out_sb[:, g:g + 4, cols], in_=o_ps[:])
-            if h == H - 1:
-                nc.sync.dma_start(out=out[b, :, :].rearrange("(n p) c -> p n c", p=P), in_=out_sb[:])
-
-        jobs = [(b, h) for b in range(B) for h in range(H)]
-        load(0)
-        for n, (b, h) in enumerate(jobs):
-            if h == 0:
-                if b + 1 < B:
+        def qk_transpose(r):
+            n, i, b, cols = place(r)
+            if i == 0:
+                if first_of_sequence(r) and b + 1 < B:
                     load(b + 1)
-                quantise_v(b)
-            scores(b, h)
-            if n > 0:
-                finish(*jobs[n - 1])
-        finish(*jobs[-1])
+                open_job(n, b, cols)
+            qk_ps = psum_qk.tile([P, 2, P], BF16, name="qk_ps")
+            nc.tensor.transpose(qk_ps[:, 0, :], raw[b][0][:, i, cols], ident_bf[:])
+            nc.tensor.transpose(qk_ps[:, 1, :], raw[b][1][:, i, cols], key_perm[:])
+            job[n]["qk_ps"][i] = qk_ps
+
+        def qk_copy(r):
+            n, i, b, cols = place(r)
+            nc.vector.tensor_copy(out=job[n]["qkT"][:, i], in_=job[n]["qk_ps"][i][:])
+
+        def score_row(r):
+            n, i, b, cols = place(r)
+            st = job[n]
+            used = BLOCK * (i + 1)
+            if 2 * used <= BANK:
+                s_ps = psum_s.tile([P, BANK], F32, name="s_ps")
+                halves = [s_ps[:, u * used:(u + 1) * used] for u in range(2)]
+                st["s"][i] = [s_ps[:, :2 * used]]
+            else:
+                halves = []
+                for u in range(2):
+                    s_ps = psum_s.tile([P, BANK], F32, name="s_ps")
+                    halves.append(s_ps[:, :used])
+                st["s"][i] = halves
+            for u in range(2):
+                nc.tensor.matmul(halves[u].rearrange("q (j x) -> q j x", x=BLOCK), lhsT=st["qkT"][:, i, 0, :],
+                                 rhs=st["qkT"][:, :i + 1, 1, u * BLOCK:(u + 1) * BLOCK], start=True, stop=False)
+                nc.tensor.matmul(halves[u][:, used - BLOCK:], lhsT=ident_bf[:],
+                                 rhs=mask_add[:, u * BLOCK:(u + 1) * BLOCK], start=False, stop=True)
+
+        def max_row(r):
+            n, i, b, cols = place(r)
+            st = job[n]
+            used = BLOCK * (i + 1)
+            e_t = heads.tile([P, 2 * used], F32, name="e%d" % i)
+            st["e"][i] = e_t
+            banks = st["s"][i]
+            width = 2 * used // len(banks)
+            start = None
+            for m, s_ap in enumerate(banks):
+                dest = st["neg_max"] if m == len(banks) - 1 else st["neg_max_half"]
+                nc.vector.tensor_scalar(out=e_t[:, m * width:(m + 1) * width], in0=s_ap, scalar1=-scale,
+                                        scalar2=start, op0=ALU.mult, op1=ALU.min,
+                                        accum_out=dest[:, i:i + 1])
+                start = dest[:, i:i + 1]
+
+        def exp_row(r):
+            n, i, b, cols = place(r)
+            st = job[n]
+            nc.scalar.activation(out=st["e"][i][:], in_=st["e"][i][:], func=EXP,
+                                 bias=st["neg_max"][:, i:i + 1], scale=-1.0,
+                                 accum_out=st["row_sum"][:, i:i + 1])
+
+        def diagonal_tile(r):
+            n, i, b, cols = place(r)
+            st = job[n]
+            if i == 0:
+                gain = heads.tile([P, NT], F32, name="gain")
+                nc.vector.reciprocal(out=gain[:], in_=st["row_sum"][:])
+                nc.vector.tensor_scalar(out=gain[:], in0=gain[:], scalar1=beta_f[:, 0:1], scalar2=None,
+                                        op0=ALU.mult)
+                st["gain"] = gain
+                st["grouped"] = heads.tile([P, len(UNITS), P, 4], BF16, name="grouped", align_bytes=64)
+                st["codes"] = heads.tile([P, len(UNITS), P], U32, name="codes", align_bytes=64)
+                st["scales"] = heads.tile([P, len(UNITS), P], U8, name="scales", align_bytes=64)
+            used = BLOCK * (i + 1)
+            e_v = st["e"][i][:].rearrange("q (u x) -> q u x", u=2)
+            nc.vector.scalar_tensor_tensor(
+                out=a_tiles[n % 2][i][:, :, used - BLOCK:used], in0=e_v[:, :, used - BLOCK:],
+                scalar=st["gain"][:, i:i + 1], in1=shape_add[:, i, :].rearrange("q (u x) -> q u x", u=2),
+                op0=ALU.mult, op1=ALU.add)
+
+        def normalise_row(r):
+            n, i, b, cols = place(r)
+            st = job[n]
+            used = BLOCK * (i + 1)
+            if i > 0:
+                e_v = st["e"][i][:].rearrange("q (u x) -> q u x", u=2)
+                nc.gpsimd.tensor_scalar(out=a_tiles[n % 2][i][:, :, :used - BLOCK], in0=e_v[:, :, :used - BLOCK],
+                                        scalar1=st["gain"][:, i:i + 1], scalar2=below[:, i:i + 1],
+                                        op0=ALU.mult, op1=ALU.add)
+
+        def a_transpose(r):
+            n, i, b, cols = place(r)
+            words = a_tiles[n % 2][i][:].bitcast(F32)
+            bank = psum_t.tile([P, passes_of(i), 2, P], F32, name="bank")
+            for c in range(passes_of(i)):
+                for u in range(2):
+                    nc.tensor.transpose(bank[:, c, u, :], words[:, u, c * P:(c + 1) * P], ident_f32[:])
+            job[n]["bank"][i] = bank
+
+        def a_copy(r):
+            n, i, b, cols = place(r)
+            first = UNITS.index((i, 0))
+            nc.scalar.copy(out=job[n]["grouped"][:, first:first + passes_of(i)].bitcast(F32),
+                           in_=job[n]["bank"][i][:].rearrange("p c u i -> p c i u"))
+
+        def group_ending_at(i):
+            end = UNITS.index((i, 0)) + passes_of(i)
+            if end % QUANT_UNITS != 0:
+                return []
+            return [m for m in range(NT) if end - QUANT_UNITS <= UNITS.index((m, 0)) < end]
+
+        def quantise_rows(r):
+            n, i, b, cols = place(r)
+            st = job[n]
+            rows = group_ending_at(i)
+            if rows:
+                g = UNITS.index((rows[0], 0))
+                nc.vector.quantize_mx(
+                    out=st["codes"][:, g:g + QUANT_UNITS].rearrange("p n i -> p (n i)").bitcast(FP8X4),
+                    scales=st["scales"][:, g:g + QUANT_UNITS].rearrange("p n i -> p (n i)"),
+                    in_=st["grouped"][:, g:g + QUANT_UNITS].rearrange("p n i t -> p (n i t)"),
+                )
+
+        def multiply_rows(r):
+            n, i, b, cols = place(r)
+            st = job[n]
+            for m in group_ending_at(i):
+                if m % 4 == 0:
+                    st["o_ps"] = psum_o.tile([P, 4, P], F32, name="o_ps")
+                for c in range(PASSES):
+                    if c < passes_of(m):
+                        unit = UNITS.index((m, c))
+                        a_codes, a_scales = st["codes"][:, unit, :], st["scales"][:, unit, :]
+                    else:
+                        a_codes, a_scales = far_codes[:, m, :], far_scales[:, m, :]
+                    nc.tensor.matmul_mx(
+                        out=st["o_ps"][:, m % 4, :],
+                        lhsT=a_codes.bitcast(FP8X4), lhsT_scale=a_scales,
+                        rhs=st["v_codes"][:, c, :].bitcast(FP8X4), rhs_scale=st["v_scales"][:, c, :],
+                        start=(c == 0), stop=(c == PASSES - 1),
+                    )
+
+        def out_copy(r):
+            n, i, b, cols = place(r)
+            st = job[n]
+            if i == 3:
+                st["out_sb"] = heads.tile([P, NT, D], F32, name="out_sb")
+            if i % 4 == 3:
+                nc.scalar.copy(out=st["out_sb"][:, i - 3:i + 1, :], in_=st["o_ps"][:])
+            if i == NT - 1:
+                nc.sync.dma_start(out=out[b, :, cols].rearrange("(n p) c -> p n c", p=P), in_=st["out_sb"][:])
+
+        def far_units():
+            for g in range(0, N_FAR, 2):
+                transpose_units([far_a[:, g + m].bitcast(F32) for m in range(2)],
+                                far_grouped[:, g:g + 2].bitcast(F32))
+            nc.vector.quantize_mx(
+                out=far_codes[:].rearrange("p n i -> p (n i)").bitcast(FP8X4),
+                scales=far_scales[:].rearrange("p n i -> p (n i)"),
+                in_=far_grouped[:].rearrange("p n i t -> p (n i t)"),
+            )
+
+        def run(stage, r):
+            if 0 <= r < n_rows:
+                stage(r)
+
+        for s in range(-3, n_rows + 18):
+            run(score_row, s + 1)
+            run(qk_copy, s + 2)
+            run(max_row, s)
+            run(a_copy, s - 14)
+            run(out_copy, s - 17)
+            run(exp_row, s)
+            run(diagonal_tile, s - 12)
+            run(normalise_row, s - 12)
+            run(a_transpose, s - 13)
+            run(quantise_rows, s - 15)
+            run(multiply_rows, s - 16)
+            run(qk_transpose, s + 3)
+            if s == FAR_STEP:
+                far_units()

@@ -22,6 +22,7 @@ PASSES = T // K_PASS
 HALF = T // 2
 BLOCK = P // 2
 BANK = 512
+BANK_TILES = BANK // P
 MASKED = -1e20
 FLOPS = 2 * 2 * B * H * T * T * D
 
@@ -43,10 +44,10 @@ def tile_causalshapedattention_pa_t_kernel(tc, q, k, v, alpha, beta, gamma, out)
         const = ctx.enter_context(tc.tile_pool(name="const", bufs=1))
         loads = ctx.enter_context(tc.tile_pool(name="loads", bufs=2))
         heads = ctx.enter_context(tc.tile_pool(name="heads", bufs=2))
-        psum_s = ctx.enter_context(tc.psum_pool(name="psum_s", bufs=4))
+        psum_s = ctx.enter_context(tc.psum_pool(name="psum_s", bufs=3))
         psum_t = ctx.enter_context(tc.psum_pool(name="psum_t", bufs=2))
         psum_o = ctx.enter_context(tc.psum_pool(name="psum_o", bufs=1))
-        psum_qk = ctx.enter_context(tc.psum_pool(name="psum_qk", bufs=1))
+        psum_w = ctx.enter_context(tc.psum_pool(name="psum_w", bufs=1))
         long_lived = ctx.enter_context(tc.tile_pool(name="long_lived", bufs=4))
 
         raw = {}
@@ -165,6 +166,17 @@ def tile_causalshapedattention_pa_t_kernel(tc, q, k, v, alpha, beta, gamma, out)
                                            in1=shape_add[:, i, :], op0=ALU.mult, op1=ALU.add)
             nc.vector.scalar_tensor_tensor(out=shape_add[:, i, :], in0=diag[:], scalar=alpha_f[:, 0:1],
                                            in1=shape_add[:, i, :], op0=ALU.mult, op1=ALU.add)
+        shape_t = const.tile([P, NT, P], F32)
+        shape_ps = psum_w.tile([P, NT, P], F32)
+
+        def shape_to_psum():
+            for g in range(0, NT, BANK_TILES):
+                flipped = psum_t.tile([P, BANK_TILES, P], F32, name="bank")
+                for m in range(BANK_TILES):
+                    nc.tensor.transpose(flipped[:, m, :], shape_add[:, g + m, :], ident_f32[:])
+                nc.vector.tensor_copy(out=shape_t[:, g:g + BANK_TILES, :], in_=flipped[:])
+            for i in range(NT):
+                nc.tensor.transpose(shape_ps[:, i, :], shape_t[:, i, :], ident_f32[:])
 
         n_rows = B * H * NT
 
@@ -200,7 +212,7 @@ def tile_causalshapedattention_pa_t_kernel(tc, q, k, v, alpha, beta, gamma, out)
                 if first_of_sequence(r) and b + 1 < B:
                     load(b + 1)
                 open_job(n, b, cols)
-            qk_ps = psum_qk.tile([P, 2, P], BF16, name="qk_ps")
+            qk_ps = psum_o.tile([P, 2, P], BF16, name="o_ps")
             nc.tensor.transpose(qk_ps[:, 0, :], raw[b][0][:, i, cols], ident_bf[:])
             nc.tensor.transpose(qk_ps[:, 1, :], raw[b][1][:, i, cols], key_perm[:])
             job[n]["qk_ps"][i] = qk_ps
@@ -212,36 +224,27 @@ def tile_causalshapedattention_pa_t_kernel(tc, q, k, v, alpha, beta, gamma, out)
         def score_row(r):
             n, i, b, cols = place(r)
             st = job[n]
-            used = BLOCK * (i + 1)
-            if 2 * used <= BANK:
-                s_ps = psum_s.tile([P, BANK], F32, name="s_ps")
-                halves = [s_ps[:, u * used:(u + 1) * used] for u in range(2)]
-                st["s"][i] = [s_ps[:, :2 * used]]
-            else:
-                halves = []
-                for u in range(2):
-                    s_ps = psum_s.tile([P, BANK], F32, name="s_ps")
-                    halves.append(s_ps[:, :used])
-                st["s"][i] = halves
-            for u in range(2):
-                nc.tensor.matmul(halves[u].rearrange("q (j x) -> q j x", x=BLOCK), lhsT=st["qkT"][:, i, 0, :],
-                                 rhs=st["qkT"][:, :i + 1, 1, u * BLOCK:(u + 1) * BLOCK], start=True, stop=False)
-                nc.tensor.matmul(halves[u][:, used - BLOCK:], lhsT=ident_bf[:],
-                                 rhs=mask_add[:, u * BLOCK:(u + 1) * BLOCK], start=False, stop=True)
+            st["s"][i] = []
+            for j0 in range(0, i + 1, BANK_TILES):
+                tiles = min(BANK_TILES, i + 1 - j0)
+                on_diagonal = j0 + tiles == i + 1
+                s_ps = psum_s.tile([P, BANK_TILES, P], F32, name="s_ps")
+                nc.tensor.matmul(s_ps[:, :tiles, :], lhsT=st["qkT"][:, i, 0, :], rhs=st["qkT"][:, j0:j0 + tiles, 1, :],
+                                 start=True, stop=not on_diagonal)
+                if on_diagonal:
+                    nc.tensor.matmul(s_ps[:, tiles - 1, :], lhsT=ident_bf[:], rhs=mask_add[:], start=False, stop=True)
+                st["s"][i].append(s_ps[:, :tiles, :])
 
         def max_row(r):
             n, i, b, cols = place(r)
             st = job[n]
-            used = BLOCK * (i + 1)
-            e_t = heads.tile([P, 2 * used], F32, name="e%d" % i)
+            e_t = heads.tile([P, i + 1, P], F32, name="e%d" % i)
             st["e"][i] = e_t
-            banks = st["s"][i]
-            width = 2 * used // len(banks)
             start = None
-            for m, s_ap in enumerate(banks):
-                dest = st["neg_max"] if m == len(banks) - 1 else st["neg_max_half"]
-                nc.vector.tensor_scalar(out=e_t[:, m * width:(m + 1) * width], in0=s_ap, scalar1=-scale,
-                                        scalar2=start, op0=ALU.mult, op1=ALU.min,
+            for m, s_ap in enumerate(st["s"][i]):
+                dest = st["neg_max"] if m == len(st["s"][i]) - 1 else st["neg_max_half"]
+                nc.vector.tensor_scalar(out=e_t[:, m * BANK_TILES:min((m + 1) * BANK_TILES, i + 1), :], in0=s_ap,
+                                        scalar1=-scale, scalar2=start, op0=ALU.mult, op1=ALU.min,
                                         accum_out=dest[:, i:i + 1])
                 start = dest[:, i:i + 1]
 
@@ -265,10 +268,10 @@ def tile_causalshapedattention_pa_t_kernel(tc, q, k, v, alpha, beta, gamma, out)
                 st["codes"] = heads.tile([P, len(UNITS), P], U32, name="codes", align_bytes=64)
                 st["scales"] = heads.tile([P, len(UNITS), P], U8, name="scales", align_bytes=64)
             used = BLOCK * (i + 1)
-            e_v = st["e"][i][:].rearrange("q (u x) -> q u x", u=2)
             nc.vector.scalar_tensor_tensor(
-                out=a_tiles[n % 2][i][:, :, used - BLOCK:used], in0=e_v[:, :, used - BLOCK:],
-                scalar=st["gain"][:, i:i + 1], in1=shape_add[:, i, :].rearrange("q (u x) -> q u x", u=2),
+                out=a_tiles[n % 2][i][:, :, used - BLOCK:used],
+                in0=st["e"][i][:, i, :].rearrange("q (u x) -> q u x", u=2),
+                scalar=st["gain"][:, i:i + 1], in1=shape_ps[:, i, :].rearrange("q (u x) -> q u x", u=2),
                 op0=ALU.mult, op1=ALU.add)
 
         def normalise_row(r):
@@ -276,8 +279,8 @@ def tile_causalshapedattention_pa_t_kernel(tc, q, k, v, alpha, beta, gamma, out)
             st = job[n]
             used = BLOCK * (i + 1)
             if i > 0:
-                e_v = st["e"][i][:].rearrange("q (u x) -> q u x", u=2)
-                nc.gpsimd.tensor_scalar(out=a_tiles[n % 2][i][:, :, :used - BLOCK], in0=e_v[:, :, :used - BLOCK],
+                nc.gpsimd.tensor_scalar(out=a_tiles[n % 2][i][:, :, :used - BLOCK].rearrange("q u (j x) -> q u j x", x=BLOCK),
+                                        in0=st["e"][i][:, :i, :].rearrange("q j (u x) -> q u j x", u=2),
                                         scalar1=st["gain"][:, i:i + 1], scalar2=below[:, i:i + 1],
                                         op0=ALU.mult, op1=ALU.add)
 
@@ -371,4 +374,5 @@ def tile_causalshapedattention_pa_t_kernel(tc, q, k, v, alpha, beta, gamma, out)
             run(multiply_rows, s - 16)
             run(qk_transpose, s + 3)
             if s == FAR_STEP:
+                shape_to_psum()
                 far_units()

@@ -11,7 +11,7 @@ U32 = mybir.dt.uint32
 U8 = mybir.dt.uint8
 FP8X4 = mybir.dt.float8_e4m3fn_x4
 ALU = mybir.AluOpType
-EXP = mybir.ActivationFunctionType.Exp
+ACT = mybir.ActivationFunctionType
 
 B, T, C, H = 8, 1024, 256, 2
 D = C // H
@@ -19,7 +19,6 @@ P = 128
 NT = T // P
 K_PASS = 4 * P
 PASSES = T // K_PASS
-HALF = T // 2
 BLOCK = P // 2
 BANK = 512
 BANK_TILES = BANK // P
@@ -34,6 +33,7 @@ def passes_of(i):
 UNITS = [(i, c) for i in range(NT) for c in range(passes_of(i))]
 QUANT_UNITS = 4
 N_FAR = len([i for i in range(NT) if passes_of(i) < PASSES])
+CONST_STEP = 0
 FAR_STEP = 8
 
 
@@ -44,11 +44,11 @@ def tile_causalshapedattention_pa_t_kernel(tc, q, k, v, alpha, beta, gamma, out)
         const = ctx.enter_context(tc.tile_pool(name="const", bufs=1))
         loads = ctx.enter_context(tc.tile_pool(name="loads", bufs=2))
         heads = ctx.enter_context(tc.tile_pool(name="heads", bufs=2))
-        psum_s = ctx.enter_context(tc.psum_pool(name="psum_s", bufs=3))
+        long_lived = ctx.enter_context(tc.tile_pool(name="long_lived", bufs=4))
+        psum_s = ctx.enter_context(tc.psum_pool(name="psum_s", bufs=4))
         psum_t = ctx.enter_context(tc.psum_pool(name="psum_t", bufs=2))
         psum_o = ctx.enter_context(tc.psum_pool(name="psum_o", bufs=1))
-        psum_w = ctx.enter_context(tc.psum_pool(name="psum_w", bufs=1))
-        long_lived = ctx.enter_context(tc.tile_pool(name="long_lived", bufs=4))
+        psum_qk = ctx.enter_context(tc.psum_pool(name="psum_qk", bufs=1))
 
         raw = {}
         job = {}
@@ -57,8 +57,11 @@ def tile_causalshapedattention_pa_t_kernel(tc, q, k, v, alpha, beta, gamma, out)
             q_sb = loads.tile([P, NT, C], BF16, name="q_sb")
             k_sb = loads.tile([P, NT, C], BF16, name="k_sb")
             v_sb = loads.tile([P, PASSES, 4, C], BF16, name="v_sb")
-            nc.sync.dma_start(out=q_sb[:], in_=q[b, :, :].rearrange("(n p) c -> p n c", p=P))
-            nc.sync.dma_start(out=k_sb[:], in_=k[b, :, :].rearrange("(n p) c -> p n c", p=P))
+            for first in range(0, NT, NT // 2):
+                tiles = slice(first, first + NT // 2)
+                rows = slice(first * P, (first + NT // 2) * P)
+                nc.sync.dma_start(out=q_sb[:, tiles, :], in_=q[b, rows, :].rearrange("(n p) c -> p n c", p=P))
+                nc.sync.dma_start(out=k_sb[:, tiles, :], in_=k[b, rows, :].rearrange("(n p) c -> p n c", p=P))
             nc.sync.dma_start(out=v_sb[:], in_=v[b, :, :].rearrange("(c p t) w -> p c t w", p=P, t=4))
             raw[b] = (q_sb, k_sb, v_sb)
 
@@ -70,113 +73,98 @@ def tile_causalshapedattention_pa_t_kernel(tc, q, k, v, alpha, beta, gamma, out)
         nc.scalar.dma_start(out=beta_bf[:], in_=beta.partition_broadcast(P))
         load(0)
 
-        ident_bf = const.tile([P, P], BF16)
-        make_identity(nc, ident_bf[:])
-        ident_f32 = const.tile([P, P], F32)
-        make_identity(nc, ident_f32[:])
-        lower_nat = const.tile([P, P], F32)
-        nc.gpsimd.memset(lower_nat[:], 1.0)
-        nc.gpsimd.affine_select(
-            out=lower_nat[:], in_=lower_nat[:], compare_op=ALU.is_ge, fill=0.0,
-            base=0, pattern=[[-1, P]], channel_multiplier=1,
-        )
-        row_i32 = const.tile([P, NT], I32)
-        nc.gpsimd.iota(row_i32[:], pattern=[[P, NT]], base=0, channel_multiplier=1)
-        ones = const.tile([P, 2, 2 * P], F32)
-        nc.gpsimd.memset(ones[:], 1.0)
-
         def to_key_order(dst, src):
             nc.vector.tensor_copy(
                 out=dst[:].rearrange("k (u p e) -> k u p e", u=2, e=2),
                 in_=src[:].rearrange("k (p u e) -> k u p e", u=2, e=2),
             )
 
+        ident_bf = const.tile([P, P], BF16)
+        make_identity(nc, ident_bf[:])
         key_perm = const.tile([P, P], BF16)
         to_key_order(key_perm, ident_bf)
+        lower_nat = const.tile([P, P], F32)
+        nc.gpsimd.memset(lower_nat[:], 1.0)
+        nc.gpsimd.affine_select(
+            out=lower_nat[:], in_=lower_nat[:], compare_op=ALU.is_ge, fill=0.0,
+            base=0, pattern=[[-1, P]], channel_multiplier=1,
+        )
         lower = const.tile([P, P], F32)
         to_key_order(lower, lower_nat)
-        diag = const.tile([P, P], F32)
-        to_key_order(diag, ident_f32)
-        upper = const.tile([P, P], F32)
-        nc.vector.tensor_scalar(out=upper[:], in0=lower[:], scalar1=-1.0, scalar2=1.0,
-                                op0=ALU.mult, op1=ALU.add)
         mask_add = const.tile([P, P], BF16)
-        nc.vector.tensor_scalar(out=mask_add[:], in0=upper[:], scalar1=MASKED, scalar2=None,
-                                op0=ALU.mult)
-
-        alpha_f = const.tile([P, 1], F32)
-        beta_f = const.tile([P, 1], F32)
-        gamma_f = const.tile([P, 1], F32)
-        nc.vector.tensor_copy(out=gamma_f[:], in_=gamma_bf[:])
-        nc.vector.tensor_copy(out=alpha_f[:], in_=alpha_bf[:])
-        nc.vector.tensor_copy(out=beta_f[:], in_=beta_bf[:])
-
-        row_f = const.tile([P, NT], F32)
-        nc.vector.tensor_copy(out=row_f[:], in_=row_i32[:])
-        later = const.tile([P, NT], F32)
-        nc.vector.tensor_scalar(out=later[:], in0=row_f[:], scalar1=-1.0, scalar2=float(T - 1),
+        nc.vector.tensor_scalar(out=mask_add[:], in0=lower[:], scalar1=-MASKED, scalar2=MASKED,
                                 op0=ALU.mult, op1=ALU.add)
-        nc.vector.tensor_scalar_max(out=later[:], in0=later[:], scalar1=1.0)
-        inv_later = const.tile([P, NT], F32)
-        nc.vector.reciprocal(out=inv_later[:], in_=later[:])
+
+        ident_f32 = const.tile([P, P], F32)
+        diag = const.tile([P, P], F32)
+        ones = const.tile([P, 2, 2 * P], F32)
+        beta_f = const.tile([P, 1], F32)
         above = const.tile([P, NT], F32)
-        nc.vector.tensor_scalar(out=above[:], in0=inv_later[:], scalar1=gamma_f[:, 0:1], scalar2=-1.0,
-                                op0=ALU.mult, op1=ALU.mult)
-        last_row = const.tile([P, NT], F32)
-        nc.vector.tensor_scalar(out=last_row[:], in0=row_f[:], scalar1=float(T - 1), scalar2=-1.0 / T,
-                                op0=ALU.is_equal, op1=ALU.mult)
         below = const.tile([P, NT], F32)
-        nc.vector.tensor_scalar(out=below[:], in0=last_row[:], scalar1=gamma_f[:, 0:1], scalar2=None,
-                                op0=ALU.mult)
-
-        a_tiles = []
-        for s in range(2):
-            row_set = []
-            for i in range(NT):
-                width = 2 * P * passes_of(i)
-                a_t = const.tile([P, 2, width], BF16, name="a%d_%d" % (s, i))
-                used = BLOCK * (i + 1)
-                if used < width:
-                    nc.gpsimd.tensor_scalar(out=a_t[:, :, used:], in0=ones[:, :, :width - used],
-                                            scalar1=above[:, i:i + 1], scalar2=0.0, op0=ALU.mult, op1=ALU.add)
-                row_set.append(a_t)
-            a_tiles.append(row_set)
-
-        def transpose_units(word_views, grouped_words):
-            n_units = len(word_views)
-            bank = psum_t.tile([P, n_units, 2, P], F32, name="bank")
-            for n in range(n_units):
-                for u in range(2):
-                    nc.tensor.transpose(bank[:, n, u, :], word_views[n][:, u, :], ident_f32[:])
-            nc.scalar.copy(out=grouped_words, in_=bank[:].rearrange("p n u i -> p n i u"))
-
+        shape_add = const.tile([P, NT, P], F32)
+        a_tiles = [[const.tile([P, 2, 2 * P * passes_of(i)], BF16, name="a%d_%d" % (s, i)) for i in range(NT)]
+                   for s in range(2)]
         far_a = const.tile([P, N_FAR, 2, 2 * P], BF16)
         far_grouped = const.tile([P, N_FAR, P, 4], BF16, align_bytes=64)
         far_codes = const.tile([P, N_FAR, P], U32, align_bytes=64)
         far_scales = const.tile([P, N_FAR, P], U8, align_bytes=64)
-        for i in range(N_FAR):
-            nc.gpsimd.tensor_scalar(out=far_a[:, i], in0=ones[:], scalar1=above[:, i:i + 1],
-                                    scalar2=0.0, op0=ALU.mult, op1=ALU.add)
 
-        shape_add = const.tile([P, NT, P], F32)
-        for i in range(NT):
-            nc.vector.tensor_scalar(out=shape_add[:, i, :], in0=upper[:], scalar1=above[:, i:i + 1],
-                                    scalar2=None, op0=ALU.mult)
-            nc.vector.scalar_tensor_tensor(out=shape_add[:, i, :], in0=lower[:], scalar=below[:, i:i + 1],
-                                           in1=shape_add[:, i, :], op0=ALU.mult, op1=ALU.add)
-            nc.vector.scalar_tensor_tensor(out=shape_add[:, i, :], in0=diag[:], scalar=alpha_f[:, 0:1],
-                                           in1=shape_add[:, i, :], op0=ALU.mult, op1=ALU.add)
-        shape_t = const.tile([P, NT, P], F32)
-        shape_ps = psum_w.tile([P, NT, P], F32)
-
-        def shape_to_psum():
-            for g in range(0, NT, BANK_TILES):
-                flipped = psum_t.tile([P, BANK_TILES, P], F32, name="bank")
-                for m in range(BANK_TILES):
-                    nc.tensor.transpose(flipped[:, m, :], shape_add[:, g + m, :], ident_f32[:])
-                nc.vector.tensor_copy(out=shape_t[:, g:g + BANK_TILES, :], in_=flipped[:])
+        def late_constants():
+            make_identity(nc, ident_f32[:])
+            to_key_order(diag, ident_f32)
+            nc.gpsimd.memset(ones[:], 1.0)
+            alpha_f = const.tile([P, 1], F32)
+            gamma_f = const.tile([P, 1], F32)
+            nc.vector.tensor_copy(out=gamma_f[:], in_=gamma_bf[:])
+            nc.vector.tensor_copy(out=alpha_f[:], in_=alpha_bf[:])
+            nc.vector.tensor_copy(out=beta_f[:], in_=beta_bf[:])
+            row_i32 = const.tile([P, NT], I32)
+            nc.gpsimd.iota(row_i32[:], pattern=[[P, NT]], base=0, channel_multiplier=1)
+            row_f = const.tile([P, NT], F32)
+            nc.vector.tensor_copy(out=row_f[:], in_=row_i32[:])
+            is_last = const.tile([P, NT], F32)
+            nc.vector.tensor_scalar(out=is_last[:], in0=row_f[:], scalar1=float(T - 1), scalar2=None,
+                                    op0=ALU.is_equal)
+            spread = const.tile([P, NT], F32)
+            nc.vector.tensor_scalar(out=spread[:], in0=row_f[:], scalar1=-1.0, scalar2=float(T - 1),
+                                    op0=ALU.mult, op1=ALU.add)
+            nc.vector.scalar_tensor_tensor(out=spread[:], in0=is_last[:], scalar=float(T), in1=spread[:],
+                                           op0=ALU.mult, op1=ALU.add)
+            nc.vector.reciprocal(out=spread[:], in_=spread[:])
+            nc.vector.tensor_scalar(out=above[:], in0=spread[:], scalar1=gamma_f[:, 0:1], scalar2=-1.0,
+                                    op0=ALU.mult, op1=ALU.mult)
+            nc.vector.tensor_tensor(out=below[:], in0=above[:], in1=is_last[:], op=ALU.mult)
+            step_down = const.tile([P, NT], F32)
+            nc.vector.tensor_tensor(out=step_down[:], in0=below[:], in1=above[:], op=ALU.subtract)
             for i in range(NT):
-                nc.tensor.transpose(shape_ps[:, i, :], shape_t[:, i, :], ident_f32[:])
+                nc.scalar.activation(out=shape_add[:, i, :], in_=lower[:], func=ACT.Identity,
+                                     bias=above[:, i:i + 1], scale=step_down[:, i:i + 1])
+            for i in range(NT):
+                nc.vector.scalar_tensor_tensor(out=shape_add[:, i, :], in0=diag[:], scalar=alpha_f[:, 0:1],
+                                               in1=shape_add[:, i, :], op0=ALU.mult, op1=ALU.add)
+            for row_set in a_tiles:
+                for i in range(NT):
+                    used = BLOCK * (i + 1)
+                    width = 2 * P * passes_of(i)
+                    if used < width:
+                        nc.gpsimd.tensor_scalar(out=row_set[i][:, :, used:], in0=ones[:, :, :width - used],
+                                                scalar1=above[:, i:i + 1], scalar2=0.0, op0=ALU.mult, op1=ALU.add)
+            for i in range(N_FAR):
+                nc.gpsimd.tensor_scalar(out=far_a[:, i], in0=ones[:], scalar1=above[:, i:i + 1],
+                                        scalar2=0.0, op0=ALU.mult, op1=ALU.add)
+
+        def far_units():
+            for g in range(0, N_FAR, 2):
+                bank = psum_t.tile([P, 2, 2, P], F32, name="bank")
+                for m in range(2):
+                    for u in range(2):
+                        nc.tensor.transpose(bank[:, m, u, :], far_a[:, g + m].bitcast(F32)[:, u, :], ident_f32[:])
+                nc.scalar.copy(out=far_grouped[:, g:g + 2].bitcast(F32), in_=bank[:].rearrange("p c u i -> p c i u"))
+            nc.vector.quantize_mx(
+                out=far_codes[:].rearrange("p n i -> p (n i)").bitcast(FP8X4),
+                scales=far_scales[:].rearrange("p n i -> p (n i)"),
+                in_=far_grouped[:].rearrange("p n i t -> p (n i t)"),
+            )
 
         n_rows = B * H * NT
 
@@ -188,31 +176,37 @@ def tile_causalshapedattention_pa_t_kernel(tc, q, k, v, alpha, beta, gamma, out)
         def first_of_sequence(r):
             return r % (H * NT) == 0
 
-        def open_job(n, b, cols):
-            v_grouped = heads.tile([P, PASSES, D, 4], BF16, name="v_grouped", align_bytes=64)
-            v_codes = long_lived.tile([P, PASSES, D], U32, name="v_codes", align_bytes=64)
-            v_scales = long_lived.tile([P, PASSES, D], U8, name="v_scales", align_bytes=64)
-            nc.vector.tensor_copy(out=v_grouped[:], in_=raw[b][2][:, :, :, cols].rearrange("p c t w -> p c w t"))
-            nc.vector.quantize_mx(
-                out=v_codes[:].rearrange("p c w -> p (c w)").bitcast(FP8X4),
-                scales=v_scales[:].rearrange("p c w -> p (c w)"),
-                in_=v_grouped[:].rearrange("p c w t -> p (c w t)"),
-            )
+        def open_job(n):
             job[n] = {
-                "v_codes": v_codes, "v_scales": v_scales, "qk_ps": {}, "s": {}, "e": {}, "bank": {},
+                "qk_ps": {}, "s": {}, "e": {}, "bank": {},
                 "qkT": heads.tile([P, NT, 2, P], BF16, name="qkT"),
                 "neg_max": heads.tile([P, NT], F32, name="neg_max"),
                 "neg_max_half": heads.tile([P, NT], F32, name="neg_max_half"),
                 "row_sum": heads.tile([P, NT], F32, name="row_sum"),
             }
 
+        def quantise_v(r):
+            n, i, b, cols = place(r)
+            if i == 0:
+                v_grouped = heads.tile([P, PASSES, D, 4], BF16, name="v_grouped", align_bytes=64)
+                v_codes = long_lived.tile([P, PASSES, D], U32, name="v_codes", align_bytes=64)
+                v_scales = long_lived.tile([P, PASSES, D], U8, name="v_scales", align_bytes=64)
+                nc.gpsimd.tensor_scalar(out=v_grouped[:], in0=raw[b][2][:, :, :, cols].rearrange("p c t w -> p c w t"),
+                                        scalar1=1.0, scalar2=0.0, op0=ALU.mult, op1=ALU.add)
+                nc.vector.quantize_mx(
+                    out=v_codes[:].rearrange("p c w -> p (c w)").bitcast(FP8X4),
+                    scales=v_scales[:].rearrange("p c w -> p (c w)"),
+                    in_=v_grouped[:].rearrange("p c w t -> p (c w t)"),
+                )
+                job[n]["v_codes"], job[n]["v_scales"] = v_codes, v_scales
+
         def qk_transpose(r):
             n, i, b, cols = place(r)
             if i == 0:
                 if first_of_sequence(r) and b + 1 < B:
                     load(b + 1)
-                open_job(n, b, cols)
-            qk_ps = psum_o.tile([P, 2, P], BF16, name="o_ps")
+                open_job(n)
+            qk_ps = psum_qk.tile([P, 2, P], BF16, name="qk_ps")
             nc.tensor.transpose(qk_ps[:, 0, :], raw[b][0][:, i, cols], ident_bf[:])
             nc.tensor.transpose(qk_ps[:, 1, :], raw[b][1][:, i, cols], key_perm[:])
             job[n]["qk_ps"][i] = qk_ps
@@ -235,23 +229,29 @@ def tile_causalshapedattention_pa_t_kernel(tc, q, k, v, alpha, beta, gamma, out)
                     nc.tensor.matmul(s_ps[:, tiles - 1, :], lhsT=ident_bf[:], rhs=mask_add[:], start=False, stop=True)
                 st["s"][i].append(s_ps[:, :tiles, :])
 
-        def max_row(r):
+        def max_bank(r, m):
             n, i, b, cols = place(r)
             st = job[n]
-            e_t = heads.tile([P, i + 1, P], F32, name="e%d" % i)
-            st["e"][i] = e_t
-            start = None
-            for m, s_ap in enumerate(st["s"][i]):
-                dest = st["neg_max"] if m == len(st["s"][i]) - 1 else st["neg_max_half"]
-                nc.vector.tensor_scalar(out=e_t[:, m * BANK_TILES:min((m + 1) * BANK_TILES, i + 1), :], in0=s_ap,
-                                        scalar1=-scale, scalar2=start, op0=ALU.mult, op1=ALU.min,
-                                        accum_out=dest[:, i:i + 1])
-                start = dest[:, i:i + 1]
+            banks = st["s"][i]
+            if m == 0:
+                st["e"][i] = heads.tile([P, i + 1, P], F32, name="e%d" % i)
+            if m < len(banks):
+                dest = st["neg_max"] if m == len(banks) - 1 else st["neg_max_half"]
+                nc.vector.tensor_scalar(out=st["e"][i][:, m * BANK_TILES:min((m + 1) * BANK_TILES, i + 1), :],
+                                        in0=banks[m], scalar1=-scale,
+                                        scalar2=st["neg_max_half"][:, i:i + 1] if m > 0 else None,
+                                        op0=ALU.mult, op1=ALU.min, accum_out=dest[:, i:i + 1])
+
+        def max_first_bank(r):
+            max_bank(r, 0)
+
+        def max_second_bank(r):
+            max_bank(r, 1)
 
         def exp_row(r):
             n, i, b, cols = place(r)
             st = job[n]
-            nc.scalar.activation(out=st["e"][i][:], in_=st["e"][i][:], func=EXP,
+            nc.scalar.activation(out=st["e"][i][:], in_=st["e"][i][:], func=ACT.Exp,
                                  bias=st["neg_max"][:, i:i + 1], scale=-1.0,
                                  accum_out=st["row_sum"][:, i:i + 1])
 
@@ -271,7 +271,7 @@ def tile_causalshapedattention_pa_t_kernel(tc, q, k, v, alpha, beta, gamma, out)
             nc.vector.scalar_tensor_tensor(
                 out=a_tiles[n % 2][i][:, :, used - BLOCK:used],
                 in0=st["e"][i][:, i, :].rearrange("q (u x) -> q u x", u=2),
-                scalar=st["gain"][:, i:i + 1], in1=shape_ps[:, i, :].rearrange("q (u x) -> q u x", u=2),
+                scalar=st["gain"][:, i:i + 1], in1=shape_add[:, i, :].rearrange("q (u x) -> q u x", u=2),
                 op0=ALU.mult, op1=ALU.add)
 
         def normalise_row(r):
@@ -346,33 +346,26 @@ def tile_causalshapedattention_pa_t_kernel(tc, q, k, v, alpha, beta, gamma, out)
             if i == NT - 1:
                 nc.sync.dma_start(out=out[b, :, cols].rearrange("(n p) c -> p n c", p=P), in_=st["out_sb"][:])
 
-        def far_units():
-            for g in range(0, N_FAR, 2):
-                transpose_units([far_a[:, g + m].bitcast(F32) for m in range(2)],
-                                far_grouped[:, g:g + 2].bitcast(F32))
-            nc.vector.quantize_mx(
-                out=far_codes[:].rearrange("p n i -> p (n i)").bitcast(FP8X4),
-                scales=far_scales[:].rearrange("p n i -> p (n i)"),
-                in_=far_grouped[:].rearrange("p n i t -> p (n i t)"),
-            )
-
         def run(stage, r):
             if 0 <= r < n_rows:
                 stage(r)
 
         for s in range(-3, n_rows + 18):
             run(score_row, s + 1)
+            run(max_first_bank, s)
             run(qk_copy, s + 2)
-            run(max_row, s)
+            run(diagonal_tile, s - 12)
+            run(max_second_bank, s)
             run(a_copy, s - 14)
             run(out_copy, s - 17)
             run(exp_row, s)
-            run(diagonal_tile, s - 12)
             run(normalise_row, s - 12)
             run(a_transpose, s - 13)
             run(quantise_rows, s - 15)
             run(multiply_rows, s - 16)
             run(qk_transpose, s + 3)
+            run(quantise_v, s - 2)
+            if s == CONST_STEP:
+                late_constants()
             if s == FAR_STEP:
-                shape_to_psum()
                 far_units()

@@ -342,7 +342,7 @@ def tile_causalshapedattention_pa_t_kernel(tc, q, k, v, alpha, beta, gamma, out)
             if i == 3:
                 st["out_sb"] = heads.tile([P, NT, D], F32, name="out_sb")
             if i % 4 == 3:
-                nc.scalar.copy(out=st["out_sb"][:, i - 3:i + 1, :], in_=st["o_ps"][:])
+                nc.vector.tensor_copy(out=st["out_sb"][:, i - 3:i + 1, :], in_=st["o_ps"][:])
             if i == NT - 1:
                 nc.sync.dma_start(out=out[b, :, cols].rearrange("(n p) c -> p n c", p=P), in_=st["out_sb"][:])
 

@@ -213,7 +213,7 @@ def tile_causalshapedattention_pa_t_kernel(tc, q, k, v, alpha, beta, gamma, out)
 
         def qk_copy(r):
             n, i, b, cols = place(r)
-            nc.vector.tensor_copy(out=job[n]["qkT"][:, i], in_=job[n]["qk_ps"][i][:])
+            nc.scalar.copy(out=job[n]["qkT"][:, i], in_=job[n]["qk_ps"][i][:])
 
         def score_row(r):
             n, i, b, cols = place(r)
@@ -342,7 +342,7 @@ def tile_causalshapedattention_pa_t_kernel(tc, q, k, v, alpha, beta, gamma, out)
             if i == 3:
                 st["out_sb"] = heads.tile([P, NT, D], F32, name="out_sb")
             if i % 4 == 3:
-                nc.vector.tensor_copy(out=st["out_sb"][:, i - 3:i + 1, :], in_=st["o_ps"][:])
+                nc.scalar.copy(out=st["out_sb"][:, i - 3:i + 1, :], in_=st["o_ps"][:])
             if i == NT - 1:
                 nc.sync.dma_start(out=out[b, :, cols].rearrange("(n p) c -> p n c", p=P), in_=st["out_sb"][:])
 

@@ -31,6 +31,7 @@ def passes_of(i):
 
 
 UNITS = [(i, c) for i in range(NT) for c in range(passes_of(i))]
+BANK_UNITS = 2
 QUANT_UNITS = 4
 N_FAR = len([i for i in range(NT) if passes_of(i) < PASSES])
 CONST_STEP = 0
@@ -178,8 +179,9 @@ def tile_causalshapedattention_pa_t_kernel(tc, q, k, v, alpha, beta, gamma, out)
 
         def open_job(n):
             job[n] = {
-                "qk_ps": {}, "s": {}, "e": {}, "bank": {},
-                "qkT": heads.tile([P, NT, 2, P], BF16, name="qkT"),
+                "s": {}, "e": {}, "bank": {},
+                "qT": heads.tile([P, NT, P], BF16, name="qT"),
+                "kT": heads.tile([P, NT, P], BF16, name="kT"),
                 "neg_max": heads.tile([P, NT], F32, name="neg_max"),
                 "neg_max_half": heads.tile([P, NT], F32, name="neg_max_half"),
                 "row_sum": heads.tile([P, NT], F32, name="row_sum"),
@@ -200,20 +202,24 @@ def tile_causalshapedattention_pa_t_kernel(tc, q, k, v, alpha, beta, gamma, out)
                 )
                 job[n]["v_codes"], job[n]["v_scales"] = v_codes, v_scales
 
-        def qk_transpose(r):
+        def q_transpose(r):
             n, i, b, cols = place(r)
             if i == 0:
                 if first_of_sequence(r) and b + 1 < B:
                     load(b + 1)
                 open_job(n)
-            qk_ps = psum_qk.tile([P, 2, P], BF16, name="qk_ps")
-            nc.tensor.transpose(qk_ps[:, 0, :], raw[b][0][:, i, cols], ident_bf[:])
-            nc.tensor.transpose(qk_ps[:, 1, :], raw[b][1][:, i, cols], key_perm[:])
-            job[n]["qk_ps"][i] = qk_ps
+                qT_ps = psum_qk.tile([P, NT, P], BF16, name="qk_ps")
+                for t in range(NT):
+                    nc.tensor.transpose(qT_ps[:, t, :], raw[b][0][:, t, cols], ident_bf[:])
+                nc.scalar.copy(out=job[n]["qT"][:], in_=qT_ps[:])
 
-        def qk_copy(r):
+        def k_transpose(r):
             n, i, b, cols = place(r)
-            nc.scalar.copy(out=job[n]["qkT"][:, i], in_=job[n]["qk_ps"][i][:])
+            if i == 0:
+                kT_ps = psum_qk.tile([P, NT, P], BF16, name="qk_ps")
+                for t in range(NT):
+                    nc.tensor.transpose(kT_ps[:, t, :], raw[b][1][:, t, cols], key_perm[:])
+                nc.vector.tensor_copy(out=job[n]["kT"][:], in_=kT_ps[:])
 
         def score_row(r):
             n, i, b, cols = place(r)
@@ -223,7 +229,7 @@ def tile_causalshapedattention_pa_t_kernel(tc, q, k, v, alpha, beta, gamma, out)
                 tiles = min(BANK_TILES, i + 1 - j0)
                 on_diagonal = j0 + tiles == i + 1
                 s_ps = psum_s.tile([P, BANK_TILES, P], F32, name="s_ps")
-                nc.tensor.matmul(s_ps[:, :tiles, :], lhsT=st["qkT"][:, i, 0, :], rhs=st["qkT"][:, j0:j0 + tiles, 1, :],
+                nc.tensor.matmul(s_ps[:, :tiles, :], lhsT=st["qT"][:, i, :], rhs=st["kT"][:, j0:j0 + tiles, :],
                                  start=True, stop=not on_diagonal)
                 if on_diagonal:
                     nc.tensor.matmul(s_ps[:, tiles - 1, :], lhsT=ident_bf[:], rhs=mask_add[:], start=False, stop=True)
@@ -284,31 +290,37 @@ def tile_causalshapedattention_pa_t_kernel(tc, q, k, v, alpha, beta, gamma, out)
                                         scalar1=st["gain"][:, i:i + 1], scalar2=below[:, i:i + 1],
                                         op0=ALU.mult, op1=ALU.add)
 
+        def rows_filling(i, n_units):
+            end = UNITS.index((i, 0)) + passes_of(i)
+            if end % n_units != 0:
+                return []
+            return [m for m in range(NT) if end - n_units <= UNITS.index((m, 0)) < end]
+
         def a_transpose(r):
             n, i, b, cols = place(r)
-            words = a_tiles[n % 2][i][:].bitcast(F32)
-            bank = psum_t.tile([P, passes_of(i), 2, P], F32, name="bank")
-            for c in range(passes_of(i)):
-                for u in range(2):
-                    nc.tensor.transpose(bank[:, c, u, :], words[:, u, c * P:(c + 1) * P], ident_f32[:])
-            job[n]["bank"][i] = bank
+            rows = rows_filling(i, BANK_UNITS)
+            if rows:
+                bank = psum_t.tile([P, BANK_UNITS, 2, P], F32, name="bank")
+                first = UNITS.index((rows[0], 0))
+                for m, c in UNITS[first:first + BANK_UNITS]:
+                    words = a_tiles[n % 2][m][:].bitcast(F32)
+                    for u in range(2):
+                        nc.tensor.transpose(bank[:, UNITS.index((m, c)) - first, u, :],
+                                            words[:, u, c * P:(c + 1) * P], ident_f32[:])
+                job[n]["bank"][i] = bank
 
         def a_copy(r):
             n, i, b, cols = place(r)
-            first = UNITS.index((i, 0))
-            nc.scalar.copy(out=job[n]["grouped"][:, first:first + passes_of(i)].bitcast(F32),
-                           in_=job[n]["bank"][i][:].rearrange("p c u i -> p c i u"))
-
-        def group_ending_at(i):
-            end = UNITS.index((i, 0)) + passes_of(i)
-            if end % QUANT_UNITS != 0:
-                return []
-            return [m for m in range(NT) if end - QUANT_UNITS <= UNITS.index((m, 0)) < end]
+            rows = rows_filling(i, BANK_UNITS)
+            if rows:
+                first = UNITS.index((rows[0], 0))
+                nc.scalar.copy(out=job[n]["grouped"][:, first:first + BANK_UNITS].bitcast(F32),
+                               in_=job[n]["bank"][i][:].rearrange("p c u i -> p c i u"))
 
         def quantise_rows(r):
             n, i, b, cols = place(r)
             st = job[n]
-            rows = group_ending_at(i)
+            rows = rows_filling(i, QUANT_UNITS)
             if rows:
                 g = UNITS.index((rows[0], 0))
                 nc.vector.quantize_mx(
@@ -320,7 +332,7 @@ def tile_causalshapedattention_pa_t_kernel(tc, q, k, v, alpha, beta, gamma, out)
         def multiply_rows(r):
             n, i, b, cols = place(r)
             st = job[n]
-            for m in group_ending_at(i):
+            for m in rows_filling(i, QUANT_UNITS):
                 if m % 4 == 0:
                     st["o_ps"] = psum_o.tile([P, 4, P], F32, name="o_ps")
                 for c in range(PASSES):
@@ -350,10 +362,9 @@ def tile_causalshapedattention_pa_t_kernel(tc, q, k, v, alpha, beta, gamma, out)
             if 0 <= r < n_rows:
                 stage(r)
 
-        for s in range(-3, n_rows + 18):
+        for s in range(-4, n_rows + 18):
             run(score_row, s + 1)
             run(max_first_bank, s)
-            run(qk_copy, s + 2)
             run(diagonal_tile, s - 12)
             run(max_second_bank, s)
             run(a_copy, s - 14)
@@ -363,7 +374,8 @@ def tile_causalshapedattention_pa_t_kernel(tc, q, k, v, alpha, beta, gamma, out)
             run(a_transpose, s - 13)
             run(quantise_rows, s - 15)
             run(multiply_rows, s - 16)
-            run(qk_transpose, s + 3)
+            run(k_transpose, s + 3)
+            run(q_transpose, s + 4)
             run(quantise_v, s - 2)
             if s == CONST_STEP:
                 late_constants()

@@ -219,7 +219,7 @@ def tile_causalshapedattention_pa_t_kernel(tc, q, k, v, alpha, beta, gamma, out)
                 kT_ps = psum_qk.tile([P, NT, P], BF16, name="qk_ps")
                 for t in range(NT):
                     nc.tensor.transpose(kT_ps[:, t, :], raw[b][1][:, t, cols], key_perm[:])
-                nc.vector.tensor_copy(out=job[n]["kT"][:], in_=kT_ps[:])
+                nc.scalar.copy(out=job[n]["kT"][:], in_=kT_ps[:])
 
         def score_row(r):
             n, i, b, cols = place(r)

@@ -23,6 +23,7 @@ BLOCK = P // 2
 BANK = 512
 BANK_TILES = BANK // P
 MASKED = -1e20
+EXP_SHIFT = 10.1
 FLOPS = 2 * 2 * B * H * T * T * D
 
 
@@ -185,6 +186,7 @@ def tile_causalshapedattention_pa_t_kernel(tc, q, k, v, alpha, beta, gamma, out)
                 "neg_max": heads.tile([P, NT], F32, name="neg_max"),
                 "neg_max_half": heads.tile([P, NT], F32, name="neg_max_half"),
                 "row_sum": heads.tile([P, NT], F32, name="row_sum"),
+                "bias": heads.tile([P, NT], F32, name="bias"),
             }
 
         def quantise_v(r):
@@ -244,9 +246,12 @@ def tile_causalshapedattention_pa_t_kernel(tc, q, k, v, alpha, beta, gamma, out)
             if m < len(banks):
                 dest = st["neg_max"] if m == len(banks) - 1 else st["neg_max_half"]
                 nc.vector.tensor_scalar(out=st["e"][i][:, m * BANK_TILES:min((m + 1) * BANK_TILES, i + 1), :],
-                                        in0=banks[m], scalar1=-scale,
+                                        in0=banks[m], scalar1=-1.0,
                                         scalar2=st["neg_max_half"][:, i:i + 1] if m > 0 else None,
                                         op0=ALU.mult, op1=ALU.min, accum_out=dest[:, i:i + 1])
+                if m == len(banks) - 1:
+                    nc.gpsimd.tensor_scalar(out=st["bias"][:, i:i + 1], in0=st["neg_max"][:, i:i + 1],
+                                            scalar1=scale, scalar2=EXP_SHIFT, op0=ALU.mult, op1=ALU.add)
 
         def max_first_bank(r):
             max_bank(r, 0)
@@ -258,7 +263,7 @@ def tile_causalshapedattention_pa_t_kernel(tc, q, k, v, alpha, beta, gamma, out)
             n, i, b, cols = place(r)
             st = job[n]
             nc.scalar.activation(out=st["e"][i][:], in_=st["e"][i][:], func=ACT.Exp,
-                                 bias=st["neg_max"][:, i:i + 1], scale=-1.0,
+                                 bias=st["bias"][:, i:i + 1], scale=-scale,
                                  accum_out=st["row_sum"][:, i:i + 1])
 
         def diagonal_tile(r):

@@ -47,6 +47,7 @@ def tile_causalshapedattention_pa_t_kernel(tc, q, k, v, alpha, beta, gamma, out)
         loads = ctx.enter_context(tc.tile_pool(name="loads", bufs=2))
         heads = ctx.enter_context(tc.tile_pool(name="heads", bufs=2))
         long_lived = ctx.enter_context(tc.tile_pool(name="long_lived", bufs=4))
+        scores = ctx.enter_context(tc.tile_pool(name="scores", bufs=3))
         psum_s = ctx.enter_context(tc.psum_pool(name="psum_s", bufs=4))
         psum_t = ctx.enter_context(tc.psum_pool(name="psum_t", bufs=2))
         psum_o = ctx.enter_context(tc.psum_pool(name="psum_o", bufs=1))
@@ -183,10 +184,10 @@ def tile_causalshapedattention_pa_t_kernel(tc, q, k, v, alpha, beta, gamma, out)
                 "s": {}, "e": {}, "bank": {},
                 "qT": heads.tile([P, NT, P], BF16, name="qT"),
                 "kT": heads.tile([P, NT, P], BF16, name="kT"),
-                "neg_max": heads.tile([P, NT], F32, name="neg_max"),
-                "neg_max_half": heads.tile([P, NT], F32, name="neg_max_half"),
-                "row_sum": heads.tile([P, NT], F32, name="row_sum"),
-                "bias": heads.tile([P, NT], F32, name="bias"),
+                "neg_max": long_lived.tile([P, NT], F32, name="neg_max"),
+                "neg_max_half": long_lived.tile([P, NT], F32, name="neg_max_half"),
+                "row_sum": long_lived.tile([P, NT], F32, name="row_sum"),
+                "bias": long_lived.tile([P, NT], F32, name="bias"),
             }
 
         def quantise_v(r):
@@ -195,8 +196,7 @@ def tile_causalshapedattention_pa_t_kernel(tc, q, k, v, alpha, beta, gamma, out)
                 v_grouped = heads.tile([P, PASSES, D, 4], BF16, name="v_grouped", align_bytes=64)
                 v_codes = long_lived.tile([P, PASSES, D], U32, name="v_codes", align_bytes=64)
                 v_scales = long_lived.tile([P, PASSES, D], U8, name="v_scales", align_bytes=64)
-                nc.gpsimd.tensor_scalar(out=v_grouped[:], in0=raw[b][2][:, :, :, cols].rearrange("p c t w -> p c w t"),
-                                        scalar1=1.0, scalar2=0.0, op0=ALU.mult, op1=ALU.add)
+                nc.vector.tensor_copy(out=v_grouped[:], in_=raw[b][2][:, :, :, cols].rearrange("p c t w -> p c w t"))
                 nc.vector.quantize_mx(
                     out=v_codes[:].rearrange("p c w -> p (c w)").bitcast(FP8X4),
                     scales=v_scales[:].rearrange("p c w -> p (c w)"),
@@ -242,15 +242,15 @@ def tile_causalshapedattention_pa_t_kernel(tc, q, k, v, alpha, beta, gamma, out)
             st = job[n]
             banks = st["s"][i]
             if m == 0:
-                st["e"][i] = heads.tile([P, i + 1, P], F32, name="e%d" % i)
+                st["e"][i] = scores.tile([P, i + 1, P], F32, name="e%d" % i)
             if m < len(banks):
                 dest = st["neg_max"] if m == len(banks) - 1 else st["neg_max_half"]
                 nc.vector.tensor_scalar(out=st["e"][i][:, m * BANK_TILES:min((m + 1) * BANK_TILES, i + 1), :],
                                         in0=banks[m], scalar1=-1.0,
                                         scalar2=st["neg_max_half"][:, i:i + 1] if m > 0 else None,
                                         op0=ALU.mult, op1=ALU.min, accum_out=dest[:, i:i + 1])
-                if m == len(banks) - 1:
-                    nc.gpsimd.tensor_scalar(out=st["bias"][:, i:i + 1], in0=st["neg_max"][:, i:i + 1],
+                if m == len(banks) - 1 and i == NT - 1:
+                    nc.vector.tensor_scalar(out=st["bias"][:], in0=st["neg_max"][:],
                                             scalar1=scale, scalar2=EXP_SHIFT, op0=ALU.mult, op1=ALU.add)
 
         def max_first_bank(r):
@@ -290,7 +290,7 @@ def tile_causalshapedattention_pa_t_kernel(tc, q, k, v, alpha, beta, gamma, out)
             st = job[n]
             used = BLOCK * (i + 1)
             if i > 0:
-                nc.gpsimd.tensor_scalar(out=a_tiles[n % 2][i][:, :, :used - BLOCK].rearrange("q u (j x) -> q u j x", x=BLOCK),
+                nc.vector.tensor_scalar(out=a_tiles[n % 2][i][:, :, :used - BLOCK].rearrange("q u (j x) -> q u j x", x=BLOCK),
                                         in0=st["e"][i][:, :i, :].rearrange("q j (u x) -> q u j x", u=2),
                                         scalar1=st["gain"][:, i:i + 1], scalar2=below[:, i:i + 1],
                                         op0=ALU.mult, op1=ALU.add)
@@ -367,18 +367,18 @@ def tile_causalshapedattention_pa_t_kernel(tc, q, k, v, alpha, beta, gamma, out)
             if 0 <= r < n_rows:
                 stage(r)
 
-        for s in range(-4, n_rows + 18):
+        for s in range(-4, n_rows + 26):
             run(score_row, s + 1)
             run(max_first_bank, s)
-            run(diagonal_tile, s - 12)
+            run(diagonal_tile, s - 20)
             run(max_second_bank, s)
-            run(a_copy, s - 14)
-            run(out_copy, s - 17)
-            run(exp_row, s)
-            run(normalise_row, s - 12)
-            run(a_transpose, s - 13)
-            run(quantise_rows, s - 15)
-            run(multiply_rows, s - 16)
+            run(a_copy, s - 22)
+            run(out_copy, s - 25)
+            run(exp_row, s - 8)
+            run(normalise_row, s - 20)
+            run(a_transpose, s - 21)
+            run(quantise_rows, s - 23)
+            run(multiply_rows, s - 24)
             run(k_transpose, s + 3)
             run(q_transpose, s + 4)
             run(quantise_v, s - 2)

@@ -37,6 +37,7 @@ QUANT_UNITS = 4
 N_FAR = len([i for i in range(NT) if passes_of(i) < PASSES])
 CONST_STEP = 0
 FAR_STEP = 8
+WARM_ROWS = (1, 2, 3)
 
 
 def tile_causalshapedattention_pa_t_kernel(tc, q, k, v, alpha, beta, gamma, out):
@@ -231,7 +232,10 @@ def tile_causalshapedattention_pa_t_kernel(tc, q, k, v, alpha, beta, gamma, out)
                 tiles = min(BANK_TILES, i + 1 - j0)
                 on_diagonal = j0 + tiles == i + 1
                 s_ps = psum_s.tile([P, BANK_TILES, P], F32, name="s_ps")
-                nc.tensor.matmul(s_ps[:, :tiles, :], lhsT=st["qT"][:, i, :], rhs=st["kT"][:, j0:j0 + tiles, :],
+                if i in WARM_ROWS:
+                    nc.tensor.matmul(s_ps[:], lhsT=st["qT"][:, i, :], rhs=st["kT"][:, j0:j0 + BANK_TILES, :],
+                                     start=True, stop=True)
+                nc.tensor.matmul(s_ps[:], lhsT=st["qT"][:, i, :], rhs=st["kT"][:, j0:j0 + BANK_TILES, :],
                                  start=True, stop=not on_diagonal)
                 if on_diagonal:
                     nc.tensor.matmul(s_ps[:, tiles - 1, :], lhsT=ident_bf[:], rhs=mask_add[:], start=False, stop=True)

@@ -197,7 +197,8 @@ def tile_causalshapedattention_pa_t_kernel(tc, q, k, v, alpha, beta, gamma, out)
                 v_grouped = heads.tile([P, PASSES, D, 4], BF16, name="v_grouped", align_bytes=64)
                 v_codes = long_lived.tile([P, PASSES, D], U32, name="v_codes", align_bytes=64)
                 v_scales = long_lived.tile([P, PASSES, D], U8, name="v_scales", align_bytes=64)
-                nc.vector.tensor_copy(out=v_grouped[:], in_=raw[b][2][:, :, :, cols].rearrange("p c t w -> p c w t"))
+                nc.gpsimd.tensor_scalar(out=v_grouped[:], in0=raw[b][2][:, :, :, cols].rearrange("p c t w -> p c w t"),
+                                        scalar1=1.0, scalar2=0.0, op0=ALU.mult, op1=ALU.add)
                 nc.vector.quantize_mx(
                     out=v_codes[:].rearrange("p c w -> p (c w)").bitcast(FP8X4),
                     scales=v_scales[:].rearrange("p c w -> p (c w)"),
@@ -294,7 +295,7 @@ def tile_causalshapedattention_pa_t_kernel(tc, q, k, v, alpha, beta, gamma, out)
             st = job[n]
             used = BLOCK * (i + 1)
             if i > 0:
-                nc.vector.tensor_scalar(out=a_tiles[n % 2][i][:, :, :used - BLOCK].rearrange("q u (j x) -> q u j x", x=BLOCK),
+                nc.gpsimd.tensor_scalar(out=a_tiles[n % 2][i][:, :, :used - BLOCK].rearrange("q u (j x) -> q u j x", x=BLOCK),
                                         in0=st["e"][i][:, :i, :].rearrange("q j (u x) -> q u j x", u=2),
                                         scalar1=st["gain"][:, i:i + 1], scalar2=below[:, i:i + 1],
                                         op0=ALU.mult, op1=ALU.add)
@@ -374,12 +375,12 @@ def tile_causalshapedattention_pa_t_kernel(tc, q, k, v, alpha, beta, gamma, out)
         for s in range(-4, n_rows + 26):
             run(score_row, s + 1)
             run(max_first_bank, s)
-            run(diagonal_tile, s - 20)
+            run(diagonal_tile, s - 19)
             run(max_second_bank, s)
             run(a_copy, s - 22)
             run(out_copy, s - 25)
             run(exp_row, s - 8)
-            run(normalise_row, s - 20)
+            run(normalise_row, s - 19)
             run(a_transpose, s - 21)
             run(quantise_rows, s - 23)
             run(multiply_rows, s - 24)

@@ -49,10 +49,11 @@ def tile_causalshapedattention_pa_t_kernel(tc, q, k, v, alpha, beta, gamma, out)
         heads = ctx.enter_context(tc.tile_pool(name="heads", bufs=2))
         long_lived = ctx.enter_context(tc.tile_pool(name="long_lived", bufs=4))
         scores = ctx.enter_context(tc.tile_pool(name="scores", bufs=3))
-        psum_s = ctx.enter_context(tc.psum_pool(name="psum_s", bufs=4))
+        psum_s = ctx.enter_context(tc.psum_pool(name="psum_s", bufs=3))
         psum_t = ctx.enter_context(tc.psum_pool(name="psum_t", bufs=2))
         psum_o = ctx.enter_context(tc.psum_pool(name="psum_o", bufs=1))
         psum_qk = ctx.enter_context(tc.psum_pool(name="psum_qk", bufs=1))
+        psum_shape = ctx.enter_context(tc.psum_pool(name="psum_shape", bufs=1))
 
         raw = {}
         job = {}
@@ -106,6 +107,8 @@ def tile_causalshapedattention_pa_t_kernel(tc, q, k, v, alpha, beta, gamma, out)
         above = const.tile([P, NT], F32)
         below = const.tile([P, NT], F32)
         shape_add = const.tile([P, NT, P], F32)
+        shape_bf = const.tile([P, NT, P], BF16)
+        shape_ps = psum_shape.tile([P, NT, P], BF16)
         a_tiles = [[const.tile([P, 2, 2 * P * passes_of(i)], BF16, name="a%d_%d" % (s, i)) for i in range(NT)]
                    for s in range(2)]
         far_a = const.tile([P, N_FAR, 2, 2 * P], BF16)
@@ -146,6 +149,10 @@ def tile_causalshapedattention_pa_t_kernel(tc, q, k, v, alpha, beta, gamma, out)
             for i in range(NT):
                 nc.vector.scalar_tensor_tensor(out=shape_add[:, i, :], in0=diag[:], scalar=alpha_f[:, 0:1],
                                                in1=shape_add[:, i, :], op0=ALU.mult, op1=ALU.add)
+            nc.vector.tensor_copy(out=shape_bf[:], in_=shape_add[:])
+            for first in range(0, NT, BANK_TILES):
+                nc.tensor.matmul(shape_ps[:, first:first + BANK_TILES, :], lhsT=ident_bf[:],
+                                 rhs=shape_bf[:, first:first + BANK_TILES, :], start=True, stop=True)
             for row_set in a_tiles:
                 for i in range(NT):
                     used = BLOCK * (i + 1)
@@ -287,7 +294,7 @@ def tile_causalshapedattention_pa_t_kernel(tc, q, k, v, alpha, beta, gamma, out)
             nc.vector.scalar_tensor_tensor(
                 out=a_tiles[n % 2][i][:, :, used - BLOCK:used],
                 in0=st["e"][i][:, i, :].rearrange("q (u x) -> q u x", u=2),
-                scalar=st["gain"][:, i:i + 1], in1=shape_add[:, i, :].rearrange("q (u x) -> q u x", u=2),
+                scalar=st["gain"][:, i:i + 1], in1=shape_ps[:, i, :].rearrange("q (u x) -> q u x", u=2),
                 op0=ALU.mult, op1=ALU.add)
 
         def normalise_row(r):

@@ -34,10 +34,11 @@ def passes_of(i):
 UNITS = [(i, c) for i in range(NT) for c in range(passes_of(i))]
 BANK_UNITS = 2
 QUANT_UNITS = 4
+QUANT_CALLS = ((0, 8), (8, 4))
 N_FAR = len([i for i in range(NT) if passes_of(i) < PASSES])
 CONST_STEP = 0
 FAR_STEP = 8
-WARM_ROWS = (1, 2, 3)
+WARM_ROWS = (0, 2)
 
 
 def tile_causalshapedattention_pa_t_kernel(tc, q, k, v, alpha, beta, gamma, out):
@@ -49,6 +50,7 @@ def tile_causalshapedattention_pa_t_kernel(tc, q, k, v, alpha, beta, gamma, out)
         heads = ctx.enter_context(tc.tile_pool(name="heads", bufs=2))
         long_lived = ctx.enter_context(tc.tile_pool(name="long_lived", bufs=4))
         scores = ctx.enter_context(tc.tile_pool(name="scores", bufs=3))
+        values = ctx.enter_context(tc.tile_pool(name="values", bufs=3))
         psum_s = ctx.enter_context(tc.psum_pool(name="psum_s", bufs=3))
         psum_t = ctx.enter_context(tc.psum_pool(name="psum_t", bufs=2))
         psum_o = ctx.enter_context(tc.psum_pool(name="psum_o", bufs=1))
@@ -61,7 +63,7 @@ def tile_causalshapedattention_pa_t_kernel(tc, q, k, v, alpha, beta, gamma, out)
         def load(b):
             q_sb = loads.tile([P, NT, C], BF16, name="q_sb")
             k_sb = loads.tile([P, NT, C], BF16, name="k_sb")
-            v_sb = loads.tile([P, PASSES, 4, C], BF16, name="v_sb")
+            v_sb = values.tile([P, PASSES, 4, C], BF16, name="v_sb")
             for first in range(0, NT, NT // 2):
                 tiles = slice(first, first + NT // 2)
                 rows = slice(first * P, (first + NT // 2) * P)
@@ -198,20 +200,23 @@ def tile_causalshapedattention_pa_t_kernel(tc, q, k, v, alpha, beta, gamma, out)
                 "bias": long_lived.tile([P, NT], F32, name="bias"),
             }
 
-        def quantise_v(r):
+        def regroup_v(r):
             n, i, b, cols = place(r)
-            if i == 0:
+            if i == NT - 1:
                 v_grouped = heads.tile([P, PASSES, D, 4], BF16, name="v_grouped", align_bytes=64)
-                v_codes = long_lived.tile([P, PASSES, D], U32, name="v_codes", align_bytes=64)
-                v_scales = long_lived.tile([P, PASSES, D], U8, name="v_scales", align_bytes=64)
                 nc.gpsimd.tensor_scalar(out=v_grouped[:], in0=raw[b][2][:, :, :, cols].rearrange("p c t w -> p c w t"),
                                         scalar1=1.0, scalar2=0.0, op0=ALU.mult, op1=ALU.add)
-                nc.vector.quantize_mx(
-                    out=v_codes[:].rearrange("p c w -> p (c w)").bitcast(FP8X4),
-                    scales=v_scales[:].rearrange("p c w -> p (c w)"),
-                    in_=v_grouped[:].rearrange("p c w t -> p (c w t)"),
-                )
-                job[n]["v_codes"], job[n]["v_scales"] = v_codes, v_scales
+                job[n]["v_grouped"] = v_grouped
+
+        def quantise_v(n):
+            v_codes = long_lived.tile([P, PASSES, D], U32, name="v_codes", align_bytes=64)
+            v_scales = long_lived.tile([P, PASSES, D], U8, name="v_scales", align_bytes=64)
+            nc.vector.quantize_mx(
+                out=v_codes[:].rearrange("p c w -> p (c w)").bitcast(FP8X4),
+                scales=v_scales[:].rearrange("p c w -> p (c w)"),
+                in_=job[n]["v_grouped"][:].rearrange("p c w t -> p (c w t)"),
+            )
+            job[n]["v_codes"], job[n]["v_scales"] = v_codes, v_scales
 
         def q_transpose(r):
             n, i, b, cols = place(r)
@@ -261,9 +266,6 @@ def tile_causalshapedattention_pa_t_kernel(tc, q, k, v, alpha, beta, gamma, out)
                                         in0=banks[m], scalar1=-1.0,
                                         scalar2=st["neg_max_half"][:, i:i + 1] if m > 0 else None,
                                         op0=ALU.mult, op1=ALU.min, accum_out=dest[:, i:i + 1])
-                if m == len(banks) - 1 and i == NT - 1:
-                    nc.vector.tensor_scalar(out=st["bias"][:], in0=st["neg_max"][:],
-                                            scalar1=scale, scalar2=EXP_SHIFT, op0=ALU.mult, op1=ALU.add)
 
         def max_first_bank(r):
             max_bank(r, 0)
@@ -282,11 +284,6 @@ def tile_causalshapedattention_pa_t_kernel(tc, q, k, v, alpha, beta, gamma, out)
             n, i, b, cols = place(r)
             st = job[n]
             if i == 0:
-                gain = heads.tile([P, NT], F32, name="gain")
-                nc.vector.reciprocal(out=gain[:], in_=st["row_sum"][:])
-                nc.vector.tensor_scalar(out=gain[:], in0=gain[:], scalar1=beta_f[:, 0:1], scalar2=None,
-                                        op0=ALU.mult)
-                st["gain"] = gain
                 st["grouped"] = heads.tile([P, len(UNITS), P, 4], BF16, name="grouped", align_bytes=64)
                 st["codes"] = heads.tile([P, len(UNITS), P], U32, name="codes", align_bytes=64)
                 st["scales"] = heads.tile([P, len(UNITS), P], U8, name="scales", align_bytes=64)
@@ -334,17 +331,32 @@ def tile_causalshapedattention_pa_t_kernel(tc, q, k, v, alpha, beta, gamma, out)
                 nc.scalar.copy(out=job[n]["grouped"][:, first:first + BANK_UNITS].bitcast(F32),
                                in_=job[n]["bank"][i][:].rearrange("p c u i -> p c i u"))
 
-        def quantise_rows(r):
-            n, i, b, cols = place(r)
+        def quantise_a(n):
             st = job[n]
-            rows = rows_filling(i, QUANT_UNITS)
-            if rows:
-                g = UNITS.index((rows[0], 0))
+            for g, units in QUANT_CALLS:
                 nc.vector.quantize_mx(
-                    out=st["codes"][:, g:g + QUANT_UNITS].rearrange("p n i -> p (n i)").bitcast(FP8X4),
-                    scales=st["scales"][:, g:g + QUANT_UNITS].rearrange("p n i -> p (n i)"),
-                    in_=st["grouped"][:, g:g + QUANT_UNITS].rearrange("p n i t -> p (n i t)"),
+                    out=st["codes"][:, g:g + units].rearrange("p n i -> p (n i)").bitcast(FP8X4),
+                    scales=st["scales"][:, g:g + units].rearrange("p n i -> p (n i)"),
+                    in_=st["grouped"][:, g:g + units].rearrange("p n i t -> p (n i t)"),
                 )
+
+        def port_phase(p):
+            def live(n):
+                return 0 <= n < B * H
+            if live(p - 3):
+                quantise_a(p - 3)
+            if live(p - 1):
+                quantise_v(p - 1)
+            if live(p - 1):
+                gain = heads.tile([P, NT], F32, name="gain")
+                nc.vector.reciprocal(out=gain[:], in_=job[p - 1]["row_sum"][:])
+            if live(p):
+                nc.vector.tensor_scalar(out=job[p]["bias"][:], in0=job[p]["neg_max"][:],
+                                        scalar1=scale, scalar2=EXP_SHIFT, op0=ALU.mult, op1=ALU.add)
+            if live(p - 1):
+                nc.vector.tensor_scalar(out=gain[:], in0=gain[:], scalar1=beta_f[:, 0:1], scalar2=None,
+                                        op0=ALU.mult)
+                job[p - 1]["gain"] = gain
 
         def multiply_rows(r):
             n, i, b, cols = place(r)
@@ -379,22 +391,24 @@ def tile_causalshapedattention_pa_t_kernel(tc, q, k, v, alpha, beta, gamma, out)
             if 0 <= r < n_rows:
                 stage(r)
 
-        for s in range(-4, n_rows + 26):
+        ctx.enter_context(tc.manual_schedule(engines={mybir.EngineType.DVE, mybir.EngineType.Pool}))
+        for s in range(-4, n_rows + 31):
             run(score_row, s + 1)
             run(max_first_bank, s)
-            run(diagonal_tile, s - 19)
+            run(diagonal_tile, s - 17)
             run(max_second_bank, s)
-            run(a_copy, s - 22)
-            run(out_copy, s - 25)
+            run(a_copy, s - 19)
+            run(out_copy, s - 30)
             run(exp_row, s - 8)
-            run(normalise_row, s - 19)
-            run(a_transpose, s - 21)
-            run(quantise_rows, s - 23)
-            run(multiply_rows, s - 24)
+            run(normalise_row, s - 16)
+            run(regroup_v, s - 8)
+            run(a_transpose, s - 18)
+            run(multiply_rows, s - 29)
             run(k_transpose, s + 3)
             run(q_transpose, s + 4)
-            run(quantise_v, s - 2)
             if s == CONST_STEP:
                 late_constants()
             if s == FAR_STEP:
                 far_units()
+            if s % NT == NT - 1:
+                port_phase(s // NT)

@@ -38,6 +38,7 @@ QUANT_CALLS = ((0, 8), (8, 4))
 N_FAR = len([i for i in range(NT) if passes_of(i) < PASSES])
 CONST_STEP = 0
 FAR_STEP = 8
+VECTOR_ROW = 5
 WARM_ROWS = (0, 2)
 
 
@@ -296,13 +297,16 @@ def tile_causalshapedattention_pa_t_kernel(tc, q, k, v, alpha, beta, gamma, out)
 
         def normalise_row(r):
             n, i, b, cols = place(r)
+            if i > 0 and i != VECTOR_ROW:
+                normalise(nc.gpsimd, n, i)
+
+        def normalise(engine, n, i):
             st = job[n]
             used = BLOCK * (i + 1)
-            if i > 0:
-                nc.gpsimd.tensor_scalar(out=a_tiles[n % 2][i][:, :, :used - BLOCK].rearrange("q u (j x) -> q u j x", x=BLOCK),
-                                        in0=st["e"][i][:, :i, :].rearrange("q j (u x) -> q u j x", u=2),
-                                        scalar1=st["gain"][:, i:i + 1], scalar2=below[:, i:i + 1],
-                                        op0=ALU.mult, op1=ALU.add)
+            engine.tensor_scalar(out=a_tiles[n % 2][i][:, :, :used - BLOCK].rearrange("q u (j x) -> q u j x", x=BLOCK),
+                                 in0=st["e"][i][:, :i, :].rearrange("q j (u x) -> q u j x", u=2),
+                                 scalar1=st["gain"][:, i:i + 1], scalar2=below[:, i:i + 1],
+                                 op0=ALU.mult, op1=ALU.add)
 
         def rows_filling(i, n_units):
             end = UNITS.index((i, 0)) + passes_of(i)
@@ -346,17 +350,19 @@ def tile_causalshapedattention_pa_t_kernel(tc, q, k, v, alpha, beta, gamma, out)
             if live(p - 3):
                 quantise_a(p - 3)
             if live(p - 1):
-                quantise_v(p - 1)
-            if live(p - 1):
                 gain = heads.tile([P, NT], F32, name="gain")
                 nc.vector.reciprocal(out=gain[:], in_=job[p - 1]["row_sum"][:])
-            if live(p):
-                nc.vector.tensor_scalar(out=job[p]["bias"][:], in0=job[p]["neg_max"][:],
-                                        scalar1=scale, scalar2=EXP_SHIFT, op0=ALU.mult, op1=ALU.add)
+            if live(p - 2):
+                normalise(nc.vector, p - 2, VECTOR_ROW)
             if live(p - 1):
                 nc.vector.tensor_scalar(out=gain[:], in0=gain[:], scalar1=beta_f[:, 0:1], scalar2=None,
                                         op0=ALU.mult)
                 job[p - 1]["gain"] = gain
+            if live(p - 1):
+                quantise_v(p - 1)
+            if live(p):
+                nc.vector.tensor_scalar(out=job[p]["bias"][:], in0=job[p]["neg_max"][:],
+                                        scalar1=scale, scalar2=EXP_SHIFT, op0=ALU.mult, op1=ALU.add)
 
         def multiply_rows(r):
             n, i, b, cols = place(r)
@@ -397,12 +403,12 @@ def tile_causalshapedattention_pa_t_kernel(tc, q, k, v, alpha, beta, gamma, out)
             run(max_first_bank, s)
             run(diagonal_tile, s - 17)
             run(max_second_bank, s)
-            run(a_copy, s - 19)
+            run(a_copy, s - 21)
             run(out_copy, s - 30)
             run(exp_row, s - 8)
             run(normalise_row, s - 16)
             run(regroup_v, s - 8)
-            run(a_transpose, s - 18)
+            run(a_transpose, s - 20)
             run(multiply_rows, s - 29)
             run(k_transpose, s + 3)
             run(q_transpose, s + 4)

@@ -36,8 +36,9 @@ BANK_UNITS = 2
 QUANT_UNITS = 4
 QUANT_CALLS = ((0, 8), (8, 4))
 N_FAR = len([i for i in range(NT) if passes_of(i) < PASSES])
-CONST_STEP = 0
-FAR_STEP = 8
+CONST_STEP = 1
+SECOND_SET_STEP = 10
+FAR_STEP = 14
 VECTOR_ROW = 5
 WARM_ROWS = (0, 2)
 
@@ -119,53 +120,61 @@ def tile_causalshapedattention_pa_t_kernel(tc, q, k, v, alpha, beta, gamma, out)
         far_codes = const.tile([P, N_FAR, P], U32, align_bytes=64)
         far_scales = const.tile([P, N_FAR, P], U8, align_bytes=64)
 
-        def late_constants():
+        spread = const.tile([P, NT], F32)
+        is_last = const.tile([P, NT], F32)
+
+        def early_constants():
             make_identity(nc, ident_f32[:])
-            to_key_order(diag, ident_f32)
+            nc.gpsimd.tensor_copy(out=diag[:].rearrange("k (u p e) -> k u p e", u=2, e=2),
+                                  in_=ident_f32[:].rearrange("k (p u e) -> k u p e", u=2, e=2))
             nc.gpsimd.memset(ones[:], 1.0)
+            row_f = const.tile([P, NT], F32)
+            nc.gpsimd.iota(row_f[:], pattern=[[P, NT]], base=0, channel_multiplier=1,
+                           allow_small_or_imprecise_dtypes=True)
+            nc.gpsimd.tensor_scalar(out=is_last[:], in0=row_f[:], scalar1=float(T - 1), scalar2=None,
+                                    op0=ALU.is_equal)
+            all_keys = const.tile([P, NT], F32)
+            nc.gpsimd.tensor_scalar(out=all_keys[:], in0=is_last[:], scalar1=float(T), scalar2=0.0,
+                                    op0=ALU.mult, op1=ALU.add)
+            nc.gpsimd.tensor_scalar(out=spread[:], in0=row_f[:], scalar1=-1.0, scalar2=float(T - 1),
+                                    op0=ALU.mult, op1=ALU.add)
+            nc.gpsimd.tensor_tensor(out=spread[:], in0=spread[:], in1=all_keys[:], op=ALU.add)
+
+        def fill_right_of_diagonal(row_set):
+            for i in range(NT):
+                used = BLOCK * (i + 1)
+                width = 2 * P * passes_of(i)
+                if used < width:
+                    nc.scalar.activation(out=row_set[i][:, :, used:], in_=ones[:, :, :width - used], func=ACT.Copy,
+                                         scale=above[:, i:i + 1])
+
+        def late_constants():
+            nc.vector.reciprocal(out=spread[:], in_=spread[:])
             alpha_f = const.tile([P, 1], F32)
             gamma_f = const.tile([P, 1], F32)
-            nc.vector.tensor_copy(out=gamma_f[:], in_=gamma_bf[:])
-            nc.vector.tensor_copy(out=alpha_f[:], in_=alpha_bf[:])
-            nc.vector.tensor_copy(out=beta_f[:], in_=beta_bf[:])
-            row_i32 = const.tile([P, NT], I32)
-            nc.gpsimd.iota(row_i32[:], pattern=[[P, NT]], base=0, channel_multiplier=1)
-            row_f = const.tile([P, NT], F32)
-            nc.vector.tensor_copy(out=row_f[:], in_=row_i32[:])
-            is_last = const.tile([P, NT], F32)
-            nc.vector.tensor_scalar(out=is_last[:], in0=row_f[:], scalar1=float(T - 1), scalar2=None,
-                                    op0=ALU.is_equal)
-            spread = const.tile([P, NT], F32)
-            nc.vector.tensor_scalar(out=spread[:], in0=row_f[:], scalar1=-1.0, scalar2=float(T - 1),
-                                    op0=ALU.mult, op1=ALU.add)
-            nc.vector.scalar_tensor_tensor(out=spread[:], in0=is_last[:], scalar=float(T), in1=spread[:],
-                                           op0=ALU.mult, op1=ALU.add)
-            nc.vector.reciprocal(out=spread[:], in_=spread[:])
-            nc.vector.tensor_scalar(out=above[:], in0=spread[:], scalar1=gamma_f[:, 0:1], scalar2=-1.0,
+            nc.gpsimd.tensor_copy(out=gamma_f[:], in_=gamma_bf[:])
+            nc.gpsimd.tensor_copy(out=alpha_f[:], in_=alpha_bf[:])
+            nc.gpsimd.tensor_copy(out=beta_f[:], in_=beta_bf[:])
+            nc.gpsimd.tensor_scalar(out=above[:], in0=spread[:], scalar1=gamma_f[:, 0:1], scalar2=-1.0,
                                     op0=ALU.mult, op1=ALU.mult)
-            nc.vector.tensor_tensor(out=below[:], in0=above[:], in1=is_last[:], op=ALU.mult)
+            nc.gpsimd.tensor_tensor(out=below[:], in0=above[:], in1=is_last[:], op=ALU.mult)
             step_down = const.tile([P, NT], F32)
-            nc.vector.tensor_tensor(out=step_down[:], in0=below[:], in1=above[:], op=ALU.subtract)
-            for i in range(NT):
-                nc.scalar.activation(out=shape_add[:, i, :], in_=lower[:], func=ACT.Identity,
-                                     bias=above[:, i:i + 1], scale=step_down[:, i:i + 1])
-            for i in range(NT):
-                nc.vector.scalar_tensor_tensor(out=shape_add[:, i, :], in0=diag[:], scalar=alpha_f[:, 0:1],
-                                               in1=shape_add[:, i, :], op0=ALU.mult, op1=ALU.add)
-            nc.vector.tensor_copy(out=shape_bf[:], in_=shape_add[:])
-            for first in range(0, NT, BANK_TILES):
-                nc.tensor.matmul(shape_ps[:, first:first + BANK_TILES, :], lhsT=ident_bf[:],
-                                 rhs=shape_bf[:, first:first + BANK_TILES, :], start=True, stop=True)
-            for row_set in a_tiles:
-                for i in range(NT):
-                    used = BLOCK * (i + 1)
-                    width = 2 * P * passes_of(i)
-                    if used < width:
-                        nc.gpsimd.tensor_scalar(out=row_set[i][:, :, used:], in0=ones[:, :, :width - used],
-                                                scalar1=above[:, i:i + 1], scalar2=0.0, op0=ALU.mult, op1=ALU.add)
+            nc.gpsimd.tensor_tensor(out=step_down[:], in0=below[:], in1=above[:], op=ALU.subtract)
             for i in range(N_FAR):
                 nc.gpsimd.tensor_scalar(out=far_a[:, i], in0=ones[:], scalar1=above[:, i:i + 1],
                                         scalar2=0.0, op0=ALU.mult, op1=ALU.add)
+            for i in range(NT):
+                nc.scalar.activation(out=shape_add[:, i, :], in_=lower[:], func=ACT.Identity,
+                                     bias=above[:, i:i + 1], scale=step_down[:, i:i + 1])
+            fill_right_of_diagonal(a_tiles[0])
+            alpha_diag = const.tile([P, P], F32)
+            nc.gpsimd.tensor_scalar(out=alpha_diag[:], in0=diag[:], scalar1=alpha_f[:, 0:1], scalar2=0.0,
+                                    op0=ALU.mult, op1=ALU.add)
+            for i in range(NT):
+                nc.gpsimd.tensor_tensor(out=shape_bf[:, i, :], in0=shape_add[:, i, :], in1=alpha_diag[:], op=ALU.add)
+            for first in range(0, NT, BANK_TILES):
+                nc.tensor.matmul(shape_ps[:, first:first + BANK_TILES, :], lhsT=ident_bf[:],
+                                 rhs=shape_bf[:, first:first + BANK_TILES, :], start=True, stop=True)
 
         def far_units():
             for g in range(0, N_FAR, 2):
@@ -397,6 +406,7 @@ def tile_causalshapedattention_pa_t_kernel(tc, q, k, v, alpha, beta, gamma, out)
             if 0 <= r < n_rows:
                 stage(r)
 
+        early_constants()
         ctx.enter_context(tc.manual_schedule(engines={mybir.EngineType.DVE, mybir.EngineType.Pool}))
         for s in range(-4, n_rows + 31):
             run(score_row, s + 1)
@@ -414,6 +424,8 @@ def tile_causalshapedattention_pa_t_kernel(tc, q, k, v, alpha, beta, gamma, out)
             run(q_transpose, s + 4)
             if s == CONST_STEP:
                 late_constants()
+            if s == SECOND_SET_STEP:
+                fill_right_of_diagonal(a_tiles[1])
             if s == FAR_STEP:
                 far_units()
             if s % NT == NT - 1:

@@ -39,6 +39,7 @@ N_FAR = len([i for i in range(NT) if passes_of(i) < PASSES])
 CONST_STEP = 1
 SECOND_SET_STEP = 10
 FAR_STEP = 14
+LAST_JOBS = 2
 VECTOR_ROW = 5
 WARM_ROWS = (0, 2)
 
@@ -306,8 +307,11 @@ def tile_causalshapedattention_pa_t_kernel(tc, q, k, v, alpha, beta, gamma, out)
 
         def normalise_row(r):
             n, i, b, cols = place(r)
-            if i > 0 and i != VECTOR_ROW:
+            if i > 0 and i != VECTOR_ROW and not all_on_vector(n):
                 normalise(nc.gpsimd, n, i)
+
+        def all_on_vector(n):
+            return n >= B * H - LAST_JOBS
 
         def normalise(engine, n, i):
             st = job[n]
@@ -358,20 +362,22 @@ def tile_causalshapedattention_pa_t_kernel(tc, q, k, v, alpha, beta, gamma, out)
                 return 0 <= n < B * H
             if live(p - 3):
                 quantise_a(p - 3)
+            if live(p):
+                nc.vector.tensor_scalar(out=job[p]["bias"][:], in0=job[p]["neg_max"][:],
+                                        scalar1=scale, scalar2=EXP_SHIFT, op0=ALU.mult, op1=ALU.add)
             if live(p - 1):
                 gain = heads.tile([P, NT], F32, name="gain")
                 nc.vector.reciprocal(out=gain[:], in_=job[p - 1]["row_sum"][:])
-            if live(p - 2):
+            if live(p - 2) and not all_on_vector(p - 2):
                 normalise(nc.vector, p - 2, VECTOR_ROW)
             if live(p - 1):
                 nc.vector.tensor_scalar(out=gain[:], in0=gain[:], scalar1=beta_f[:, 0:1], scalar2=None,
                                         op0=ALU.mult)
                 job[p - 1]["gain"] = gain
-            if live(p - 1):
+                if all_on_vector(p - 1):
+                    for i in range(1, NT):
+                        normalise(nc.vector, p - 1, i)
                 quantise_v(p - 1)
-            if live(p):
-                nc.vector.tensor_scalar(out=job[p]["bias"][:], in0=job[p]["neg_max"][:],
-                                        scalar1=scale, scalar2=EXP_SHIFT, op0=ALU.mult, op1=ALU.add)
 
         def multiply_rows(r):
             n, i, b, cols = place(r)
@@ -399,8 +405,8 @@ def tile_causalshapedattention_pa_t_kernel(tc, q, k, v, alpha, beta, gamma, out)
                 st["out_sb"] = heads.tile([P, NT, D], F32, name="out_sb")
             if i % 4 == 3:
                 nc.scalar.copy(out=st["out_sb"][:, i - 3:i + 1, :], in_=st["o_ps"][:])
-            if i == NT - 1:
-                nc.sync.dma_start(out=out[b, :, cols].rearrange("(n p) c -> p n c", p=P), in_=st["out_sb"][:])
+                nc.sync.dma_start(out=out[b, (i - 3) * P:(i + 1) * P, cols].rearrange("(n p) c -> p n c", p=P),
+                                  in_=st["out_sb"][:, i - 3:i + 1, :])
 
         def run(stage, r):
             if 0 <= r < n_rows:
@@ -411,7 +417,7 @@ def tile_causalshapedattention_pa_t_kernel(tc, q, k, v, alpha, beta, gamma, out)
         for s in range(-4, n_rows + 31):
             run(score_row, s + 1)
             run(max_first_bank, s)
-            run(diagonal_tile, s - 17)
+            run(diagonal_tile, s - 16)
             run(max_second_bank, s)
             run(a_copy, s - 21)
             run(out_copy, s - 30)

@@ -238,7 +238,7 @@ def tile_causalshapedattention_pa_t_kernel(tc, q, k, v, alpha, beta, gamma, out)
                 qT_ps = psum_qk.tile([P, NT, P], BF16, name="qk_ps")
                 for t in range(NT):
                     nc.tensor.transpose(qT_ps[:, t, :], raw[b][0][:, t, cols], ident_bf[:])
-                nc.scalar.copy(out=job[n]["qT"][:], in_=qT_ps[:])
+                nc.scalar.copy(out=job[n]["qT"][:].bitcast(F32), in_=qT_ps[:].bitcast(F32))
 
         def k_transpose(r):
             n, i, b, cols = place(r)
@@ -246,7 +246,7 @@ def tile_causalshapedattention_pa_t_kernel(tc, q, k, v, alpha, beta, gamma, out)
                 kT_ps = psum_qk.tile([P, NT, P], BF16, name="qk_ps")
                 for t in range(NT):
                     nc.tensor.transpose(kT_ps[:, t, :], raw[b][1][:, t, cols], key_perm[:])
-                nc.scalar.copy(out=job[n]["kT"][:], in_=kT_ps[:])
+                nc.scalar.copy(out=job[n]["kT"][:].bitcast(F32), in_=kT_ps[:].bitcast(F32))
 
         def score_row(r):
             n, i, b, cols = place(r)

@@ -19,29 +19,30 @@ P = 128
 NT = T // P
 K_PASS = 4 * P
 PASSES = T // K_PASS
+HALF = NT // PASSES
+QUAD = 32
 BLOCK = P // 2
 BANK = 512
-BANK_TILES = BANK // P
 MASKED = -1e20
 EXP_SHIFT = 10.1
 FLOPS = 2 * 2 * B * H * T * T * D
 
-
-def passes_of(i):
-    return (P * (i + 1) + K_PASS - 1) // K_PASS
-
-
-UNITS = [(i, c) for i in range(NT) for c in range(passes_of(i))]
-BANK_UNITS = 2
-QUANT_UNITS = 4
-QUANT_CALLS = ((0, 8), (8, 4))
-N_FAR = len([i for i in range(NT) if passes_of(i) < PASSES])
+UNIT_LOW = (5, 3, 1, 0, 2, 4, 6, 8)
+UNIT_HIGH = (None, None, None, None, 1, 3, 5, 7)
+N_UNITS = 9
+UNIT_BANKS = {3: (0,), 4: (1, 2), 5: (3, 4), 6: (5, 6), 7: (7, 8)}
+QUANT_CALLS = ((0, 8), (8, 1))
 CONST_STEP = 1
-SECOND_SET_STEP = 10
 FAR_STEP = 14
 LAST_JOBS = 2
-VECTOR_ROW = 5
+VECTOR_ROWS = (5,)
 WARM_ROWS = (0, 2)
+L_DIAG, L_ACOPY, L_OUT, L_EXP, L_NORM, L_V, L_AT, L_MUL = 16, 21, 33, 8, 16, 8, 20, 32
+HALF_BIAS = (0,)
+
+
+def tile_at(pos):
+    return pos if pos < HALF else NT + HALF - 1 - pos
 
 
 def tile_causalshapedattention_pa_t_kernel(tc, q, k, v, alpha, beta, gamma, out):
@@ -62,6 +63,7 @@ def tile_causalshapedattention_pa_t_kernel(tc, q, k, v, alpha, beta, gamma, out)
 
         raw = {}
         job = {}
+        seq = {}
 
         def load(b):
             q_sb = loads.tile([P, NT, C], BF16, name="q_sb")
@@ -72,7 +74,10 @@ def tile_causalshapedattention_pa_t_kernel(tc, q, k, v, alpha, beta, gamma, out)
                 rows = slice(first * P, (first + NT // 2) * P)
                 nc.sync.dma_start(out=q_sb[:, tiles, :], in_=q[b, rows, :].rearrange("(n p) c -> p n c", p=P))
                 nc.sync.dma_start(out=k_sb[:, tiles, :], in_=k[b, rows, :].rearrange("(n p) c -> p n c", p=P))
-            nc.sync.dma_start(out=v_sb[:], in_=v[b, :, :].rearrange("(c p t) w -> p c t w", p=P, t=4))
+            nc.sync.dma_start(out=v_sb[:, 0], in_=v[b, :K_PASS, :].rearrange("(p t) w -> p t w", t=4))
+            for j in range(HALF, NT):
+                quad = slice(QUAD * (NT - 1 - j), QUAD * (NT - j))
+                nc.sync.dma_start(out=v_sb[quad, 1], in_=v[b, j * P:(j + 1) * P, :].rearrange("(p t) w -> p t w", t=4))
             raw[b] = (q_sb, k_sb, v_sb)
 
         alpha_bf = const.tile([P, 1], BF16)
@@ -107,28 +112,36 @@ def tile_causalshapedattention_pa_t_kernel(tc, q, k, v, alpha, beta, gamma, out)
 
         ident_f32 = const.tile([P, P], F32)
         diag = const.tile([P, P], F32)
-        ones = const.tile([P, 2, 2 * P], F32)
         beta_f = const.tile([P, 1], F32)
         above = const.tile([P, NT], F32)
+        above_pair = const.tile([P, NT, 2], BF16)
         below = const.tile([P, NT], F32)
         shape_add = const.tile([P, NT, P], F32)
         shape_bf = const.tile([P, NT, P], BF16)
         shape_ps = psum_shape.tile([P, NT, P], BF16)
-        a_tiles = [[const.tile([P, 2, 2 * P * passes_of(i)], BF16, name="a%d_%d" % (s, i)) for i in range(NT)]
-                   for s in range(2)]
-        far_a = const.tile([P, N_FAR, 2, 2 * P], BF16)
-        far_grouped = const.tile([P, N_FAR, P, 4], BF16, align_bytes=64)
-        far_codes = const.tile([P, N_FAR, P], U32, align_bytes=64)
-        far_scales = const.tile([P, N_FAR, P], U8, align_bytes=64)
+        a_sets = [const.tile([P, 2, N_UNITS, 4 * BLOCK], BF16, name="a%d" % s) for s in range(2)]
+        n_far = NT + HALF - 2
+        far_grouped = const.tile([P, n_far, P, 4], BF16, align_bytes=64)
+        far_codes = const.tile([P, n_far, P], U32, align_bytes=64)
+        far_scales = const.tile([P, n_far, P], U8, align_bytes=64)
+        MASKS = [(c, m) for c in range(PASSES) for m in range(1, HALF)]
+        v_masked = [{key: const.tile([P, H, D], I32, name="vm%d_%d_%d" % ((s,) + key), align_bytes=64) for key in MASKS}
+                    for s in range(3)]
 
         spread = const.tile([P, NT], F32)
         is_last = const.tile([P, NT], F32)
 
+        def kept(c, m):
+            return slice(0, QUAD * m) if c == 0 else slice(P - QUAD * m, P)
+
         def early_constants():
+            nc.vector.memset(far_grouped[:].rearrange("p n i t -> p (n i t)").bitcast(I32), 0)
+            for vm in v_masked:
+                for key in MASKS:
+                    nc.vector.memset(vm[key][:], 0)
             make_identity(nc, ident_f32[:])
             nc.gpsimd.tensor_copy(out=diag[:].rearrange("k (u p e) -> k u p e", u=2, e=2),
                                   in_=ident_f32[:].rearrange("k (p u e) -> k u p e", u=2, e=2))
-            nc.gpsimd.memset(ones[:], 1.0)
             row_f = const.tile([P, NT], F32)
             nc.gpsimd.iota(row_f[:], pattern=[[P, NT]], base=0, channel_multiplier=1,
                            allow_small_or_imprecise_dtypes=True)
@@ -141,14 +154,6 @@ def tile_causalshapedattention_pa_t_kernel(tc, q, k, v, alpha, beta, gamma, out)
                                     op0=ALU.mult, op1=ALU.add)
             nc.gpsimd.tensor_tensor(out=spread[:], in0=spread[:], in1=all_keys[:], op=ALU.add)
 
-        def fill_right_of_diagonal(row_set):
-            for i in range(NT):
-                used = BLOCK * (i + 1)
-                width = 2 * P * passes_of(i)
-                if used < width:
-                    nc.scalar.activation(out=row_set[i][:, :, used:], in_=ones[:, :, :width - used], func=ACT.Copy,
-                                         scale=above[:, i:i + 1])
-
         def late_constants():
             nc.vector.reciprocal(out=spread[:], in_=spread[:])
             alpha_f = const.tile([P, 1], F32)
@@ -158,37 +163,57 @@ def tile_causalshapedattention_pa_t_kernel(tc, q, k, v, alpha, beta, gamma, out)
             nc.gpsimd.tensor_copy(out=beta_f[:], in_=beta_bf[:])
             nc.gpsimd.tensor_scalar(out=above[:], in0=spread[:], scalar1=gamma_f[:, 0:1], scalar2=-1.0,
                                     op0=ALU.mult, op1=ALU.mult)
+            for e in range(2):
+                nc.gpsimd.tensor_scalar(out=above_pair[:, :, e], in0=above[:], scalar1=1.0, scalar2=0.0,
+                                        op0=ALU.mult, op1=ALU.add)
             nc.gpsimd.tensor_tensor(out=below[:], in0=above[:], in1=is_last[:], op=ALU.mult)
             step_down = const.tile([P, NT], F32)
             nc.gpsimd.tensor_tensor(out=step_down[:], in0=below[:], in1=above[:], op=ALU.subtract)
-            for i in range(N_FAR):
-                nc.gpsimd.tensor_scalar(out=far_a[:, i], in0=ones[:], scalar1=above[:, i:i + 1],
-                                        scalar2=0.0, op0=ALU.mult, op1=ALU.add)
             for i in range(NT):
                 nc.scalar.activation(out=shape_add[:, i, :], in_=lower[:], func=ACT.Identity,
                                      bias=above[:, i:i + 1], scale=step_down[:, i:i + 1])
-            fill_right_of_diagonal(a_tiles[0])
             alpha_diag = const.tile([P, P], F32)
             nc.gpsimd.tensor_scalar(out=alpha_diag[:], in0=diag[:], scalar1=alpha_f[:, 0:1], scalar2=0.0,
                                     op0=ALU.mult, op1=ALU.add)
             for i in range(NT):
                 nc.gpsimd.tensor_tensor(out=shape_bf[:, i, :], in0=shape_add[:, i, :], in1=alpha_diag[:], op=ALU.add)
-            for first in range(0, NT, BANK_TILES):
-                nc.tensor.matmul(shape_ps[:, first:first + BANK_TILES, :], lhsT=ident_bf[:],
-                                 rhs=shape_bf[:, first:first + BANK_TILES, :], start=True, stop=True)
+            for first in range(0, NT, HALF):
+                nc.tensor.matmul(shape_ps[:, first:first + HALF, :], lhsT=ident_bf[:],
+                                 rhs=shape_bf[:, first:first + HALF, :], start=True, stop=True)
+
+        def far_index(c, i):
+            return i if c == 0 else HALF - 1 + i
 
         def far_units():
-            for g in range(0, N_FAR, 2):
-                bank = psum_t.tile([P, 2, 2, P], F32, name="bank")
-                for m in range(2):
-                    for u in range(2):
-                        nc.tensor.transpose(bank[:, m, u, :], far_a[:, g + m].bitcast(F32)[:, u, :], ident_f32[:])
-                nc.scalar.copy(out=far_grouped[:, g:g + 2].bitcast(F32), in_=bank[:].rearrange("p c u i -> p c i u"))
-            nc.vector.quantize_mx(
-                out=far_codes[:].rearrange("p n i -> p (n i)").bitcast(FP8X4),
-                scales=far_scales[:].rearrange("p n i -> p (n i)"),
-                in_=far_grouped[:].rearrange("p n i t -> p (n i t)"),
-            )
+            words = above_pair[:].rearrange("p n e -> p (n e)").bitcast(F32)
+            grouped = far_grouped[:].rearrange("p n i t -> p n (i t)").bitcast(F32).rearrange("p n (i u) -> p n i u", u=2)
+            for first in range(0, NT, HALF):
+                rows = range(first, min(first + HALF, NT - 1))
+                bank = psum_t.tile([P, HALF, P], F32, name="bank")
+                for i in rows:
+                    nc.tensor.transpose(bank[:, i - first, :], words[:, i:i + 1].to_broadcast([P, P]), ident_f32[:])
+                for i in rows:
+                    for c in range(PASSES):
+                        if c == 0:
+                            quads = range(i + 1, HALF)
+                        else:
+                            quads = range(0, min(HALF, NT - 1 - i))
+                        for a, z in spans(quads):
+                            parts = slice(QUAD * a, QUAD * z)
+                            nc.scalar.copy(out=grouped[parts, far_index(c, i)],
+                                           in_=bank[parts, i - first, :].unsqueeze(2).to_broadcast([QUAD * (z - a), P, 2]))
+            for first, n in ((0, 8), (8, 2)):
+                nc.vector.quantize_mx(
+                    out=far_codes[:, first:first + n].rearrange("p n i -> p (n i)").bitcast(FP8X4),
+                    scales=far_scales[:, first:first + n].rearrange("p n i -> p (n i)"),
+                    in_=far_grouped[:, first:first + n].rearrange("p n i t -> p (n i t)"),
+                )
+
+        def spans(quads):
+            if len(quads) == 0:
+                return []
+            a, z = quads[0], quads[-1] + 1
+            return [(1, 2), (2, z)] if a == 1 and z > 2 else [(a, z)]
 
         n_rows = B * H * NT
 
@@ -220,14 +245,27 @@ def tile_causalshapedattention_pa_t_kernel(tc, q, k, v, alpha, beta, gamma, out)
                 job[n]["v_grouped"] = v_grouped
 
         def quantise_v(n):
-            v_codes = long_lived.tile([P, PASSES, D], U32, name="v_codes", align_bytes=64)
-            v_scales = long_lived.tile([P, PASSES, D], U8, name="v_scales", align_bytes=64)
+            b, h = divmod(n, H)
+            if h == 0:
+                seq[b] = (long_lived.tile([P, H, PASSES, D], I32, name="v_codes", align_bytes=64),
+                          long_lived.tile([P, H, PASSES, D], U8, name="v_scales", align_bytes=64))
+            v_codes, v_scales = seq[b]
             nc.vector.quantize_mx(
-                out=v_codes[:].rearrange("p c w -> p (c w)").bitcast(FP8X4),
-                scales=v_scales[:].rearrange("p c w -> p (c w)"),
+                out=v_codes[:, h].rearrange("p c w -> p (c w)").bitcast(FP8X4),
+                scales=v_scales[:, h].rearrange("p c w -> p (c w)"),
                 in_=job[n]["v_grouped"][:].rearrange("p c w t -> p (c w t)"),
             )
-            job[n]["v_codes"], job[n]["v_scales"] = v_codes, v_scales
+            if h == H - 1:
+                for c, m in MASKS:
+                    nc.sync.dma_start(out=v_masked[b % 3][(c, m)][kept(c, m)], in_=v_codes[kept(c, m), :, c, :])
+
+        def transpose_qk(n, bank, src, cols, moving, dst, tile_of):
+            step = NT // 2 if n == 0 else NT
+            for first in range(0, NT, step):
+                for t in range(first, first + step):
+                    nc.tensor.transpose(bank[:, t, :], src[:, tile_of(t), cols], moving[:])
+                nc.scalar.copy(out=dst[:, first:first + step, :].bitcast(F32),
+                               in_=bank[:, first:first + step, :].bitcast(F32))
 
         def q_transpose(r):
             n, i, b, cols = place(r)
@@ -235,35 +273,40 @@ def tile_causalshapedattention_pa_t_kernel(tc, q, k, v, alpha, beta, gamma, out)
                 if first_of_sequence(r) and b + 1 < B:
                     load(b + 1)
                 open_job(n)
-                qT_ps = psum_qk.tile([P, NT, P], BF16, name="qk_ps")
-                for t in range(NT):
-                    nc.tensor.transpose(qT_ps[:, t, :], raw[b][0][:, t, cols], ident_bf[:])
-                nc.scalar.copy(out=job[n]["qT"][:].bitcast(F32), in_=qT_ps[:].bitcast(F32))
+                bank = psum_qk.tile([P, NT, P], BF16, name="qk_ps")
+                transpose_qk(n, bank, raw[b][0], cols, ident_bf, job[n]["qT"], lambda t: t)
 
         def k_transpose(r):
             n, i, b, cols = place(r)
             if i == 0:
-                kT_ps = psum_qk.tile([P, NT, P], BF16, name="qk_ps")
-                for t in range(NT):
-                    nc.tensor.transpose(kT_ps[:, t, :], raw[b][1][:, t, cols], key_perm[:])
-                nc.scalar.copy(out=job[n]["kT"][:].bitcast(F32), in_=kT_ps[:].bitcast(F32))
+                if n == 0:
+                    bank = psum_t.tile([P, NT, P], BF16, name="bank")
+                else:
+                    bank = psum_qk.tile([P, NT, P], BF16, name="qk_ps")
+                transpose_qk(n, bank, raw[b][1], cols, key_perm, job[n]["kT"], tile_at)
 
         def score_row(r):
             n, i, b, cols = place(r)
             st = job[n]
             st["s"][i] = []
-            for j0 in range(0, i + 1, BANK_TILES):
-                tiles = min(BANK_TILES, i + 1 - j0)
-                on_diagonal = j0 + tiles == i + 1
-                s_ps = psum_s.tile([P, BANK_TILES, P], F32, name="s_ps")
+            for c in reversed(range(PASSES)):
+                if c == 1 and i < HALF:
+                    continue
+                own = c == i // HALF
+                if not own:
+                    first, last, on = 0, HALF, None
+                elif c == 0:
+                    first, last, on = 0, i + 1, i
+                else:
+                    first, last, on = NT - 1 - i, HALF, NT - 1 - i
+                s_ps = psum_s.tile([P, HALF, P], F32, name="s_ps")
+                keys = st["kT"][:, c * HALF:(c + 1) * HALF, :]
                 if i in WARM_ROWS:
-                    nc.tensor.matmul(s_ps[:], lhsT=st["qT"][:, i, :], rhs=st["kT"][:, j0:j0 + BANK_TILES, :],
-                                     start=True, stop=True)
-                nc.tensor.matmul(s_ps[:], lhsT=st["qT"][:, i, :], rhs=st["kT"][:, j0:j0 + BANK_TILES, :],
-                                 start=True, stop=not on_diagonal)
-                if on_diagonal:
-                    nc.tensor.matmul(s_ps[:, tiles - 1, :], lhsT=ident_bf[:], rhs=mask_add[:], start=False, stop=True)
-                st["s"][i].append(s_ps[:, :tiles, :])
+                    nc.tensor.matmul(s_ps[:], lhsT=st["qT"][:, i, :], rhs=keys, start=True, stop=True)
+                nc.tensor.matmul(s_ps[:], lhsT=st["qT"][:, i, :], rhs=keys, start=True, stop=on is None)
+                if on is not None:
+                    nc.tensor.matmul(s_ps[:, on, :], lhsT=ident_bf[:], rhs=mask_add[:], start=False, stop=True)
+                st["s"][i].append((s_ps[:, first:last, :], last - first))
 
         def max_bank(r, m):
             n, i, b, cols = place(r)
@@ -273,8 +316,10 @@ def tile_causalshapedattention_pa_t_kernel(tc, q, k, v, alpha, beta, gamma, out)
                 st["e"][i] = scores.tile([P, i + 1, P], F32, name="e%d" % i)
             if m < len(banks):
                 dest = st["neg_max"] if m == len(banks) - 1 else st["neg_max_half"]
-                nc.vector.tensor_scalar(out=st["e"][i][:, m * BANK_TILES:min((m + 1) * BANK_TILES, i + 1), :],
-                                        in0=banks[m], scalar1=-1.0,
+                done = sum(width for view, width in banks[:m])
+                view, width = banks[m]
+                nc.vector.tensor_scalar(out=st["e"][i][:, done:done + width, :],
+                                        in0=view, scalar1=-1.0,
                                         scalar2=st["neg_max_half"][:, i:i + 1] if m > 0 else None,
                                         op0=ALU.mult, op1=ALU.min, accum_out=dest[:, i:i + 1])
 
@@ -295,19 +340,22 @@ def tile_causalshapedattention_pa_t_kernel(tc, q, k, v, alpha, beta, gamma, out)
             n, i, b, cols = place(r)
             st = job[n]
             if i == 0:
-                st["grouped"] = heads.tile([P, len(UNITS), P, 4], BF16, name="grouped", align_bytes=64)
-                st["codes"] = heads.tile([P, len(UNITS), P], U32, name="codes", align_bytes=64)
-                st["scales"] = heads.tile([P, len(UNITS), P], U8, name="scales", align_bytes=64)
-            used = BLOCK * (i + 1)
+                st["grouped"] = heads.tile([P, N_UNITS, P, 4], BF16, name="grouped", align_bytes=64)
+                st["codes"] = heads.tile([P, N_UNITS, P], U32, name="codes", align_bytes=64)
+                st["scales"] = heads.tile([P, N_UNITS, P], U8, name="scales", align_bytes=64)
+            if i < HALF:
+                unit, quad, at = UNIT_LOW[i], i, i
+            else:
+                unit, quad, at = UNIT_HIGH[i], NT - 1 - i, 0
             nc.vector.scalar_tensor_tensor(
-                out=a_tiles[n % 2][i][:, :, used - BLOCK:used],
-                in0=st["e"][i][:, i, :].rearrange("q (u x) -> q u x", u=2),
+                out=a_sets[n % 2][:, :, unit, BLOCK * quad:BLOCK * (quad + 1)],
+                in0=st["e"][i][:, at, :].rearrange("q (u x) -> q u x", u=2),
                 scalar=st["gain"][:, i:i + 1], in1=shape_ps[:, i, :].rearrange("q (u x) -> q u x", u=2),
                 op0=ALU.mult, op1=ALU.add)
 
         def normalise_row(r):
             n, i, b, cols = place(r)
-            if i > 0 and i != VECTOR_ROW and not all_on_vector(n):
+            if i > 0 and i not in VECTOR_ROWS and not all_on_vector(n):
                 normalise(nc.gpsimd, n, i)
 
         def all_on_vector(n):
@@ -315,37 +363,33 @@ def tile_causalshapedattention_pa_t_kernel(tc, q, k, v, alpha, beta, gamma, out)
 
         def normalise(engine, n, i):
             st = job[n]
-            used = BLOCK * (i + 1)
-            engine.tensor_scalar(out=a_tiles[n % 2][i][:, :, :used - BLOCK].rearrange("q u (j x) -> q u j x", x=BLOCK),
-                                 in0=st["e"][i][:, :i, :].rearrange("q j (u x) -> q u j x", u=2),
+            flat = a_sets[n % 2][:].rearrange("q u n x -> q u (n x)")
+            if i < HALF:
+                first, at = 4 * BLOCK * UNIT_LOW[i], 0
+            else:
+                first, at = 4 * BLOCK * UNIT_HIGH[i] + BLOCK * (NT - i), 1
+            engine.tensor_scalar(out=flat[:, :, first:first + BLOCK * i].rearrange("q u (j x) -> q u j x", x=BLOCK),
+                                 in0=st["e"][i][:, at:at + i, :].rearrange("q j (u x) -> q u j x", u=2),
                                  scalar1=st["gain"][:, i:i + 1], scalar2=below[:, i:i + 1],
                                  op0=ALU.mult, op1=ALU.add)
 
-        def rows_filling(i, n_units):
-            end = UNITS.index((i, 0)) + passes_of(i)
-            if end % n_units != 0:
-                return []
-            return [m for m in range(NT) if end - n_units <= UNITS.index((m, 0)) < end]
-
         def a_transpose(r):
             n, i, b, cols = place(r)
-            rows = rows_filling(i, BANK_UNITS)
-            if rows:
-                bank = psum_t.tile([P, BANK_UNITS, 2, P], F32, name="bank")
-                first = UNITS.index((rows[0], 0))
-                for m, c in UNITS[first:first + BANK_UNITS]:
-                    words = a_tiles[n % 2][m][:].bitcast(F32)
+            if i in UNIT_BANKS:
+                units = UNIT_BANKS[i]
+                bank = psum_t.tile([P, len(units), 2, P], F32, name="bank")
+                words = a_sets[n % 2][:].rearrange("q u n x -> q (u n x)").bitcast(F32).rearrange(
+                    "q (u n w) -> q u n w", u=2, n=N_UNITS)
+                for m, unit in enumerate(units):
                     for u in range(2):
-                        nc.tensor.transpose(bank[:, UNITS.index((m, c)) - first, u, :],
-                                            words[:, u, c * P:(c + 1) * P], ident_f32[:])
+                        nc.tensor.transpose(bank[:, m, u, :], words[:, u, unit, :], ident_f32[:])
                 job[n]["bank"][i] = bank
 
         def a_copy(r):
             n, i, b, cols = place(r)
-            rows = rows_filling(i, BANK_UNITS)
-            if rows:
-                first = UNITS.index((rows[0], 0))
-                nc.scalar.copy(out=job[n]["grouped"][:, first:first + BANK_UNITS].bitcast(F32),
+            if i in UNIT_BANKS:
+                units = UNIT_BANKS[i]
+                nc.scalar.copy(out=job[n]["grouped"][:, units[0]:units[-1] + 1].bitcast(F32),
                                in_=job[n]["bank"][i][:].rearrange("p c u i -> p c i u"))
 
         def quantise_a(n):
@@ -357,19 +401,23 @@ def tile_causalshapedattention_pa_t_kernel(tc, q, k, v, alpha, beta, gamma, out)
                     in_=st["grouped"][:, g:g + units].rearrange("p n i t -> p (n i t)"),
                 )
 
+        def make_bias(n, first, last=NT):
+            nc.vector.tensor_scalar(out=job[n]["bias"][:, first:last], in0=job[n]["neg_max"][:, first:last],
+                                    scalar1=scale, scalar2=EXP_SHIFT, op0=ALU.mult, op1=ALU.add)
+
         def port_phase(p):
             def live(n):
                 return 0 <= n < B * H
             if live(p - 3):
                 quantise_a(p - 3)
             if live(p):
-                nc.vector.tensor_scalar(out=job[p]["bias"][:], in0=job[p]["neg_max"][:],
-                                        scalar1=scale, scalar2=EXP_SHIFT, op0=ALU.mult, op1=ALU.add)
+                make_bias(p, HALF if p in HALF_BIAS else 0)
             if live(p - 1):
                 gain = heads.tile([P, NT], F32, name="gain")
                 nc.vector.reciprocal(out=gain[:], in_=job[p - 1]["row_sum"][:])
             if live(p - 2) and not all_on_vector(p - 2):
-                normalise(nc.vector, p - 2, VECTOR_ROW)
+                for i in VECTOR_ROWS:
+                    normalise(nc.vector, p - 2, i)
             if live(p - 1):
                 nc.vector.tensor_scalar(out=gain[:], in0=gain[:], scalar1=beta_f[:, 0:1], scalar2=None,
                                         op0=ALU.mult)
@@ -382,21 +430,28 @@ def tile_causalshapedattention_pa_t_kernel(tc, q, k, v, alpha, beta, gamma, out)
         def multiply_rows(r):
             n, i, b, cols = place(r)
             st = job[n]
-            for m in rows_filling(i, QUANT_UNITS):
-                if m % 4 == 0:
-                    st["o_ps"] = psum_o.tile([P, 4, P], F32, name="o_ps")
-                for c in range(PASSES):
-                    if c < passes_of(m):
-                        unit = UNITS.index((m, c))
-                        a_codes, a_scales = st["codes"][:, unit, :], st["scales"][:, unit, :]
-                    else:
-                        a_codes, a_scales = far_codes[:, m, :], far_scales[:, m, :]
-                    nc.tensor.matmul_mx(
-                        out=st["o_ps"][:, m % 4, :],
-                        lhsT=a_codes.bitcast(FP8X4), lhsT_scale=a_scales,
-                        rhs=st["v_codes"][:, c, :].bitcast(FP8X4), rhs_scale=st["v_scales"][:, c, :],
-                        start=(c == 0), stop=(c == PASSES - 1),
-                    )
+            h = n % H
+            v_codes, v_scales = seq[b]
+            if i % 4 == 0:
+                st["o_ps"] = psum_o.tile([P, 4, P], F32, name="o_ps")
+            passes = []
+            for c in range(PASSES):
+                unit = (UNIT_LOW, UNIT_HIGH)[c][i]
+                tiles = min(HALF, max(0, i + 1 - c * HALF))
+                if tiles == HALF:
+                    passes.append((st["codes"][:, unit, :], st["scales"][:, unit, :], c, v_codes[:, h, c, :]))
+                elif tiles > 0:
+                    passes.append((st["codes"][:, unit, :], st["scales"][:, unit, :], c, v_masked[b % 3][(c, tiles)][:, h, :]))
+                if tiles < HALF:
+                    far = far_index(c, i)
+                    passes.append((far_codes[:, far, :], far_scales[:, far, :], c, v_codes[:, h, c, :]))
+            for m, (a_codes, a_scales, c, moving) in enumerate(passes):
+                nc.tensor.matmul_mx(
+                    out=st["o_ps"][:, i % 4, :],
+                    lhsT=a_codes.bitcast(FP8X4), lhsT_scale=a_scales,
+                    rhs=moving.bitcast(FP8X4), rhs_scale=v_scales[:, h, c, :],
+                    start=(m == 0), stop=(m == len(passes) - 1),
+                )
 
         def out_copy(r):
             n, i, b, cols = place(r)
@@ -414,24 +469,24 @@ def tile_causalshapedattention_pa_t_kernel(tc, q, k, v, alpha, beta, gamma, out)
 
         early_constants()
         ctx.enter_context(tc.manual_schedule(engines={mybir.EngineType.DVE, mybir.EngineType.Pool}))
-        for s in range(-4, n_rows + 31):
+        for s in range(-4, n_rows + 36):
             run(score_row, s + 1)
             run(max_first_bank, s)
-            run(diagonal_tile, s - 16)
+            run(diagonal_tile, s - L_DIAG)
             run(max_second_bank, s)
-            run(a_copy, s - 21)
-            run(out_copy, s - 30)
-            run(exp_row, s - 8)
-            run(normalise_row, s - 16)
-            run(regroup_v, s - 8)
-            run(a_transpose, s - 20)
-            run(multiply_rows, s - 29)
+            run(a_copy, s - L_ACOPY)
+            run(out_copy, s - L_OUT)
+            run(exp_row, s - L_EXP)
+            run(normalise_row, s - L_NORM)
+            run(regroup_v, s - L_V)
+            run(a_transpose, s - L_AT)
+            run(multiply_rows, s - L_MUL)
             run(k_transpose, s + 3)
             run(q_transpose, s + 4)
+            if s == 3:
+                make_bias(0, 0, HALF)
             if s == CONST_STEP:
                 late_constants()
-            if s == SECOND_SET_STEP:
-                fill_right_of_diagonal(a_tiles[1])
             if s == FAR_STEP:
                 far_units()
             if s % NT == NT - 1:

@@ -27,18 +27,21 @@ MASKED = -1e20
 EXP_SHIFT = 10.1
 FLOPS = 2 * 2 * B * H * T * T * D
 
-UNIT_LOW = (5, 3, 1, 0, 2, 4, 6, 8)
-UNIT_HIGH = (None, None, None, None, 1, 3, 5, 7)
+UNIT_LOW = (1, 7, 5, 0, 6, 8, 2, 4)
+UNIT_HIGH = (None, None, None, None, 5, 7, 1, 3)
 N_UNITS = 9
-UNIT_BANKS = {3: (0,), 4: (1, 2), 5: (3, 4), 6: (5, 6), 7: (7, 8)}
-QUANT_CALLS = ((0, 8), (8, 1))
-CONST_STEP = 1
-FAR_STEP = 14
-LAST_JOBS = 2
-VECTOR_ROWS = (5,)
+UNIT_BANKS = {3: (0,), 6: (1, 2), 7: (3, 4), 4: (5, 6), 5: (7, 8)}
+ROWS = ((0, 3, 6, 7), (1, 2, 4, 5))
+BATCH = 4
+BATCHES = NT // BATCH
+QUANT_CALLS = (((0, 4), (4, 1)), ((5, 4),))
+FAR_STEP = 12
+SHAPE_STEP = 4
+LAST_BATCHES = 3
+VECTOR_ROWS = (3, 4)
+SCALAR_ROWS = ()
 WARM_ROWS = (0, 2)
-L_DIAG, L_ACOPY, L_OUT, L_EXP, L_NORM, L_V, L_AT, L_MUL = 16, 21, 33, 8, 16, 8, 20, 32
-HALF_BIAS = (0,)
+L_DIAG, L_ACOPY, L_OUT, L_EXP, L_NORM, L_AT, L_MUL = 8, 12, 17, 4, 8, 11, 16
 
 
 def tile_at(pos):
@@ -98,6 +101,9 @@ def tile_causalshapedattention_pa_t_kernel(tc, q, k, v, alpha, beta, gamma, out)
         make_identity(nc, ident_bf[:])
         key_perm = const.tile([P, P], BF16)
         to_key_order(key_perm, ident_bf)
+        row_f = const.tile([P, NT], F32)
+        nc.gpsimd.iota(row_f[:], pattern=[[P, NT]], base=0, channel_multiplier=1,
+                       allow_small_or_imprecise_dtypes=True)
         lower_nat = const.tile([P, P], F32)
         nc.gpsimd.memset(lower_nat[:], 1.0)
         nc.gpsimd.affine_select(
@@ -111,12 +117,9 @@ def tile_causalshapedattention_pa_t_kernel(tc, q, k, v, alpha, beta, gamma, out)
                                 op0=ALU.mult, op1=ALU.add)
 
         ident_f32 = const.tile([P, P], F32)
-        diag = const.tile([P, P], F32)
-        beta_f = const.tile([P, 1], F32)
         above = const.tile([P, NT], F32)
         above_pair = const.tile([P, NT, 2], BF16)
         below = const.tile([P, NT], F32)
-        shape_add = const.tile([P, NT, P], F32)
         shape_bf = const.tile([P, NT, P], BF16)
         shape_ps = psum_shape.tile([P, NT, P], BF16)
         a_sets = [const.tile([P, 2, N_UNITS, 4 * BLOCK], BF16, name="a%d" % s) for s in range(2)]
@@ -125,61 +128,45 @@ def tile_causalshapedattention_pa_t_kernel(tc, q, k, v, alpha, beta, gamma, out)
         far_codes = const.tile([P, n_far, P], U32, align_bytes=64)
         far_scales = const.tile([P, n_far, P], U8, align_bytes=64)
         MASKS = [(c, m) for c in range(PASSES) for m in range(1, HALF)]
-        v_masked = [{key: const.tile([P, H, D], I32, name="vm%d_%d_%d" % ((s,) + key), align_bytes=64) for key in MASKS}
-                    for s in range(3)]
-
-        spread = const.tile([P, NT], F32)
-        is_last = const.tile([P, NT], F32)
+        v_masked = const.tile([P, 2, len(MASKS), H, D], I32, align_bytes=64)
 
         def kept(c, m):
             return slice(0, QUAD * m) if c == 0 else slice(P - QUAD * m, P)
 
-        def early_constants():
-            nc.vector.memset(far_grouped[:].rearrange("p n i t -> p (n i t)").bitcast(I32), 0)
-            for vm in v_masked:
-                for key in MASKS:
-                    nc.vector.memset(vm[key][:], 0)
-            make_identity(nc, ident_f32[:])
-            nc.gpsimd.tensor_copy(out=diag[:].rearrange("k (u p e) -> k u p e", u=2, e=2),
-                                  in_=ident_f32[:].rearrange("k (p u e) -> k u p e", u=2, e=2))
-            row_f = const.tile([P, NT], F32)
-            nc.gpsimd.iota(row_f[:], pattern=[[P, NT]], base=0, channel_multiplier=1,
-                           allow_small_or_imprecise_dtypes=True)
-            nc.gpsimd.tensor_scalar(out=is_last[:], in0=row_f[:], scalar1=float(T - 1), scalar2=None,
-                                    op0=ALU.is_equal)
-            all_keys = const.tile([P, NT], F32)
-            nc.gpsimd.tensor_scalar(out=all_keys[:], in0=is_last[:], scalar1=float(T), scalar2=0.0,
+        def constants():
+            is_last = const.tile([P, NT], F32)
+            nc.vector.tensor_scalar(out=is_last[:], in0=row_f[:], scalar1=float(T - 1), scalar2=None, op0=ALU.is_equal)
+            spread = const.tile([P, NT], F32)
+            nc.vector.tensor_scalar(out=spread[:], in0=row_f[:], scalar1=-1.0, scalar2=float(T - 1),
                                     op0=ALU.mult, op1=ALU.add)
-            nc.gpsimd.tensor_scalar(out=spread[:], in0=row_f[:], scalar1=-1.0, scalar2=float(T - 1),
-                                    op0=ALU.mult, op1=ALU.add)
-            nc.gpsimd.tensor_tensor(out=spread[:], in0=spread[:], in1=all_keys[:], op=ALU.add)
-
-        def late_constants():
+            nc.vector.scalar_tensor_tensor(out=spread[:], in0=is_last[:], scalar=float(T), in1=spread[:],
+                                           op0=ALU.mult, op1=ALU.add)
             nc.vector.reciprocal(out=spread[:], in_=spread[:])
             alpha_f = const.tile([P, 1], F32)
             gamma_f = const.tile([P, 1], F32)
-            nc.gpsimd.tensor_copy(out=gamma_f[:], in_=gamma_bf[:])
-            nc.gpsimd.tensor_copy(out=alpha_f[:], in_=alpha_bf[:])
-            nc.gpsimd.tensor_copy(out=beta_f[:], in_=beta_bf[:])
-            nc.gpsimd.tensor_scalar(out=above[:], in0=spread[:], scalar1=gamma_f[:, 0:1], scalar2=-1.0,
+            nc.vector.tensor_copy(out=gamma_f[:], in_=gamma_bf[:])
+            nc.vector.tensor_scalar(out=above[:], in0=spread[:], scalar1=gamma_f[:, 0:1], scalar2=-1.0,
                                     op0=ALU.mult, op1=ALU.mult)
-            for e in range(2):
-                nc.gpsimd.tensor_scalar(out=above_pair[:, :, e], in0=above[:], scalar1=1.0, scalar2=0.0,
-                                        op0=ALU.mult, op1=ALU.add)
-            nc.gpsimd.tensor_tensor(out=below[:], in0=above[:], in1=is_last[:], op=ALU.mult)
+            nc.vector.tensor_copy(out=alpha_f[:], in_=alpha_bf[:])
+            nc.vector.tensor_tensor(out=below[:], in0=above[:], in1=is_last[:], op=ALU.mult)
             step_down = const.tile([P, NT], F32)
-            nc.gpsimd.tensor_tensor(out=step_down[:], in0=below[:], in1=above[:], op=ALU.subtract)
+            nc.vector.tensor_tensor(out=step_down[:], in0=below[:], in1=above[:], op=ALU.subtract)
+            alpha_diag = const.tile([P, P], BF16)
+            nc.vector.tensor_scalar(out=alpha_diag[:], in0=key_perm[:], scalar1=alpha_f[:, 0:1], scalar2=None,
+                                    op0=ALU.mult)
+            for e in range(2):
+                nc.vector.tensor_copy(out=above_pair[:, :, e], in_=above[:])
+            nc.vector.memset(v_masked[:].rearrange("p s m h w -> p (s m h w)"), 0)
+            return step_down, alpha_diag
+
+        def shape_constants(step_down, alpha_diag):
             for i in range(NT):
-                nc.scalar.activation(out=shape_add[:, i, :], in_=lower[:], func=ACT.Identity,
+                nc.scalar.activation(out=shape_bf[:, i, :], in_=lower[:], func=ACT.Identity,
                                      bias=above[:, i:i + 1], scale=step_down[:, i:i + 1])
-            alpha_diag = const.tile([P, P], F32)
-            nc.gpsimd.tensor_scalar(out=alpha_diag[:], in0=diag[:], scalar1=alpha_f[:, 0:1], scalar2=0.0,
-                                    op0=ALU.mult, op1=ALU.add)
             for i in range(NT):
-                nc.gpsimd.tensor_tensor(out=shape_bf[:, i, :], in0=shape_add[:, i, :], in1=alpha_diag[:], op=ALU.add)
-            for first in range(0, NT, HALF):
-                nc.tensor.matmul(shape_ps[:, first:first + HALF, :], lhsT=ident_bf[:],
-                                 rhs=shape_bf[:, first:first + HALF, :], start=True, stop=True)
+                nc.tensor.matmul(shape_ps[:, i, :], lhsT=ident_bf[:], rhs=shape_bf[:, i, :], start=True, stop=False)
+                nc.tensor.matmul(shape_ps[:, i, :], lhsT=ident_bf[:], rhs=alpha_diag[:], start=False, stop=True)
+            make_identity(nc, ident_f32[:])
 
         def far_index(c, i):
             return i if c == 0 else HALF - 1 + i
@@ -202,6 +189,8 @@ def tile_causalshapedattention_pa_t_kernel(tc, q, k, v, alpha, beta, gamma, out)
                             parts = slice(QUAD * a, QUAD * z)
                             nc.scalar.copy(out=grouped[parts, far_index(c, i)],
                                            in_=bank[parts, i - first, :].unsqueeze(2).to_broadcast([QUAD * (z - a), P, 2]))
+
+        def far_quantise():
             for first, n in ((0, 8), (8, 2)):
                 nc.vector.quantize_mx(
                     out=far_codes[:, first:first + n].rearrange("p n i -> p (n i)").bitcast(FP8X4),
@@ -218,9 +207,13 @@ def tile_causalshapedattention_pa_t_kernel(tc, q, k, v, alpha, beta, gamma, out)
         n_rows = B * H * NT
 
         def place(r):
-            n, i = divmod(r, NT)
+            n, m = divmod(r, NT)
             b, h = divmod(n, H)
-            return n, i, b, slice(h * D, (h + 1) * D)
+            return n, ROWS[m // BATCH][m % BATCH], b, slice(h * D, (h + 1) * D)
+
+        def at(i):
+            g = 0 if i in ROWS[0] else 1
+            return g, ROWS[g].index(i)
 
         def first_of_sequence(r):
             return r % (H * NT) == 0
@@ -230,15 +223,17 @@ def tile_causalshapedattention_pa_t_kernel(tc, q, k, v, alpha, beta, gamma, out)
                 "s": {}, "e": {}, "bank": {},
                 "qT": heads.tile([P, NT, P], BF16, name="qT"),
                 "kT": heads.tile([P, NT, P], BF16, name="kT"),
-                "neg_max": long_lived.tile([P, NT], F32, name="neg_max"),
-                "neg_max_half": long_lived.tile([P, NT], F32, name="neg_max_half"),
-                "row_sum": long_lived.tile([P, NT], F32, name="row_sum"),
-                "bias": long_lived.tile([P, NT], F32, name="bias"),
             }
+            for name in ("neg_max", "neg_max_half", "row_sum", "bias", "gain"):
+                job[n][name] = [long_lived.tile([P, BATCH], F32, name="%s%d" % (name, g)) for g in range(BATCHES)]
+
+        def stat(n, name, i):
+            g, m = at(i)
+            return job[n][name][g][:, m:m + 1]
 
         def regroup_v(r):
             n, i, b, cols = place(r)
-            if i == NT - 1:
+            if i == 0:
                 v_grouped = heads.tile([P, PASSES, D, 4], BF16, name="v_grouped", align_bytes=64)
                 nc.gpsimd.tensor_scalar(out=v_grouped[:], in0=raw[b][2][:, :, :, cols].rearrange("p c t w -> p c w t"),
                                         scalar1=1.0, scalar2=0.0, op0=ALU.mult, op1=ALU.add)
@@ -257,7 +252,7 @@ def tile_causalshapedattention_pa_t_kernel(tc, q, k, v, alpha, beta, gamma, out)
             )
             if h == H - 1:
                 for c, m in MASKS:
-                    nc.sync.dma_start(out=v_masked[b % 3][(c, m)][kept(c, m)], in_=v_codes[kept(c, m), :, c, :])
+                    nc.sync.dma_start(out=v_masked[kept(c, m), b % 2, MASKS.index((c, m))], in_=v_codes[kept(c, m), :, c, :])
 
         def transpose_qk(n, bank, src, cols, moving, dst, tile_of):
             step = NT // 2 if n == 0 else NT
@@ -315,13 +310,13 @@ def tile_causalshapedattention_pa_t_kernel(tc, q, k, v, alpha, beta, gamma, out)
             if m == 0:
                 st["e"][i] = scores.tile([P, i + 1, P], F32, name="e%d" % i)
             if m < len(banks):
-                dest = st["neg_max"] if m == len(banks) - 1 else st["neg_max_half"]
+                dest = stat(n, "neg_max" if m == len(banks) - 1 else "neg_max_half", i)
                 done = sum(width for view, width in banks[:m])
                 view, width = banks[m]
                 nc.vector.tensor_scalar(out=st["e"][i][:, done:done + width, :],
                                         in0=view, scalar1=-1.0,
-                                        scalar2=st["neg_max_half"][:, i:i + 1] if m > 0 else None,
-                                        op0=ALU.mult, op1=ALU.min, accum_out=dest[:, i:i + 1])
+                                        scalar2=stat(n, "neg_max_half", i) if m > 0 else None,
+                                        op0=ALU.mult, op1=ALU.min, accum_out=dest)
 
         def max_first_bank(r):
             max_bank(r, 0)
@@ -333,8 +328,7 @@ def tile_causalshapedattention_pa_t_kernel(tc, q, k, v, alpha, beta, gamma, out)
             n, i, b, cols = place(r)
             st = job[n]
             nc.scalar.activation(out=st["e"][i][:], in_=st["e"][i][:], func=ACT.Exp,
-                                 bias=st["bias"][:, i:i + 1], scale=-scale,
-                                 accum_out=st["row_sum"][:, i:i + 1])
+                                 bias=stat(n, "bias", i), scale=-scale, accum_out=stat(n, "row_sum", i))
 
         def diagonal_tile(r):
             n, i, b, cols = place(r)
@@ -344,34 +338,37 @@ def tile_causalshapedattention_pa_t_kernel(tc, q, k, v, alpha, beta, gamma, out)
                 st["codes"] = heads.tile([P, N_UNITS, P], U32, name="codes", align_bytes=64)
                 st["scales"] = heads.tile([P, N_UNITS, P], U8, name="scales", align_bytes=64)
             if i < HALF:
-                unit, quad, at = UNIT_LOW[i], i, i
+                unit, quad, pos = UNIT_LOW[i], i, i
             else:
-                unit, quad, at = UNIT_HIGH[i], NT - 1 - i, 0
+                unit, quad, pos = UNIT_HIGH[i], NT - 1 - i, 0
             nc.vector.scalar_tensor_tensor(
                 out=a_sets[n % 2][:, :, unit, BLOCK * quad:BLOCK * (quad + 1)],
-                in0=st["e"][i][:, at, :].rearrange("q (u x) -> q u x", u=2),
-                scalar=st["gain"][:, i:i + 1], in1=shape_ps[:, i, :].rearrange("q (u x) -> q u x", u=2),
+                in0=st["e"][i][:, pos, :].rearrange("q (u x) -> q u x", u=2),
+                scalar=stat(n, "gain", i), in1=shape_ps[:, i, :].rearrange("q (u x) -> q u x", u=2),
                 op0=ALU.mult, op1=ALU.add)
 
         def normalise_row(r):
             n, i, b, cols = place(r)
-            if i > 0 and i not in VECTOR_ROWS and not all_on_vector(n):
-                normalise(nc.gpsimd, n, i)
+            if i > 0 and i not in VECTOR_ROWS and not all_on_vector(r // BATCH):
+                normalise(nc.scalar if i in SCALAR_ROWS else nc.gpsimd, n, i)
 
-        def all_on_vector(n):
-            return n >= B * H - LAST_JOBS
+        def all_on_vector(g):
+            return g >= B * H * BATCHES - LAST_BATCHES
 
         def normalise(engine, n, i):
             st = job[n]
             flat = a_sets[n % 2][:].rearrange("q u n x -> q u (n x)")
             if i < HALF:
-                first, at = 4 * BLOCK * UNIT_LOW[i], 0
+                first, pos = 4 * BLOCK * UNIT_LOW[i], 0
             else:
-                first, at = 4 * BLOCK * UNIT_HIGH[i] + BLOCK * (NT - i), 1
-            engine.tensor_scalar(out=flat[:, :, first:first + BLOCK * i].rearrange("q u (j x) -> q u j x", x=BLOCK),
-                                 in0=st["e"][i][:, at:at + i, :].rearrange("q j (u x) -> q u j x", u=2),
-                                 scalar1=st["gain"][:, i:i + 1], scalar2=below[:, i:i + 1],
-                                 op0=ALU.mult, op1=ALU.add)
+                first, pos = 4 * BLOCK * UNIT_HIGH[i] + BLOCK * (NT - i), 1
+            a_out = flat[:, :, first:first + BLOCK * i].rearrange("q u (j x) -> q u j x", x=BLOCK)
+            e_in = st["e"][i][:, pos:pos + i, :].rearrange("q j (u x) -> q u j x", u=2)
+            if engine is nc.scalar:
+                nc.scalar.activation(out=a_out, in_=e_in, func=ACT.Identity, scale=stat(n, "gain", i), bias=below[:, i:i + 1])
+            else:
+                engine.tensor_scalar(out=a_out, in0=e_in, scalar1=stat(n, "gain", i), scalar2=below[:, i:i + 1],
+                                     op0=ALU.mult, op1=ALU.add)
 
         def a_transpose(r):
             n, i, b, cols = place(r)
@@ -392,48 +389,51 @@ def tile_causalshapedattention_pa_t_kernel(tc, q, k, v, alpha, beta, gamma, out)
                 nc.scalar.copy(out=job[n]["grouped"][:, units[0]:units[-1] + 1].bitcast(F32),
                                in_=job[n]["bank"][i][:].rearrange("p c u i -> p c i u"))
 
-        def quantise_a(n):
+        def quantise_a(x):
+            n, g = divmod(x, BATCHES)
             st = job[n]
-            for g, units in QUANT_CALLS:
+            for first, units in QUANT_CALLS[g]:
                 nc.vector.quantize_mx(
-                    out=st["codes"][:, g:g + units].rearrange("p n i -> p (n i)").bitcast(FP8X4),
-                    scales=st["scales"][:, g:g + units].rearrange("p n i -> p (n i)"),
-                    in_=st["grouped"][:, g:g + units].rearrange("p n i t -> p (n i t)"),
+                    out=st["codes"][:, first:first + units].rearrange("p n i -> p (n i)").bitcast(FP8X4),
+                    scales=st["scales"][:, first:first + units].rearrange("p n i -> p (n i)"),
+                    in_=st["grouped"][:, first:first + units].rearrange("p n i t -> p (n i t)"),
                 )
 
-        def make_bias(n, first, last=NT):
-            nc.vector.tensor_scalar(out=job[n]["bias"][:, first:last], in0=job[n]["neg_max"][:, first:last],
-                                    scalar1=scale, scalar2=EXP_SHIFT, op0=ALU.mult, op1=ALU.add)
-
-        def port_phase(p):
-            def live(n):
-                return 0 <= n < B * H
-            if live(p - 3):
-                quantise_a(p - 3)
-            if live(p):
-                make_bias(p, HALF if p in HALF_BIAS else 0)
-            if live(p - 1):
-                gain = heads.tile([P, NT], F32, name="gain")
-                nc.vector.reciprocal(out=gain[:], in_=job[p - 1]["row_sum"][:])
-            if live(p - 2) and not all_on_vector(p - 2):
+        def port_phase(x):
+            def live(y):
+                return 0 <= y < B * H * BATCHES
+            if live(x - 3):
+                quantise_a(x - 3)
+            if live(x):
+                n, g = divmod(x, BATCHES)
+                nc.vector.tensor_scalar(out=job[n]["bias"][g][:], in0=job[n]["neg_max"][g][:],
+                                        scalar1=scale, scalar2=EXP_SHIFT, op0=ALU.mult, op1=ALU.add)
+            if live(x - 1):
+                n, g = divmod(x - 1, BATCHES)
+                gain = job[n]["gain"][g]
+                nc.vector.reciprocal(out=gain[:], in_=job[n]["row_sum"][g][:])
+            if live(x - 2) and not all_on_vector(x - 2):
+                m, f = divmod(x - 2, BATCHES)
                 for i in VECTOR_ROWS:
-                    normalise(nc.vector, p - 2, i)
-            if live(p - 1):
-                nc.vector.tensor_scalar(out=gain[:], in0=gain[:], scalar1=beta_f[:, 0:1], scalar2=None,
-                                        op0=ALU.mult)
-                job[p - 1]["gain"] = gain
-                if all_on_vector(p - 1):
-                    for i in range(1, NT):
-                        normalise(nc.vector, p - 1, i)
-                quantise_v(p - 1)
+                    if i in ROWS[f]:
+                        normalise(nc.vector, m, i)
+            if live(x - 1):
+                nc.vector.tensor_scalar(out=gain[:], in0=gain[:], scalar1=beta_bf[:, 0:1], scalar2=None, op0=ALU.mult)
+                if all_on_vector(x - 1):
+                    for i in ROWS[g]:
+                        if i > 0:
+                            normalise(nc.vector, n, i)
+            if live(x) and x % BATCHES == 0:
+                quantise_v(x // BATCHES)
 
         def multiply_rows(r):
             n, i, b, cols = place(r)
             st = job[n]
             h = n % H
             v_codes, v_scales = seq[b]
-            if i % 4 == 0:
-                st["o_ps"] = psum_o.tile([P, 4, P], F32, name="o_ps")
+            g, place_in_batch = at(i)
+            if place_in_batch == 0:
+                st["o_ps"] = psum_o.tile([P, BATCH, P], F32, name="o_ps")
             passes = []
             for c in range(PASSES):
                 unit = (UNIT_LOW, UNIT_HIGH)[c][i]
@@ -441,13 +441,13 @@ def tile_causalshapedattention_pa_t_kernel(tc, q, k, v, alpha, beta, gamma, out)
                 if tiles == HALF:
                     passes.append((st["codes"][:, unit, :], st["scales"][:, unit, :], c, v_codes[:, h, c, :]))
                 elif tiles > 0:
-                    passes.append((st["codes"][:, unit, :], st["scales"][:, unit, :], c, v_masked[b % 3][(c, tiles)][:, h, :]))
+                    passes.append((st["codes"][:, unit, :], st["scales"][:, unit, :], c, v_masked[:, b % 2, MASKS.index((c, tiles)), h, :]))
                 if tiles < HALF:
                     far = far_index(c, i)
                     passes.append((far_codes[:, far, :], far_scales[:, far, :], c, v_codes[:, h, c, :]))
             for m, (a_codes, a_scales, c, moving) in enumerate(passes):
                 nc.tensor.matmul_mx(
-                    out=st["o_ps"][:, i % 4, :],
+                    out=st["o_ps"][:, place_in_batch, :],
                     lhsT=a_codes.bitcast(FP8X4), lhsT_scale=a_scales,
                     rhs=moving.bitcast(FP8X4), rhs_scale=v_scales[:, h, c, :],
                     start=(m == 0), stop=(m == len(passes) - 1),
@@ -455,21 +455,21 @@ def tile_causalshapedattention_pa_t_kernel(tc, q, k, v, alpha, beta, gamma, out)
 
         def out_copy(r):
             n, i, b, cols = place(r)
-            st = job[n]
-            if i == 3:
-                st["out_sb"] = heads.tile([P, NT, D], F32, name="out_sb")
-            if i % 4 == 3:
-                nc.scalar.copy(out=st["out_sb"][:, i - 3:i + 1, :], in_=st["o_ps"][:])
-                nc.sync.dma_start(out=out[b, (i - 3) * P:(i + 1) * P, cols].rearrange("(n p) c -> p n c", p=P),
-                                  in_=st["out_sb"][:, i - 3:i + 1, :])
+            g, m = at(i)
+            if m == BATCH - 1:
+                out_sb = heads.tile([P, BATCH, D], F32, name="out_sb")
+                nc.scalar.copy(out=out_sb[:], in_=job[n]["o_ps"][:])
+                rows = out[b, :, cols].rearrange("(n p) c -> p n c", p=P)
+                for first, tiles in (((0, slice(0, 7, 3)), (3, slice(7, 8))) if g == 0 else ((0, slice(1, 3)), (2, slice(4, 6)))):
+                    nc.sync.dma_start(out=rows[:, tiles, :], in_=out_sb[:, first:first + (3 if first == 0 and g == 0 else 2 if g == 1 else 1), :])
 
         def run(stage, r):
             if 0 <= r < n_rows:
                 stage(r)
 
-        early_constants()
         ctx.enter_context(tc.manual_schedule(engines={mybir.EngineType.DVE, mybir.EngineType.Pool}))
-        for s in range(-4, n_rows + 36):
+        shape_parts = constants()
+        for s in range(-4, n_rows + 20):
             run(score_row, s + 1)
             run(max_first_bank, s)
             run(diagonal_tile, s - L_DIAG)
@@ -478,16 +478,18 @@ def tile_causalshapedattention_pa_t_kernel(tc, q, k, v, alpha, beta, gamma, out)
             run(out_copy, s - L_OUT)
             run(exp_row, s - L_EXP)
             run(normalise_row, s - L_NORM)
-            run(regroup_v, s - L_V)
+            run(regroup_v, s + 1 if s > 2 else s - 2)
             run(a_transpose, s - L_AT)
             run(multiply_rows, s - L_MUL)
             run(k_transpose, s + 3)
             run(q_transpose, s + 4)
-            if s == 3:
-                make_bias(0, 0, HALF)
-            if s == CONST_STEP:
-                late_constants()
+            if s == SHAPE_STEP:
+                shape_constants(*shape_parts)
+            if s == 2:
+                nc.gpsimd.memset(far_grouped[:].rearrange("p n i t -> p (n i t)").bitcast(F32), 0.0)
             if s == FAR_STEP:
                 far_units()
-            if s % NT == NT - 1:
-                port_phase(s // NT)
+            if s == FAR_STEP + 3:
+                far_quantise()
+            if s % BATCH == BATCH - 1:
+                port_phase(s // BATCH)

@@ -64,6 +64,7 @@ def tile_causalshapedattention_pa_t_kernel(tc, q, k, v, alpha, beta, gamma, out)
         psum_qk = ctx.enter_context(tc.psum_pool(name="psum_qk", bufs=1))
         psum_shape = ctx.enter_context(tc.psum_pool(name="psum_shape", bufs=1))
 
+        ctx.enter_context(tc.manual_schedule(engines={mybir.EngineType.DVE, mybir.EngineType.Pool}))
         raw = {}
         job = {}
         seq = {}
@@ -122,7 +123,8 @@ def tile_causalshapedattention_pa_t_kernel(tc, q, k, v, alpha, beta, gamma, out)
         below = const.tile([P, NT], F32)
         shape_bf = const.tile([P, NT, P], BF16)
         shape_ps = psum_shape.tile([P, NT, P], BF16)
-        a_sets = [const.tile([P, 2, N_UNITS, 4 * BLOCK], BF16, name="a%d" % s) for s in range(2)]
+        a_sets = [{i: const.tile([P, 2, len(units), 4 * BLOCK], BF16, name="a%d_%d" % (s, i)) for i, units in UNIT_BANKS.items()}
+                  for s in range(2)]
         n_far = NT + HALF - 2
         far_grouped = const.tile([P, n_far, P, 4], BF16, align_bytes=64)
         far_codes = const.tile([P, n_far, P], U32, align_bytes=64)
@@ -342,7 +344,7 @@ def tile_causalshapedattention_pa_t_kernel(tc, q, k, v, alpha, beta, gamma, out)
             else:
                 unit, quad, pos = UNIT_HIGH[i], NT - 1 - i, 0
             nc.vector.scalar_tensor_tensor(
-                out=a_sets[n % 2][:, :, unit, BLOCK * quad:BLOCK * (quad + 1)],
+                out=a_sets[n % 2][bank_of(unit)][:, :, UNIT_BANKS[bank_of(unit)].index(unit), BLOCK * quad:BLOCK * (quad + 1)],
                 in0=st["e"][i][:, pos, :].rearrange("q (u x) -> q u x", u=2),
                 scalar=stat(n, "gain", i), in1=shape_ps[:, i, :].rearrange("q (u x) -> q u x", u=2),
                 op0=ALU.mult, op1=ALU.add)
@@ -352,16 +354,17 @@ def tile_causalshapedattention_pa_t_kernel(tc, q, k, v, alpha, beta, gamma, out)
             if i > 0 and i not in VECTOR_ROWS and not all_on_vector(r // BATCH):
                 normalise(nc.scalar if i in SCALAR_ROWS else nc.gpsimd, n, i)
 
+        def bank_of(unit):
+            return [i for i, units in UNIT_BANKS.items() if unit in units][0]
+
         def all_on_vector(g):
             return g >= B * H * BATCHES - LAST_BATCHES
 
         def normalise(engine, n, i):
             st = job[n]
-            flat = a_sets[n % 2][:].rearrange("q u n x -> q u (n x)")
-            if i < HALF:
-                first, pos = 4 * BLOCK * UNIT_LOW[i], 0
-            else:
-                first, pos = 4 * BLOCK * UNIT_HIGH[i] + BLOCK * (NT - i), 1
+            bank = bank_of(UNIT_LOW[i])
+            flat = a_sets[n % 2][bank][:].rearrange("q u n x -> q u (n x)")
+            first, pos = (0, 0) if i < HALF else (BLOCK * (NT - i), 1)
             a_out = flat[:, :, first:first + BLOCK * i].rearrange("q u (j x) -> q u j x", x=BLOCK)
             e_in = st["e"][i][:, pos:pos + i, :].rearrange("q j (u x) -> q u j x", u=2)
             if engine is nc.scalar:
@@ -375,11 +378,10 @@ def tile_causalshapedattention_pa_t_kernel(tc, q, k, v, alpha, beta, gamma, out)
             if i in UNIT_BANKS:
                 units = UNIT_BANKS[i]
                 bank = psum_t.tile([P, len(units), 2, P], F32, name="bank")
-                words = a_sets[n % 2][:].rearrange("q u n x -> q (u n x)").bitcast(F32).rearrange(
-                    "q (u n w) -> q u n w", u=2, n=N_UNITS)
-                for m, unit in enumerate(units):
+                words = a_sets[n % 2][i][:].bitcast(F32)
+                for m in range(len(units)):
                     for u in range(2):
-                        nc.tensor.transpose(bank[:, m, u, :], words[:, u, unit, :], ident_f32[:])
+                        nc.tensor.transpose(bank[:, m, u, :], words[:, u, m, :], ident_f32[:])
                 job[n]["bank"][i] = bank
 
         def a_copy(r):
@@ -467,7 +469,6 @@ def tile_causalshapedattention_pa_t_kernel(tc, q, k, v, alpha, beta, gamma, out)
             if 0 <= r < n_rows:
                 stage(r)
 
-        ctx.enter_context(tc.manual_schedule(engines={mybir.EngineType.DVE, mybir.EngineType.Pool}))
         shape_parts = constants()
         for s in range(-4, n_rows + 20):
             run(score_row, s + 1)

@@ -41,7 +41,15 @@ LAST_BATCHES = 3
 VECTOR_ROWS = (3, 4)
 SCALAR_ROWS = ()
 WARM_ROWS = (0, 2)
-L_DIAG, L_ACOPY, L_OUT, L_EXP, L_NORM, L_AT, L_MUL = 8, 12, 17, 4, 8, 11, 16
+V_AHEAD = 5
+GAIN = 2
+QUANT = 5
+L_EXP = BATCH
+L_DIAG = L_NORM = BATCH * (GAIN + 1)
+L_AT = L_DIAG + 3
+L_ACOPY = L_AT + 1
+L_MUL = BATCH * (QUANT + 1)
+L_OUT = L_MUL + 1
 
 
 def tile_at(pos):
@@ -68,6 +76,7 @@ def tile_causalshapedattention_pa_t_kernel(tc, q, k, v, alpha, beta, gamma, out)
         raw = {}
         job = {}
         seq = {}
+        grouped_v = {}
 
         def load(b):
             q_sb = loads.tile([P, NT, C], BF16, name="q_sb")
@@ -239,7 +248,7 @@ def tile_causalshapedattention_pa_t_kernel(tc, q, k, v, alpha, beta, gamma, out)
                 v_grouped = heads.tile([P, PASSES, D, 4], BF16, name="v_grouped", align_bytes=64)
                 nc.gpsimd.tensor_scalar(out=v_grouped[:], in0=raw[b][2][:, :, :, cols].rearrange("p c t w -> p c w t"),
                                         scalar1=1.0, scalar2=0.0, op0=ALU.mult, op1=ALU.add)
-                job[n]["v_grouped"] = v_grouped
+                grouped_v[n] = v_grouped
 
         def quantise_v(n):
             b, h = divmod(n, H)
@@ -250,7 +259,7 @@ def tile_causalshapedattention_pa_t_kernel(tc, q, k, v, alpha, beta, gamma, out)
             nc.vector.quantize_mx(
                 out=v_codes[:, h].rearrange("p c w -> p (c w)").bitcast(FP8X4),
                 scales=v_scales[:, h].rearrange("p c w -> p (c w)"),
-                in_=job[n]["v_grouped"][:].rearrange("p c w t -> p (c w t)"),
+                in_=grouped_v[n][:].rearrange("p c w t -> p (c w t)"),
             )
             if h == H - 1:
                 for c, m in MASKS:
@@ -352,7 +361,7 @@ def tile_causalshapedattention_pa_t_kernel(tc, q, k, v, alpha, beta, gamma, out)
         def normalise_row(r):
             n, i, b, cols = place(r)
             if i > 0 and i not in VECTOR_ROWS and not all_on_vector(r // BATCH):
-                normalise(nc.scalar if i in SCALAR_ROWS else nc.gpsimd, n, i)
+                normalise(None if i in SCALAR_ROWS else nc.gpsimd, n, i)
 
         def bank_of(unit):
             return [i for i, units in UNIT_BANKS.items() if unit in units][0]
@@ -367,7 +376,7 @@ def tile_causalshapedattention_pa_t_kernel(tc, q, k, v, alpha, beta, gamma, out)
             first, pos = (0, 0) if i < HALF else (BLOCK * (NT - i), 1)
             a_out = flat[:, :, first:first + BLOCK * i].rearrange("q u (j x) -> q u j x", x=BLOCK)
             e_in = st["e"][i][:, pos:pos + i, :].rearrange("q j (u x) -> q u j x", u=2)
-            if engine is nc.scalar:
+            if engine is None:
                 nc.scalar.activation(out=a_out, in_=e_in, func=ACT.Identity, scale=stat(n, "gain", i), bias=below[:, i:i + 1])
             else:
                 engine.tensor_scalar(out=a_out, in0=e_in, scalar1=stat(n, "gain", i), scalar2=below[:, i:i + 1],
@@ -404,24 +413,25 @@ def tile_causalshapedattention_pa_t_kernel(tc, q, k, v, alpha, beta, gamma, out)
         def port_phase(x):
             def live(y):
                 return 0 <= y < B * H * BATCHES
-            if live(x - 3):
-                quantise_a(x - 3)
+            if live(x - QUANT):
+                quantise_a(x - QUANT)
             if live(x):
                 n, g = divmod(x, BATCHES)
                 nc.vector.tensor_scalar(out=job[n]["bias"][g][:], in0=job[n]["neg_max"][g][:],
                                         scalar1=scale, scalar2=EXP_SHIFT, op0=ALU.mult, op1=ALU.add)
-            if live(x - 1):
-                n, g = divmod(x - 1, BATCHES)
+            y = x - GAIN
+            if live(y):
+                n, g = divmod(y, BATCHES)
                 gain = job[n]["gain"][g]
                 nc.vector.reciprocal(out=gain[:], in_=job[n]["row_sum"][g][:])
-            if live(x - 2) and not all_on_vector(x - 2):
-                m, f = divmod(x - 2, BATCHES)
+            if live(y - 1) and not all_on_vector(y - 1):
+                m, f = divmod(y - 1, BATCHES)
                 for i in VECTOR_ROWS:
                     if i in ROWS[f]:
                         normalise(nc.vector, m, i)
-            if live(x - 1):
+            if live(y):
                 nc.vector.tensor_scalar(out=gain[:], in0=gain[:], scalar1=beta_bf[:, 0:1], scalar2=None, op0=ALU.mult)
-                if all_on_vector(x - 1):
+                if all_on_vector(y):
                     for i in ROWS[g]:
                         if i > 0:
                             normalise(nc.vector, n, i)
@@ -470,7 +480,7 @@ def tile_causalshapedattention_pa_t_kernel(tc, q, k, v, alpha, beta, gamma, out)
                 stage(r)
 
         shape_parts = constants()
-        for s in range(-4, n_rows + 20):
+        for s in range(-4, n_rows + L_OUT + 3):
             run(score_row, s + 1)
             run(max_first_bank, s)
             run(diagonal_tile, s - L_DIAG)
@@ -479,7 +489,7 @@ def tile_causalshapedattention_pa_t_kernel(tc, q, k, v, alpha, beta, gamma, out)
             run(out_copy, s - L_OUT)
             run(exp_row, s - L_EXP)
             run(normalise_row, s - L_NORM)
-            run(regroup_v, s + 1 if s > 2 else s - 2)
+            run(regroup_v, s + V_AHEAD if s > 2 else s - 2)
             run(a_transpose, s - L_AT)
             run(multiply_rows, s - L_MUL)
             run(k_transpose, s + 3)

@@ -37,13 +37,13 @@ BATCHES = NT // BATCH
 QUANT_CALLS = (((0, 4), (4, 1)), ((5, 4),))
 FAR_STEP = 12
 SHAPE_STEP = 4
-LAST_BATCHES = 3
-VECTOR_ROWS = (3, 4)
+LAST_BATCHES = 2
+VECTOR_ROWS = (4,)
 SCALAR_ROWS = ()
 WARM_ROWS = (0, 2)
 V_AHEAD = 5
 GAIN = 2
-QUANT = 5
+QUANT = 4
 L_EXP = BATCH
 L_DIAG = L_NORM = BATCH * (GAIN + 1)
 L_AT = L_DIAG + 3
@@ -307,7 +307,7 @@ def tile_causalshapedattention_pa_t_kernel(tc, q, k, v, alpha, beta, gamma, out)
                     first, last, on = NT - 1 - i, HALF, NT - 1 - i
                 s_ps = psum_s.tile([P, HALF, P], F32, name="s_ps")
                 keys = st["kT"][:, c * HALF:(c + 1) * HALF, :]
-                if i in WARM_ROWS:
+                if i in WARM_ROWS and r > 0:
                     nc.tensor.matmul(s_ps[:], lhsT=st["qT"][:, i, :], rhs=keys, start=True, stop=True)
                 nc.tensor.matmul(s_ps[:], lhsT=st["qT"][:, i, :], rhs=keys, start=True, stop=on is None)
                 if on is not None:
@@ -413,17 +413,17 @@ def tile_causalshapedattention_pa_t_kernel(tc, q, k, v, alpha, beta, gamma, out)
         def port_phase(x):
             def live(y):
                 return 0 <= y < B * H * BATCHES
-            if live(x - QUANT):
-                quantise_a(x - QUANT)
-            if live(x):
-                n, g = divmod(x, BATCHES)
-                nc.vector.tensor_scalar(out=job[n]["bias"][g][:], in0=job[n]["neg_max"][g][:],
-                                        scalar1=scale, scalar2=EXP_SHIFT, op0=ALU.mult, op1=ALU.add)
             y = x - GAIN
             if live(y):
                 n, g = divmod(y, BATCHES)
                 gain = job[n]["gain"][g]
                 nc.vector.reciprocal(out=gain[:], in_=job[n]["row_sum"][g][:])
+            if live(x - QUANT):
+                quantise_a(x - QUANT)
+            if live(x):
+                m, f = divmod(x, BATCHES)
+                nc.vector.tensor_scalar(out=job[m]["bias"][f][:], in0=job[m]["neg_max"][f][:],
+                                        scalar1=scale, scalar2=EXP_SHIFT, op0=ALU.mult, op1=ALU.add)
             if live(y - 1) and not all_on_vector(y - 1):
                 m, f = divmod(y - 1, BATCHES)
                 for i in VECTOR_ROWS:
@@ -435,7 +435,7 @@ def tile_causalshapedattention_pa_t_kernel(tc, q, k, v, alpha, beta, gamma, out)
                     for i in ROWS[g]:
                         if i > 0:
                             normalise(nc.vector, n, i)
-            if live(x) and x % BATCHES == 0:
+            if live(x) and x % BATCHES == 1:
                 quantise_v(x // BATCHES)
 
         def multiply_rows(r):
@@ -445,7 +445,10 @@ def tile_causalshapedattention_pa_t_kernel(tc, q, k, v, alpha, beta, gamma, out)
             v_codes, v_scales = seq[b]
             g, place_in_batch = at(i)
             if place_in_batch == 0:
-                st["o_ps"] = psum_o.tile([P, BATCH, P], F32, name="o_ps")
+                if r // BATCH >= B * H * BATCHES - 2:
+                    st["o_ps"] = psum_s.tile([P, BATCH, P], F32, name="s_ps")
+                else:
+                    st["o_ps"] = psum_o.tile([P, BATCH, P], F32, name="o_ps")
             passes = []
             for c in range(PASSES):
                 unit = (UNIT_LOW, UNIT_HIGH)[c][i]

@@ -39,7 +39,7 @@ FAR_STEP = 12
 SHAPE_STEP = 4
 LAST_BATCHES = 2
 VECTOR_ROWS = (4,)
-SCALAR_ROWS = ()
+SCALAR_ROWS = (3,)
 WARM_ROWS = (0, 2)
 V_AHEAD = 5
 GAIN = 2
@@ -397,8 +397,9 @@ def tile_causalshapedattention_pa_t_kernel(tc, q, k, v, alpha, beta, gamma, out)
             n, i, b, cols = place(r)
             if i in UNIT_BANKS:
                 units = UNIT_BANKS[i]
-                nc.scalar.copy(out=job[n]["grouped"][:, units[0]:units[-1] + 1].bitcast(F32),
-                               in_=job[n]["bank"][i][:].rearrange("p c u i -> p c i u"))
+                copy = nc.vector.tensor_copy if r == n_rows - 1 else nc.scalar.copy
+                copy(out=job[n]["grouped"][:, units[0]:units[-1] + 1].bitcast(F32),
+                     in_=job[n]["bank"][i][:].rearrange("p c u i -> p c i u"))
 
         def quantise_a(x):
             n, g = divmod(x, BATCHES)

@@ -37,13 +37,16 @@ BATCHES = NT // BATCH
 QUANT_CALLS = (((0, 4), (4, 1)), ((5, 4),))
 FAR_STEP = 12
 SHAPE_STEP = 4
+TAIL_A = (0, 4)
+TAIL_O = (4, 12)
 LAST_BATCHES = 2
+LAST_ORDER = ((3, 0, 6, 7), (2, 4, 1, 5))
 VECTOR_ROWS = (4,)
-SCALAR_ROWS = (3,)
+SCALAR_ROWS = ()
 WARM_ROWS = (0, 2)
 V_AHEAD = 5
 GAIN = 2
-QUANT = 4
+QUANT = 5
 L_EXP = BATCH
 L_DIAG = L_NORM = BATCH * (GAIN + 1)
 L_AT = L_DIAG + 3
@@ -67,9 +70,8 @@ def tile_causalshapedattention_pa_t_kernel(tc, q, k, v, alpha, beta, gamma, out)
         scores = ctx.enter_context(tc.tile_pool(name="scores", bufs=3))
         values = ctx.enter_context(tc.tile_pool(name="values", bufs=3))
         psum_s = ctx.enter_context(tc.psum_pool(name="psum_s", bufs=3))
-        psum_t = ctx.enter_context(tc.psum_pool(name="psum_t", bufs=2))
+        psum_t = ctx.enter_context(tc.psum_pool(name="psum_t", bufs=3))
         psum_o = ctx.enter_context(tc.psum_pool(name="psum_o", bufs=1))
-        psum_qk = ctx.enter_context(tc.psum_pool(name="psum_qk", bufs=1))
         psum_shape = ctx.enter_context(tc.psum_pool(name="psum_shape", bufs=1))
 
         ctx.enter_context(tc.manual_schedule(engines={mybir.EngineType.DVE, mybir.EngineType.Pool}))
@@ -279,7 +281,7 @@ def tile_causalshapedattention_pa_t_kernel(tc, q, k, v, alpha, beta, gamma, out)
                 if first_of_sequence(r) and b + 1 < B:
                     load(b + 1)
                 open_job(n)
-                bank = psum_qk.tile([P, NT, P], BF16, name="qk_ps")
+                bank = psum_t.tile([P, NT, P], BF16, name="bank")
                 transpose_qk(n, bank, raw[b][0], cols, ident_bf, job[n]["qT"], lambda t: t)
 
         def k_transpose(r):
@@ -288,7 +290,7 @@ def tile_causalshapedattention_pa_t_kernel(tc, q, k, v, alpha, beta, gamma, out)
                 if n == 0:
                     bank = psum_t.tile([P, NT, P], BF16, name="bank")
                 else:
-                    bank = psum_qk.tile([P, NT, P], BF16, name="qk_ps")
+                    bank = psum_t.tile([P, NT, P], BF16, name="bank")
                 transpose_qk(n, bank, raw[b][1], cols, key_perm, job[n]["kT"], tile_at)
 
         def score_row(r):
@@ -344,7 +346,12 @@ def tile_causalshapedattention_pa_t_kernel(tc, q, k, v, alpha, beta, gamma, out)
         def diagonal_tile(r):
             n, i, b, cols = place(r)
             st = job[n]
-            if i == 0:
+            if not all_on_vector(r // BATCH):
+                diagonal(n, i)
+
+        def diagonal(n, i):
+            st = job[n]
+            if "grouped" not in st:
                 st["grouped"] = heads.tile([P, N_UNITS, P, 4], BF16, name="grouped", align_bytes=64)
                 st["codes"] = heads.tile([P, N_UNITS, P], U32, name="codes", align_bytes=64)
                 st["scales"] = heads.tile([P, N_UNITS, P], U8, name="scales", align_bytes=64)
@@ -397,19 +404,24 @@ def tile_causalshapedattention_pa_t_kernel(tc, q, k, v, alpha, beta, gamma, out)
             n, i, b, cols = place(r)
             if i in UNIT_BANKS:
                 units = UNIT_BANKS[i]
-                copy = nc.vector.tensor_copy if r == n_rows - 1 else nc.scalar.copy
+                copy = nc.vector.tensor_copy if n_rows - 1 - r in TAIL_A else nc.scalar.copy
                 copy(out=job[n]["grouped"][:, units[0]:units[-1] + 1].bitcast(F32),
                      in_=job[n]["bank"][i][:].rearrange("p c u i -> p c i u"))
 
         def quantise_a(x):
             n, g = divmod(x, BATCHES)
             st = job[n]
-            for first, units in QUANT_CALLS[g]:
+            for first, units in QUANT_CALLS[g] if x < B * H * BATCHES - 1 else ((5, 2), (7, 2)):
                 nc.vector.quantize_mx(
                     out=st["codes"][:, first:first + units].rearrange("p n i -> p (n i)").bitcast(FP8X4),
                     scales=st["scales"][:, first:first + units].rearrange("p n i -> p (n i)"),
                     in_=st["grouped"][:, first:first + units].rearrange("p n i t -> p (n i t)"),
                 )
+
+        def make_bias(x):
+            n, g = divmod(x, BATCHES)
+            nc.vector.tensor_scalar(out=job[n]["bias"][g][:], in0=job[n]["neg_max"][g][:],
+                                    scalar1=scale, scalar2=EXP_SHIFT, op0=ALU.mult, op1=ALU.add)
 
         def port_phase(x):
             def live(y):
@@ -419,12 +431,12 @@ def tile_causalshapedattention_pa_t_kernel(tc, q, k, v, alpha, beta, gamma, out)
                 n, g = divmod(y, BATCHES)
                 gain = job[n]["gain"][g]
                 nc.vector.reciprocal(out=gain[:], in_=job[n]["row_sum"][g][:])
+            if live(x) and not live(x + 1):
+                make_bias(x)
             if live(x - QUANT):
                 quantise_a(x - QUANT)
-            if live(x):
-                m, f = divmod(x, BATCHES)
-                nc.vector.tensor_scalar(out=job[m]["bias"][f][:], in0=job[m]["neg_max"][f][:],
-                                        scalar1=scale, scalar2=EXP_SHIFT, op0=ALU.mult, op1=ALU.add)
+            if live(x) and live(x + 1):
+                make_bias(x)
             if live(y - 1) and not all_on_vector(y - 1):
                 m, f = divmod(y - 1, BATCHES)
                 for i in VECTOR_ROWS:
@@ -433,9 +445,10 @@ def tile_causalshapedattention_pa_t_kernel(tc, q, k, v, alpha, beta, gamma, out)
             if live(y):
                 nc.vector.tensor_scalar(out=gain[:], in0=gain[:], scalar1=beta_bf[:, 0:1], scalar2=None, op0=ALU.mult)
                 if all_on_vector(y):
-                    for i in ROWS[g]:
+                    for i in LAST_ORDER[g]:
                         if i > 0:
                             normalise(nc.vector, n, i)
+                        diagonal(n, i)
             if live(x) and x % BATCHES == 1:
                 quantise_v(x // BATCHES)
 
@@ -473,8 +486,9 @@ def tile_causalshapedattention_pa_t_kernel(tc, q, k, v, alpha, beta, gamma, out)
             n, i, b, cols = place(r)
             g, m = at(i)
             if m == BATCH - 1:
-                out_sb = heads.tile([P, BATCH, D], F32, name="out_sb")
-                nc.scalar.copy(out=out_sb[:], in_=job[n]["o_ps"][:])
+                out_sb = long_lived.tile([P, BATCH, D], F32, name="out_sb")
+                copy = nc.vector.tensor_copy if n_rows - 1 - r in TAIL_O else nc.scalar.copy
+                copy(out=out_sb[:], in_=job[n]["o_ps"][:])
                 rows = out[b, :, cols].rearrange("(n p) c -> p n c", p=P)
                 for first, tiles in (((0, slice(0, 7, 3)), (3, slice(7, 8))) if g == 0 else ((0, slice(1, 3)), (2, slice(4, 6)))):
                     nc.sync.dma_start(out=rows[:, tiles, :], in_=out_sb[:, first:first + (3 if first == 0 and g == 0 else 2 if g == 1 else 1), :])

@@ -37,6 +37,7 @@ BATCHES = NT // BATCH
 QUANT_CALLS = (((0, 4), (4, 1)), ((5, 4),))
 FAR_STEP = 12
 SHAPE_STEP = 4
+EARLY = 2
 TAIL_A = (0, 4)
 TAIL_O = (4, 12)
 LAST_BATCHES = 2
@@ -122,13 +123,14 @@ def tile_causalshapedattention_pa_t_kernel(tc, q, k, v, alpha, beta, gamma, out)
             out=lower_nat[:], in_=lower_nat[:], compare_op=ALU.is_ge, fill=0.0,
             base=0, pattern=[[-1, P]], channel_multiplier=1,
         )
+        ident_f32 = const.tile([P, P], F32)
+        make_identity(nc, ident_f32[:])
         lower = const.tile([P, P], F32)
         to_key_order(lower, lower_nat)
         mask_add = const.tile([P, P], BF16)
         nc.vector.tensor_scalar(out=mask_add[:], in0=lower[:], scalar1=-MASKED, scalar2=MASKED,
                                 op0=ALU.mult, op1=ALU.add)
 
-        ident_f32 = const.tile([P, P], F32)
         above = const.tile([P, NT], F32)
         above_pair = const.tile([P, NT, 2], BF16)
         below = const.tile([P, NT], F32)
@@ -169,7 +171,6 @@ def tile_causalshapedattention_pa_t_kernel(tc, q, k, v, alpha, beta, gamma, out)
                                     op0=ALU.mult)
             for e in range(2):
                 nc.vector.tensor_copy(out=above_pair[:, :, e], in_=above[:])
-            nc.vector.memset(v_masked[:].rearrange("p s m h w -> p (s m h w)"), 0)
             return step_down, alpha_diag
 
         def shape_constants(step_down, alpha_diag):
@@ -179,7 +180,6 @@ def tile_causalshapedattention_pa_t_kernel(tc, q, k, v, alpha, beta, gamma, out)
             for i in range(NT):
                 nc.tensor.matmul(shape_ps[:, i, :], lhsT=ident_bf[:], rhs=shape_bf[:, i, :], start=True, stop=False)
                 nc.tensor.matmul(shape_ps[:, i, :], lhsT=ident_bf[:], rhs=alpha_diag[:], start=False, stop=True)
-            make_identity(nc, ident_f32[:])
 
         def far_index(c, i):
             return i if c == 0 else HALF - 1 + i
@@ -418,10 +418,15 @@ def tile_causalshapedattention_pa_t_kernel(tc, q, k, v, alpha, beta, gamma, out)
                     in_=st["grouped"][:, first:first + units].rearrange("p n i t -> p (n i t)"),
                 )
 
-        def make_bias(x):
+        def make_bias(x, first=0, last=BATCH):
             n, g = divmod(x, BATCHES)
-            nc.vector.tensor_scalar(out=job[n]["bias"][g][:], in0=job[n]["neg_max"][g][:],
+            nc.vector.tensor_scalar(out=job[n]["bias"][g][:, first:last], in0=job[n]["neg_max"][g][:, first:last],
                                     scalar1=scale, scalar2=EXP_SHIFT, op0=ALU.mult, op1=ALU.add)
+
+        def early_bias(r):
+            x, m = divmod(r, BATCH)
+            if x < EARLY and m > 0:
+                make_bias(x, m - 1, m)
 
         def port_phase(x):
             def live(y):
@@ -436,7 +441,7 @@ def tile_causalshapedattention_pa_t_kernel(tc, q, k, v, alpha, beta, gamma, out)
             if live(x - QUANT):
                 quantise_a(x - QUANT)
             if live(x) and live(x + 1):
-                make_bias(x)
+                make_bias(x, BATCH - 1 if x < EARLY else 0)
             if live(y - 1) and not all_on_vector(y - 1):
                 m, f = divmod(y - 1, BATCHES)
                 for i in VECTOR_ROWS:
@@ -503,19 +508,23 @@ def tile_causalshapedattention_pa_t_kernel(tc, q, k, v, alpha, beta, gamma, out)
             run(max_first_bank, s)
             run(diagonal_tile, s - L_DIAG)
             run(max_second_bank, s)
+            run(early_bias, s)
             run(a_copy, s - L_ACOPY)
             run(out_copy, s - L_OUT)
             run(exp_row, s - L_EXP)
             run(normalise_row, s - L_NORM)
             run(regroup_v, s + V_AHEAD if s > 2 else s - 2)
             run(a_transpose, s - L_AT)
-            run(multiply_rows, s - L_MUL)
+            if s % BATCH == BATCH - 1:
+                for m in reversed(range(BATCH)):
+                    run(multiply_rows, s - m - L_MUL)
             run(k_transpose, s + 3)
             run(q_transpose, s + 4)
             if s == SHAPE_STEP:
                 shape_constants(*shape_parts)
             if s == 2:
                 nc.gpsimd.memset(far_grouped[:].rearrange("p n i t -> p (n i t)").bitcast(F32), 0.0)
+                nc.gpsimd.memset(v_masked[:].rearrange("p s m h w -> p (s m h w)").bitcast(F32), 0.0)
             if s == FAR_STEP:
                 far_units()
             if s == FAR_STEP + 3:

@@ -37,7 +37,6 @@ BATCHES = NT // BATCH
 QUANT_CALLS = (((0, 4), (4, 1)), ((5, 4),))
 FAR_STEP = 12
 SHAPE_STEP = 4
-EARLY = 2
 TAIL_A = (0, 4)
 TAIL_O = (4, 12)
 LAST_BATCHES = 2
@@ -247,25 +246,22 @@ def tile_causalshapedattention_pa_t_kernel(tc, q, k, v, alpha, beta, gamma, out)
         def regroup_v(r):
             n, i, b, cols = place(r)
             if i == 0:
-                v_grouped = heads.tile([P, PASSES, D, 4], BF16, name="v_grouped", align_bytes=64)
-                nc.gpsimd.tensor_scalar(out=v_grouped[:], in0=raw[b][2][:, :, :, cols].rearrange("p c t w -> p c w t"),
+                if n % H == 0:
+                    grouped_v[b] = heads.tile([P, H, PASSES, D, 4], BF16, name="v_grouped", align_bytes=64)
+                nc.gpsimd.tensor_scalar(out=grouped_v[b][:, n % H], in0=raw[b][2][:, :, :, cols].rearrange("p c t w -> p c w t"),
                                         scalar1=1.0, scalar2=0.0, op0=ALU.mult, op1=ALU.add)
-                grouped_v[n] = v_grouped
 
-        def quantise_v(n):
-            b, h = divmod(n, H)
-            if h == 0:
-                seq[b] = (long_lived.tile([P, H, PASSES, D], I32, name="v_codes", align_bytes=64),
-                          long_lived.tile([P, H, PASSES, D], U8, name="v_scales", align_bytes=64))
-            v_codes, v_scales = seq[b]
+        def quantise_v(b):
+            v_codes = long_lived.tile([P, H, PASSES, D], I32, name="v_codes", align_bytes=64)
+            v_scales = long_lived.tile([P, H, PASSES, D], U8, name="v_scales", align_bytes=64)
+            seq[b] = (v_codes, v_scales)
             nc.vector.quantize_mx(
-                out=v_codes[:, h].rearrange("p c w -> p (c w)").bitcast(FP8X4),
-                scales=v_scales[:, h].rearrange("p c w -> p (c w)"),
-                in_=grouped_v[n][:].rearrange("p c w t -> p (c w t)"),
+                out=v_codes[:].rearrange("p h c w -> p (h c w)").bitcast(FP8X4),
+                scales=v_scales[:].rearrange("p h c w -> p (h c w)"),
+                in_=grouped_v[b][:].rearrange("p h c w t -> p (h c w t)"),
             )
-            if h == H - 1:
-                for c, m in MASKS:
-                    nc.sync.dma_start(out=v_masked[kept(c, m), b % 2, MASKS.index((c, m))], in_=v_codes[kept(c, m), :, c, :])
+            for c, m in MASKS:
+                nc.sync.dma_start(out=v_masked[kept(c, m), b % 2, MASKS.index((c, m))], in_=v_codes[kept(c, m), :, c, :])
 
         def transpose_qk(n, bank, src, cols, moving, dst, tile_of):
             step = NT // 2 if n == 0 else NT
@@ -418,15 +414,11 @@ def tile_causalshapedattention_pa_t_kernel(tc, q, k, v, alpha, beta, gamma, out)
                     in_=st["grouped"][:, first:first + units].rearrange("p n i t -> p (n i t)"),
                 )
 
-        def make_bias(x, first=0, last=BATCH):
+        def make_bias(x):
             n, g = divmod(x, BATCHES)
-            nc.vector.tensor_scalar(out=job[n]["bias"][g][:, first:last], in0=job[n]["neg_max"][g][:, first:last],
+            nc.vector.tensor_scalar(out=job[n]["bias"][g][:], in0=job[n]["neg_max"][g][:],
                                     scalar1=scale, scalar2=EXP_SHIFT, op0=ALU.mult, op1=ALU.add)
 
-        def early_bias(r):
-            x, m = divmod(r, BATCH)
-            if x < EARLY and m > 0:
-                make_bias(x, m - 1, m)
 
         def port_phase(x):
             def live(y):
@@ -441,7 +433,7 @@ def tile_causalshapedattention_pa_t_kernel(tc, q, k, v, alpha, beta, gamma, out)
             if live(x - QUANT):
                 quantise_a(x - QUANT)
             if live(x) and live(x + 1):
-                make_bias(x, BATCH - 1 if x < EARLY else 0)
+                make_bias(x)
             if live(y - 1) and not all_on_vector(y - 1):
                 m, f = divmod(y - 1, BATCHES)
                 for i in VECTOR_ROWS:
@@ -454,8 +446,8 @@ def tile_causalshapedattention_pa_t_kernel(tc, q, k, v, alpha, beta, gamma, out)
                         if i > 0:
                             normalise(nc.vector, n, i)
                         diagonal(n, i)
-            if live(x) and x % BATCHES == 1:
-                quantise_v(x // BATCHES)
+            if live(x) and x % (H * BATCHES) == H * BATCHES - 1:
+                quantise_v(x // (H * BATCHES))
 
         def multiply_rows(r):
             n, i, b, cols = place(r)
@@ -503,23 +495,22 @@ def tile_causalshapedattention_pa_t_kernel(tc, q, k, v, alpha, beta, gamma, out)
                 stage(r)
 
         shape_parts = constants()
-        for s in range(-4, n_rows + L_OUT + 3):
+        for s in range(-5, n_rows + L_OUT + 3):
+            if s % BATCH == BATCH - 1:
+                for m in reversed(range(BATCH)):
+                    run(multiply_rows, s - m - L_MUL)
+            run(a_transpose, s - L_AT)
             run(score_row, s + 1)
             run(max_first_bank, s)
             run(diagonal_tile, s - L_DIAG)
             run(max_second_bank, s)
-            run(early_bias, s)
             run(a_copy, s - L_ACOPY)
             run(out_copy, s - L_OUT)
             run(exp_row, s - L_EXP)
             run(normalise_row, s - L_NORM)
             run(regroup_v, s + V_AHEAD if s > 2 else s - 2)
-            run(a_transpose, s - L_AT)
-            if s % BATCH == BATCH - 1:
-                for m in reversed(range(BATCH)):
-                    run(multiply_rows, s - m - L_MUL)
-            run(k_transpose, s + 3)
-            run(q_transpose, s + 4)
+            run(q_transpose, s + 5)
+            run(k_transpose, s + 5)
             if s == SHAPE_STEP:
                 shape_constants(*shape_parts)
             if s == 2:

from contextlib import ExitStack
import math

import concourse.mybir as mybir
from concourse.masks import make_identity

F32 = mybir.dt.float32
BF16 = mybir.dt.bfloat16
I32 = mybir.dt.int32
U32 = mybir.dt.uint32
U8 = mybir.dt.uint8
FP8X4 = mybir.dt.float8_e4m3fn_x4
ALU = mybir.AluOpType
ACT = mybir.ActivationFunctionType

B, T, C, H = 8, 1024, 256, 2
D = C // H
P = 128
NT = T // P
K_PASS = 4 * P
PASSES = T // K_PASS
HALF = NT // PASSES
QUAD = 32
BLOCK = P // 2
BANK = 512
MASKED = -1e20
EXP_SHIFT = 10.1
FLOPS = 2 * 2 * B * H * T * T * D

UNIT_LOW = (1, 7, 5, 0, 6, 8, 2, 4)
UNIT_HIGH = (None, None, None, None, 5, 7, 1, 3)
N_UNITS = 9
UNIT_BANKS = {3: (0,), 6: (1, 2), 7: (3, 4), 4: (5, 6), 5: (7, 8)}
ROWS = ((0, 3, 6, 7), (1, 2, 4, 5))
BATCH = 4
BATCHES = NT // BATCH
QUANT_CALLS = (((0, 4), (4, 1)), ((5, 4),))
FAR_STEP = 12
SHAPE_STEP = 4
TAIL_A = (0, 4)
TAIL_O = (4, 12)
LAST_BATCHES = 2
LAST_ORDER = ((3, 0, 6, 7), (2, 4, 1, 5))
VECTOR_ROWS = (4,)
SCALAR_ROWS = ()
WARM_ROWS = (0, 2)
V_AHEAD = 5
GAIN = 2
QUANT = 5
L_EXP = BATCH
L_DIAG = L_NORM = BATCH * (GAIN + 1)
L_AT = L_DIAG + 3
L_ACOPY = L_AT + 1
L_MUL = BATCH * (QUANT + 1)
L_OUT = L_MUL + 1


def tile_at(pos):
    return pos if pos < HALF else NT + HALF - 1 - pos


def tile_causalshapedattention_pa_t_kernel(tc, q, k, v, alpha, beta, gamma, out):
    nc = tc.nc
    scale = 1.0 / math.sqrt(D)
    with ExitStack() as ctx:
        const = ctx.enter_context(tc.tile_pool(name="const", bufs=1))
        loads = ctx.enter_context(tc.tile_pool(name="loads", bufs=2))
        heads = ctx.enter_context(tc.tile_pool(name="heads", bufs=2))
        long_lived = ctx.enter_context(tc.tile_pool(name="long_lived", bufs=4))
        scores = ctx.enter_context(tc.tile_pool(name="scores", bufs=3))
        values = ctx.enter_context(tc.tile_pool(name="values", bufs=3))
        psum_s = ctx.enter_context(tc.psum_pool(name="psum_s", bufs=3))
        psum_t = ctx.enter_context(tc.psum_pool(name="psum_t", bufs=3))
        psum_o = ctx.enter_context(tc.psum_pool(name="psum_o", bufs=1))
        psum_shape = ctx.enter_context(tc.psum_pool(name="psum_shape", bufs=1))

        ctx.enter_context(tc.manual_schedule(engines={mybir.EngineType.DVE, mybir.EngineType.Pool}))
        raw = {}
        job = {}
        seq = {}
        grouped_v = {}

        def load(b):
            q_sb = loads.tile([P, NT, C], BF16, name="q_sb")
            k_sb = loads.tile([P, NT, C], BF16, name="k_sb")
            v_sb = values.tile([P, PASSES, 4, C], BF16, name="v_sb")
            for first in range(0, NT, NT // 2):
                tiles = slice(first, first + NT // 2)
                rows = slice(first * P, (first + NT // 2) * P)
                nc.sync.dma_start(out=q_sb[:, tiles, :], in_=q[b, rows, :].rearrange("(n p) c -> p n c", p=P))
                nc.sync.dma_start(out=k_sb[:, tiles, :], in_=k[b, rows, :].rearrange("(n p) c -> p n c", p=P))
            nc.sync.dma_start(out=v_sb[:, 0], in_=v[b, :K_PASS, :].rearrange("(p t) w -> p t w", t=4))
            for j in range(HALF, NT):
                quad = slice(QUAD * (NT - 1 - j), QUAD * (NT - j))
                nc.sync.dma_start(out=v_sb[quad, 1], in_=v[b, j * P:(j + 1) * P, :].rearrange("(p t) w -> p t w", t=4))
            raw[b] = (q_sb, k_sb, v_sb)

        alpha_bf = const.tile([P, 1], BF16)
        beta_bf = const.tile([P, 1], BF16)
        gamma_bf = const.tile([P, 1], BF16)
        nc.scalar.dma_start(out=gamma_bf[:], in_=gamma.partition_broadcast(P))
        nc.scalar.dma_start(out=alpha_bf[:], in_=alpha.partition_broadcast(P))
        nc.scalar.dma_start(out=beta_bf[:], in_=beta.partition_broadcast(P))
        load(0)

        def to_key_order(dst, src):
            nc.vector.tensor_copy(
                out=dst[:].rearrange("k (u p e) -> k u p e", u=2, e=2),
                in_=src[:].rearrange("k (p u e) -> k u p e", u=2, e=2),
            )

        ident_bf = const.tile([P, P], BF16)
        make_identity(nc, ident_bf[:])
        key_perm = const.tile([P, P], BF16)
        to_key_order(key_perm, ident_bf)
        row_f = const.tile([P, NT], F32)
        nc.gpsimd.iota(row_f[:], pattern=[[P, NT]], base=0, channel_multiplier=1,
                       allow_small_or_imprecise_dtypes=True)
        lower_nat = const.tile([P, P], F32)
        nc.gpsimd.memset(lower_nat[:], 1.0)
        nc.gpsimd.affine_select(
            out=lower_nat[:], in_=lower_nat[:], compare_op=ALU.is_ge, fill=0.0,
            base=0, pattern=[[-1, P]], channel_multiplier=1,
        )
        ident_f32 = const.tile([P, P], F32)
        make_identity(nc, ident_f32[:])
        lower = const.tile([P, P], F32)
        to_key_order(lower, lower_nat)
        mask_add = const.tile([P, P], BF16)
        nc.vector.tensor_scalar(out=mask_add[:], in0=lower[:], scalar1=-MASKED, scalar2=MASKED,
                                op0=ALU.mult, op1=ALU.add)

        above = const.tile([P, NT], F32)
        above_pair = const.tile([P, NT, 2], BF16)
        below = const.tile([P, NT], F32)
        shape_bf = const.tile([P, NT, P], BF16)
        shape_ps = psum_shape.tile([P, NT, P], BF16)
        a_sets = [{i: const.tile([P, 2, len(units), 4 * BLOCK], BF16, name="a%d_%d" % (s, i)) for i, units in UNIT_BANKS.items()}
                  for s in range(2)]
        n_far = NT + HALF - 2
        far_grouped = const.tile([P, n_far, P, 4], BF16, align_bytes=64)
        far_codes = const.tile([P, n_far, P], U32, align_bytes=64)
        far_scales = const.tile([P, n_far, P], U8, align_bytes=64)
        MASKS = [(c, m) for c in range(PASSES) for m in range(1, HALF)]
        v_masked = const.tile([P, 2, len(MASKS), H, D], I32, align_bytes=64)

        def kept(c, m):
            return slice(0, QUAD * m) if c == 0 else slice(P - QUAD * m, P)

        def constants():
            is_last = const.tile([P, NT], F32)
            nc.vector.tensor_scalar(out=is_last[:], in0=row_f[:], scalar1=float(T - 1), scalar2=None, op0=ALU.is_equal)
            spread = const.tile([P, NT], F32)
            nc.vector.tensor_scalar(out=spread[:], in0=row_f[:], scalar1=-1.0, scalar2=float(T - 1),
                                    op0=ALU.mult, op1=ALU.add)
            nc.vector.scalar_tensor_tensor(out=spread[:], in0=is_last[:], scalar=float(T), in1=spread[:],
                                           op0=ALU.mult, op1=ALU.add)
            nc.vector.reciprocal(out=spread[:], in_=spread[:])
            alpha_f = const.tile([P, 1], F32)
            gamma_f = const.tile([P, 1], F32)
            nc.vector.tensor_copy(out=gamma_f[:], in_=gamma_bf[:])
            nc.vector.tensor_scalar(out=above[:], in0=spread[:], scalar1=gamma_f[:, 0:1], scalar2=-1.0,
                                    op0=ALU.mult, op1=ALU.mult)
            nc.vector.tensor_copy(out=alpha_f[:], in_=alpha_bf[:])
            nc.vector.tensor_tensor(out=below[:], in0=above[:], in1=is_last[:], op=ALU.mult)
            step_down = const.tile([P, NT], F32)
            nc.vector.tensor_tensor(out=step_down[:], in0=below[:], in1=above[:], op=ALU.subtract)
            alpha_diag = const.tile([P, P], BF16)
            nc.vector.tensor_scalar(out=alpha_diag[:], in0=key_perm[:], scalar1=alpha_f[:, 0:1], scalar2=None,
                                    op0=ALU.mult)
            for e in range(2):
                nc.vector.tensor_copy(out=above_pair[:, :, e], in_=above[:])
            return step_down, alpha_diag

        def shape_constants(step_down, alpha_diag):
            for i in range(NT):
                nc.scalar.activation(out=shape_bf[:, i, :], in_=lower[:], func=ACT.Identity,
                                     bias=above[:, i:i + 1], scale=step_down[:, i:i + 1])
            for i in range(NT):
                nc.tensor.matmul(shape_ps[:, i, :], lhsT=ident_bf[:], rhs=shape_bf[:, i, :], start=True, stop=False)
                nc.tensor.matmul(shape_ps[:, i, :], lhsT=ident_bf[:], rhs=alpha_diag[:], start=False, stop=True)

        def far_index(c, i):
            return i if c == 0 else HALF - 1 + i

        def far_units():
            words = above_pair[:].rearrange("p n e -> p (n e)").bitcast(F32)
            grouped = far_grouped[:].rearrange("p n i t -> p n (i t)").bitcast(F32).rearrange("p n (i u) -> p n i u", u=2)
            for first in range(0, NT, HALF):
                rows = range(first, min(first + HALF, NT - 1))
                bank = psum_t.tile([P, HALF, P], F32, name="bank")
                for i in rows:
                    nc.tensor.transpose(bank[:, i - first, :], words[:, i:i + 1].to_broadcast([P, P]), ident_f32[:])
                for i in rows:
                    for c in range(PASSES):
                        if c == 0:
                            quads = range(i + 1, HALF)
                        else:
                            quads = range(0, min(HALF, NT - 1 - i))
                        for a, z in spans(quads):
                            parts = slice(QUAD * a, QUAD * z)
                            nc.scalar.copy(out=grouped[parts, far_index(c, i)],
                                           in_=bank[parts, i - first, :].unsqueeze(2).to_broadcast([QUAD * (z - a), P, 2]))

        def far_quantise():
            for first, n in ((0, 8), (8, 2)):
                nc.vector.quantize_mx(
                    out=far_codes[:, first:first + n].rearrange("p n i -> p (n i)").bitcast(FP8X4),
                    scales=far_scales[:, first:first + n].rearrange("p n i -> p (n i)"),
                    in_=far_grouped[:, first:first + n].rearrange("p n i t -> p (n i t)"),
                )

        def spans(quads):
            if len(quads) == 0:
                return []
            a, z = quads[0], quads[-1] + 1
            return [(1, 2), (2, z)] if a == 1 and z > 2 else [(a, z)]

        n_rows = B * H * NT

        def place(r):
            n, m = divmod(r, NT)
            b, h = divmod(n, H)
            return n, ROWS[m // BATCH][m % BATCH], b, slice(h * D, (h + 1) * D)

        def at(i):
            g = 0 if i in ROWS[0] else 1
            return g, ROWS[g].index(i)

        def first_of_sequence(r):
            return r % (H * NT) == 0

        def open_job(n):
            job[n] = {
                "s": {}, "e": {}, "bank": {},
                "qT": heads.tile([P, NT, P], BF16, name="qT"),
                "kT": heads.tile([P, NT, P], BF16, name="kT"),
            }
            for name in ("neg_max", "neg_max_half", "row_sum", "bias", "gain"):
                job[n][name] = [long_lived.tile([P, BATCH], F32, name="%s%d" % (name, g)) for g in range(BATCHES)]

        def stat(n, name, i):
            g, m = at(i)
            return job[n][name][g][:, m:m + 1]

        def regroup_v(r):
            n, i, b, cols = place(r)
            if i == 0:
                if n % H == 0:
                    grouped_v[b] = heads.tile([P, H, PASSES, D, 4], BF16, name="v_grouped", align_bytes=64)
                nc.gpsimd.tensor_scalar(out=grouped_v[b][:, n % H], in0=raw[b][2][:, :, :, cols].rearrange("p c t w -> p c w t"),
                                        scalar1=1.0, scalar2=0.0, op0=ALU.mult, op1=ALU.add)

        def quantise_v(b):
            v_codes = long_lived.tile([P, H, PASSES, D], I32, name="v_codes", align_bytes=64)
            v_scales = long_lived.tile([P, H, PASSES, D], U8, name="v_scales", align_bytes=64)
            seq[b] = (v_codes, v_scales)
            nc.vector.quantize_mx(
                out=v_codes[:].rearrange("p h c w -> p (h c w)").bitcast(FP8X4),
                scales=v_scales[:].rearrange("p h c w -> p (h c w)"),
                in_=grouped_v[b][:].rearrange("p h c w t -> p (h c w t)"),
            )
            for c, m in MASKS:
                nc.sync.dma_start(out=v_masked[kept(c, m), b % 2, MASKS.index((c, m))], in_=v_codes[kept(c, m), :, c, :])

        def transpose_qk(n, bank, src, cols, moving, dst, tile_of):
            step = NT // 2 if n == 0 else NT
            for first in range(0, NT, step):
                for t in range(first, first + step):
                    nc.tensor.transpose(bank[:, t, :], src[:, tile_of(t), cols], moving[:])
                nc.scalar.copy(out=dst[:, first:first + step, :].bitcast(F32),
                               in_=bank[:, first:first + step, :].bitcast(F32))

        def q_transpose(r):
            n, i, b, cols = place(r)
            if i == 0:
                if first_of_sequence(r) and b + 1 < B:
                    load(b + 1)
                open_job(n)
                bank = psum_t.tile([P, NT, P], BF16, name="bank")
                transpose_qk(n, bank, raw[b][0], cols, ident_bf, job[n]["qT"], lambda t: t)

        def k_transpose(r):
            n, i, b, cols = place(r)
            if i == 0:
                if n == 0:
                    bank = psum_t.tile([P, NT, P], BF16, name="bank")
                else:
                    bank = psum_t.tile([P, NT, P], BF16, name="bank")
                transpose_qk(n, bank, raw[b][1], cols, key_perm, job[n]["kT"], tile_at)

        def score_row(r):
            n, i, b, cols = place(r)
            st = job[n]
            st["s"][i] = []
            for c in reversed(range(PASSES)):
                if c == 1 and i < HALF:
                    continue
                own = c == i // HALF
                if not own:
                    first, last, on = 0, HALF, None
                elif c == 0:
                    first, last, on = 0, i + 1, i
                else:
                    first, last, on = NT - 1 - i, HALF, NT - 1 - i
                s_ps = psum_s.tile([P, HALF, P], F32, name="s_ps")
                keys = st["kT"][:, c * HALF:(c + 1) * HALF, :]
                if i in WARM_ROWS and r > 0:
                    nc.tensor.matmul(s_ps[:], lhsT=st["qT"][:, i, :], rhs=keys, start=True, stop=True)
                nc.tensor.matmul(s_ps[:], lhsT=st["qT"][:, i, :], rhs=keys, start=True, stop=on is None)
                if on is not None:
                    nc.tensor.matmul(s_ps[:, on, :], lhsT=ident_bf[:], rhs=mask_add[:], start=False, stop=True)
                st["s"][i].append((s_ps[:, first:last, :], last - first))

        def max_bank(r, m):
            n, i, b, cols = place(r)
            st = job[n]
            banks = st["s"][i]
            if m == 0:
                st["e"][i] = scores.tile([P, i + 1, P], F32, name="e%d" % i)
            if m < len(banks):
                dest = stat(n, "neg_max" if m == len(banks) - 1 else "neg_max_half", i)
                done = sum(width for view, width in banks[:m])
                view, width = banks[m]
                nc.vector.tensor_scalar(out=st["e"][i][:, done:done + width, :],
                                        in0=view, scalar1=-1.0,
                                        scalar2=stat(n, "neg_max_half", i) if m > 0 else None,
                                        op0=ALU.mult, op1=ALU.min, accum_out=dest)

        def max_first_bank(r):
            max_bank(r, 0)

        def max_second_bank(r):
            max_bank(r, 1)

        def exp_row(r):
            n, i, b, cols = place(r)
            st = job[n]
            nc.scalar.activation(out=st["e"][i][:], in_=st["e"][i][:], func=ACT.Exp,
                                 bias=stat(n, "bias", i), scale=-scale, accum_out=stat(n, "row_sum", i))

        def diagonal_tile(r):
            n, i, b, cols = place(r)
            st = job[n]
            if not all_on_vector(r // BATCH):
                diagonal(n, i)

        def diagonal(n, i):
            st = job[n]
            if "grouped" not in st:
                st["grouped"] = heads.tile([P, N_UNITS, P, 4], BF16, name="grouped", align_bytes=64)
                st["codes"] = heads.tile([P, N_UNITS, P], U32, name="codes", align_bytes=64)
                st["scales"] = heads.tile([P, N_UNITS, P], U8, name="scales", align_bytes=64)
            if i < HALF:
                unit, quad, pos = UNIT_LOW[i], i, i
            else:
                unit, quad, pos = UNIT_HIGH[i], NT - 1 - i, 0
            nc.vector.scalar_tensor_tensor(
                out=a_sets[n % 2][bank_of(unit)][:, :, UNIT_BANKS[bank_of(unit)].index(unit), BLOCK * quad:BLOCK * (quad + 1)],
                in0=st["e"][i][:, pos, :].rearrange("q (u x) -> q u x", u=2),
                scalar=stat(n, "gain", i), in1=shape_ps[:, i, :].rearrange("q (u x) -> q u x", u=2),
                op0=ALU.mult, op1=ALU.add)

        def normalise_row(r):
            n, i, b, cols = place(r)
            if i > 0 and i not in VECTOR_ROWS and not all_on_vector(r // BATCH):
                normalise(None if i in SCALAR_ROWS else nc.gpsimd, n, i)

        def bank_of(unit):
            return [i for i, units in UNIT_BANKS.items() if unit in units][0]

        def all_on_vector(g):
            return g >= B * H * BATCHES - LAST_BATCHES

        def normalise(engine, n, i):
            st = job[n]
            bank = bank_of(UNIT_LOW[i])
            flat = a_sets[n % 2][bank][:].rearrange("q u n x -> q u (n x)")
            first, pos = (0, 0) if i < HALF else (BLOCK * (NT - i), 1)
            a_out = flat[:, :, first:first + BLOCK * i].rearrange("q u (j x) -> q u j x", x=BLOCK)
            e_in = st["e"][i][:, pos:pos + i, :].rearrange("q j (u x) -> q u j x", u=2)
            if engine is None:
                nc.scalar.activation(out=a_out, in_=e_in, func=ACT.Identity, scale=stat(n, "gain", i), bias=below[:, i:i + 1])
            else:
                engine.tensor_scalar(out=a_out, in0=e_in, scalar1=stat(n, "gain", i), scalar2=below[:, i:i + 1],
                                     op0=ALU.mult, op1=ALU.add)

        def a_transpose(r):
            n, i, b, cols = place(r)
            if i in UNIT_BANKS:
                units = UNIT_BANKS[i]
                bank = psum_t.tile([P, len(units), 2, P], F32, name="bank")
                words = a_sets[n % 2][i][:].bitcast(F32)
                for m in range(len(units)):
                    for u in range(2):
                        nc.tensor.transpose(bank[:, m, u, :], words[:, u, m, :], ident_f32[:])
                job[n]["bank"][i] = bank

        def a_copy(r):
            n, i, b, cols = place(r)
            if i in UNIT_BANKS:
                units = UNIT_BANKS[i]
                copy = nc.vector.tensor_copy if n_rows - 1 - r in TAIL_A else nc.scalar.copy
                copy(out=job[n]["grouped"][:, units[0]:units[-1] + 1].bitcast(F32),
                     in_=job[n]["bank"][i][:].rearrange("p c u i -> p c i u"))

        def quantise_a(x):
            n, g = divmod(x, BATCHES)
            st = job[n]
            for first, units in QUANT_CALLS[g] if x < B * H * BATCHES - 1 else ((5, 2), (7, 2)):
                nc.vector.quantize_mx(
                    out=st["codes"][:, first:first + units].rearrange("p n i -> p (n i)").bitcast(FP8X4),
                    scales=st["scales"][:, first:first + units].rearrange("p n i -> p (n i)"),
                    in_=st["grouped"][:, first:first + units].rearrange("p n i t -> p (n i t)"),
                )

        def make_bias(x):
            n, g = divmod(x, BATCHES)
            nc.vector.tensor_scalar(out=job[n]["bias"][g][:], in0=job[n]["neg_max"][g][:],
                                    scalar1=scale, scalar2=EXP_SHIFT, op0=ALU.mult, op1=ALU.add)


        def port_phase(x):
            def live(y):
                return 0 <= y < B * H * BATCHES
            y = x - GAIN
            if live(y):
                n, g = divmod(y, BATCHES)
                gain = job[n]["gain"][g]
                nc.vector.reciprocal(out=gain[:], in_=job[n]["row_sum"][g][:])
            if live(x) and not live(x + 1):
                make_bias(x)
            if live(x - QUANT):
                quantise_a(x - QUANT)
            if live(x) and live(x + 1):
                make_bias(x)
            if live(y - 1) and not all_on_vector(y - 1):
                m, f = divmod(y - 1, BATCHES)
                for i in VECTOR_ROWS:
                    if i in ROWS[f]:
                        normalise(nc.vector, m, i)
            if live(y):
                nc.vector.tensor_scalar(out=gain[:], in0=gain[:], scalar1=beta_bf[:, 0:1], scalar2=None, op0=ALU.mult)
                if all_on_vector(y):
                    for i in LAST_ORDER[g]:
                        if i > 0:
                            normalise(nc.vector, n, i)
                        diagonal(n, i)
            if live(x) and x % (H * BATCHES) == H * BATCHES - 1:
                quantise_v(x // (H * BATCHES))

        def multiply_rows(r):
            n, i, b, cols = place(r)
            st = job[n]
            h = n % H
            v_codes, v_scales = seq[b]
            g, place_in_batch = at(i)
            if place_in_batch == 0:
                if r // BATCH >= B * H * BATCHES - 2:
                    st["o_ps"] = psum_s.tile([P, BATCH, P], F32, name="s_ps")
                else:
                    st["o_ps"] = psum_o.tile([P, BATCH, P], F32, name="o_ps")
            passes = []
            for c in range(PASSES):
                unit = (UNIT_LOW, UNIT_HIGH)[c][i]
                tiles = min(HALF, max(0, i + 1 - c * HALF))
                if tiles == HALF:
                    passes.append((st["codes"][:, unit, :], st["scales"][:, unit, :], c, v_codes[:, h, c, :]))
                elif tiles > 0:
                    passes.append((st["codes"][:, unit, :], st["scales"][:, unit, :], c, v_masked[:, b % 2, MASKS.index((c, tiles)), h, :]))
                if tiles < HALF:
                    far = far_index(c, i)
                    passes.append((far_codes[:, far, :], far_scales[:, far, :], c, v_codes[:, h, c, :]))
            for m, (a_codes, a_scales, c, moving) in enumerate(passes):
                nc.tensor.matmul_mx(
                    out=st["o_ps"][:, place_in_batch, :],
                    lhsT=a_codes.bitcast(FP8X4), lhsT_scale=a_scales,
                    rhs=moving.bitcast(FP8X4), rhs_scale=v_scales[:, h, c, :],
                    start=(m == 0), stop=(m == len(passes) - 1),
                )

        def out_copy(r):
            n, i, b, cols = place(r)
            g, m = at(i)
            if m == BATCH - 1:
                out_sb = long_lived.tile([P, BATCH, D], F32, name="out_sb")
                copy = nc.vector.tensor_copy if n_rows - 1 - r in TAIL_O else nc.scalar.copy
                copy(out=out_sb[:], in_=job[n]["o_ps"][:])
                rows = out[b, :, cols].rearrange("(n p) c -> p n c", p=P)
                for first, tiles in (((0, slice(0, 7, 3)), (3, slice(7, 8))) if g == 0 else ((0, slice(1, 3)), (2, slice(4, 6)))):
                    nc.sync.dma_start(out=rows[:, tiles, :], in_=out_sb[:, first:first + (3 if first == 0 and g == 0 else 2 if g == 1 else 1), :])

        def run(stage, r):
            if 0 <= r < n_rows:
                stage(r)

        shape_parts = constants()
        for s in range(-5, n_rows + L_OUT + 3):
            if s % BATCH == BATCH - 1:
                for m in reversed(range(BATCH)):
                    run(multiply_rows, s - m - L_MUL)
            run(a_transpose, s - L_AT)
            run(score_row, s + 1)
            run(max_first_bank, s)
            run(diagonal_tile, s - L_DIAG)
            run(max_second_bank, s)
            run(a_copy, s - L_ACOPY)
            run(out_copy, s - L_OUT)
            run(exp_row, s - L_EXP)
            run(normalise_row, s - L_NORM)
            run(regroup_v, s + V_AHEAD if s > 2 else s - 2)
            run(q_transpose, s + 5)
            run(k_transpose, s + 5)
            if s == SHAPE_STEP:
                shape_constants(*shape_parts)
            if s == 2:
                nc.gpsimd.memset(far_grouped[:].rearrange("p n i t -> p (n i t)").bitcast(F32), 0.0)
                nc.gpsimd.memset(v_masked[:].rearrange("p s m h w -> p (s m h w)").bitcast(F32), 0.0)
            if s == FAR_STEP:
                far_units()
            if s == FAR_STEP + 3:
                far_quantise()
            if s % BATCH == BATCH - 1:
                port_phase(s // BATCH)
